import numpy as np
import ml_dtypes


def mxq(x, axis, fmt="e4m3"):
    dtype, down = {"e4m3": (ml_dtypes.float8_e4m3fn, 7), "e5m2": (ml_dtypes.float8_e5m2, 14)}[fmt]
    v = np.moveaxis(np.asarray(x, np.float32).astype(ml_dtypes.bfloat16).astype(np.float64), axis, -1)
    blocks = v.reshape(v.shape[:-1] + (-1, 32))
    amax = np.abs(blocks).max(-1, keepdims=True)
    byte = np.maximum(np.where(amax > 0, np.frexp(amax)[1] - 1 + 127, 0) - down, 1)
    scale = np.exp2(byte - 127.0)
    codes = (blocks / scale).astype(np.float32).astype(dtype).astype(np.float64)
    return np.moveaxis((codes * scale).reshape(v.shape), -1, axis)


WIDE = False


def mx_kscale(k):
    if not WIDE:
        return np.ones(k)
    levels = np.array([10, -10, 5, -5, 0])
    if k % 512:
        return np.exp2(np.random.permutation(np.resize(levels, k // 32))).repeat(32)
    a = np.empty((k // 512, 16))
    for p in range(k // 512):
        a[p, :8] = np.random.permutation(np.resize(levels, 8))
        for g in range(8):
            far = levels[np.abs(levels - a[p, g]) >= 10]
            a[p, g + 8] = far[np.random.randint(len(far))]
    return np.exp2(a.ravel()).repeat(32)


BF16 = ml_dtypes.bfloat16


def bf(x):
    return np.asarray(x, np.float32).astype(BF16)


def f64(x):
    return np.asarray(x).astype(np.float64)


B, H, NSE = 2048, 512, 1024


def sigmoid(v):
    return 1.0 / (1.0 + np.exp(-v))


def setup_inputs():
    s = mx_kscale(B)[:, None]
    e = np.frexp(mx_kscale(NSE))[1] - 1
    t = np.ldexp(1.0, e >> 1)
    u = t * t
    z_i0 = bf(np.random.standard_normal((B, H)))
    z_j = bf(np.random.standard_normal((B, H)))
    R = bf(np.eye(H) + np.random.standard_normal((H, H)) / np.sqrt(H))
    D0 = bf((1.0 + 0.3 * np.random.standard_normal((NSE, H))) * 0.9 / H ** 0.25)
    g = bf(np.random.standard_normal((B, NSE)) * np.exp2(np.random.randint(-6, 1, (B, 1))) * 4.0 / s * u[None, :])
    Rz = f64(z_j) @ f64(R).T
    scores = (f64(z_i0) * Rz) @ (f64(D0) * f64(D0)).T
    return {"z_i": bf(f64(z_i0) * s), "z_j": z_j, "R": R, "D": bf(f64(D0) / t[:, None]),
            "Rz": np.asarray(Rz, np.float32), "scores": np.asarray(scores, np.float32), "grad_out": g}


def reference(z_i, z_j, R, D, Rz, scores, grad_out):
    sg = sigmoid(f64(scores))
    dz = f64(grad_out) * (sg * (1.0 - sg))
    rz = f64(Rz)
    p = f64(z_i) * rz
    d = f64(D)
    d2 = d * d
    dp = mxq(dz, 1, "e5m2") @ mxq(d2, 0, "e4m3")
    dd2 = mxq(dz, 0, "e5m2").T @ mxq(p, 0, "e4m3")
    return dp * rz, 2.0 * d * dd2

@@ -1,0 +1,456 @@
+from contextlib import ExitStack
+
+import concourse.mybir as mybir
+from concourse.masks import make_identity
+
+B, H, R = 2048, 512, 1024
+
+FLOPS = 2 * 2 * B * H * R
+BYTES = 2 * B * H + 2 * R * H + 4 * B * H + 4 * B * R + 2 * B * R + 4 * B * H + 4 * R * H
+
+F32 = mybir.dt.float32
+BF16 = mybir.dt.bfloat16
+U32 = mybir.dt.uint32
+U8 = mybir.dt.uint8
+E4M3 = mybir.dt.float8_e4m3fn_x4
+E5M2 = mybir.dt.float8_e5m2_x4
+ACT = mybir.ActivationFunctionType
+ALU = mybir.AluOpType
+
+P = 128
+NT = B // 512
+NG = R // 512
+NU = NT * NG
+
+
+def tile_dedicomdecoder_v_kernel(tc, z_i, z_j, w_r, d_w, rz_in, scores, grad_out, out_0, out_1):
+    nc = tc.nc
+    with ExitStack() as ctx:
+        keep = ctx.enter_context(tc.tile_pool(name="keep", bufs=1))
+        s_pool = ctx.enter_context(tc.tile_pool(name="s_pool", bufs=5))
+        three = ctx.enter_context(tc.tile_pool(name="three", bufs=3))
+        two = ctx.enter_context(tc.tile_pool(name="two", bufs=2))
+        ps_wk = ctx.enter_context(tc.psum_pool(name="ps_wk", bufs=2))
+        ps_o0 = ctx.enter_context(tc.psum_pool(name="ps_o0", bufs=2))
+        ps_acc = ctx.enter_context(tc.psum_pool(name="ps_acc", bufs=1))
+        ctx.enter_context(tc.manual_schedule())
+
+        s_t, g_t, z_t, rz_t = {}, {}, {}, {}
+
+        def load_s(u, j0=0, j1=4):
+            t, g = divmod(u, NG)
+            if u not in s_t:
+                s_t[u] = s_pool.tile([P, 4, 512], F32, name="s_tile")
+            src = scores[512 * t : 512 * (t + 1), 512 * g : 512 * (g + 1)].rearrange("(p j) n -> p j n", j=4)
+            nc.sync.dma_start(out=s_t[u][:, j0:j1, :], in_=src[:, j0:j1, :])
+
+        def load_d(g):
+            src = d_w[512 * g : 512 * (g + 1), :].rearrange("(p j) h -> p j h", j=4)
+            nc.sync.dma_start(out=d_sb[:, g, :, :], in_=src)
+
+        def load_g(t, c0=0, c1=1024):
+            if t not in g_t:
+                g_t[t] = three.tile([P, 4, R], BF16, name="g_tile")
+            src = grad_out[512 * t : 512 * (t + 1), :].rearrange("(p j) n -> p j n", j=4)
+            nc.sync.dma_start(out=g_t[t][:, :, c0:c1], in_=src[:, :, c0:c1])
+
+        def load_z(t):
+            z_t[t] = two.tile([P, 4, H], BF16, name="z_tile")
+            nc.sync.dma_start(out=z_t[t][:], in_=z_i[512 * t : 512 * (t + 1), :].rearrange("(p j) n -> p j n", j=4))
+
+        def load_rz(t):
+            rz_t[t] = keep.tile([P, 4, H], F32, name="rz_tile%d" % t)
+            nc.sync.dma_start(out=rz_t[t][:], in_=rz_in[512 * t : 512 * (t + 1), :].rearrange("(p j) n -> p j n", j=4))
+
+        ident = keep.tile([P, P], F32, name="ident")
+        make_identity(nc, ident[:])
+        warm = keep.tile([P, 1], F32, name="warm")
+        nc.vector.memset(warm[:], 0.0)
+        warm2 = keep.tile([P, 1], F32, name="warm2")
+        nc.scalar.activation(out=warm2[:], in_=warm[:], func=ACT.Tanh)
+
+        d_sb = keep.tile([P, NG, 4, H], BF16, name="d_sb")
+        d2_code = keep.tile([P, NG, H], U32, name="d2_code", align_bytes=64)
+        d2_scale = keep.tile([P, NG, H], U8, name="d2_scale", align_bytes=64)
+        p_code = keep.tile([P, NT, H], U32, name="p_code", align_bytes=64)
+        p_scale = keep.tile([P, NT, H], U8, name="p_scale", align_bytes=64)
+        t_code = keep.tile([P, NT + 2, 512], U32, name="t_code", align_bytes=64)
+        t_scale = keep.tile([P, NT + 2, 512], U8, name="t_scale", align_bytes=64)
+        r_code = keep.tile([P, 4, 512], U32, name="r_code", align_bytes=64)
+        r_scale = keep.tile([P, 4, 512], U8, name="r_scale", align_bytes=64)
+
+        def act(u, func, j0, j1):
+            s = s_t[u][:, j0:j1, :]
+            nc.scalar.activation(out=s, in_=s, func=func, scale=0.5)
+
+        dz_t, dzi_t, dzr_t, p_t, tr_t = {}, {}, {}, {}, {}
+
+        def slot(u):
+            t, g = divmod(u, NG)
+            return t if g == 1 else NT + t % 2
+
+        def stt(u, j0=0, j1=4):
+            t, g = divmod(u, NG)
+            if u not in dz_t:
+                dz_t[u] = three.tile([P, 4, 512], BF16, name="dz", align_bytes=64)
+            j = slice(j0, j1)
+            nc.vector.scalar_tensor_tensor(
+                out=dz_t[u][:, j, :],
+                in0=s_t[u][:, j, :],
+                scalar=0.25,
+                in1=g_t[t][:, j, 512 * g : 512 * (g + 1)],
+                op0=ALU.subtract,
+                op1=ALU.mult,
+            )
+
+        def il(u, r0, r1, eng):
+            if r0 == r1:
+                return
+            if u not in dzi_t:
+                dzi_t[u] = two.tile([P, 4, P, 4], BF16, name="dzi", align_bytes=64)
+            dst = dzi_t[u][:, r0:r1, :, :].rearrange("p r m t -> p m t r")
+            src = dz_t[u][:].rearrange("p t (m r) -> p m t r", r=4)[:, :, :, r0:r1]
+            if eng == "s":
+                nc.scalar.copy(out=dst, in_=src)
+            else:
+                nc.vector.tensor_copy(out=dst, in_=src)
+
+        def q_t(u):
+            nc.vector.quantize_mx(
+                out=t_code[:, slot(u), :].bitcast(E5M2),
+                scales=t_scale[:, slot(u), :],
+                in_=dzi_t[u][:].rearrange("p r m t -> p (r m t)"),
+            )
+
+        def tr(u, b):
+            words = dz_t[u][:].rearrange("p j n -> p (j n)").bitcast(F32)
+            bank = ps_wk.tile([P, 2, 2, P], F32, name="bank")
+            for jj in range(2):
+                w0 = 256 * (2 * b + jj)
+                for h in range(2):
+                    nc.tensor.transpose(bank[:, jj, h, :], words[:, w0 + h : w0 + 256 : 2], ident[:])
+            tr_t[u, b] = bank
+            if u not in dzr_t:
+                dzr_t[u] = two.tile([P, 4, P, 4], BF16, name="dzr", align_bytes=64)
+
+        def cp(u, b, eng):
+            src = tr_t[u, b][:].rearrange("m j h p -> m j p h")
+            dst = dzr_t[u][:].rearrange("m j p r -> m (j p r)").bitcast(F32)[:, 512 * b : 512 * (b + 1)]
+            dst = dst.rearrange("m (j p h) -> m j p h", j=2, h=2)
+            if eng == "s":
+                nc.scalar.copy(out=dst, in_=src)
+            else:
+                nc.vector.tensor_copy(out=dst, in_=src)
+
+        def q_r(u, j0=0, j1=4):
+            nc.vector.quantize_mx(
+                out=r_code[:, u % 4, P * j0 : P * j1].bitcast(E5M2),
+                scales=r_scale[:, u % 4, P * j0 : P * j1],
+                in_=dzr_t[u][:, j0:j1, :, :].rearrange("m j p r -> m (j p r)"),
+            )
+
+        def make_p(t, half):
+            if t not in p_t:
+                p_t[t] = two.tile([P, H, 4], BF16, name="p_tile", align_bytes=64)
+            cols = slice(256 * half, 256 * (half + 1))
+            nc.vector.tensor_tensor(
+                out=p_t[t][:, cols, :].rearrange("p (c i) t -> p c t i", i=4),
+                in0=z_t[t][:, :, cols].rearrange("p t (c i) -> p c t i", i=4),
+                in1=rz_t[t][:, :, cols].rearrange("p t (c i) -> p c t i", i=4),
+                op=ALU.mult,
+            )
+
+        def q_p(t):
+            nc.vector.quantize_mx(
+                out=p_code[:, t, :].bitcast(E4M3),
+                scales=p_scale[:, t, :],
+                in_=p_t[t][:].rearrange("p h t -> p (h t)"),
+            )
+
+        d2_t = {}
+
+        def make_d2(g, eng="v"):
+            d2 = two.tile([P, H, 4], BF16, name="d2", align_bytes=64)
+            v = d_sb[:, g, :, :].rearrange("p t (c i) -> p c t i", i=4)
+            if eng == "s":
+                nc.scalar.activation(out=d2[:].rearrange("p (c i) t -> p c t i", i=4), in_=v, func=ACT.Square)
+            else:
+                nc.vector.tensor_tensor(out=d2[:].rearrange("p (c i) t -> p c t i", i=4), in0=v, in1=v, op=ALU.mult)
+            d2_t[g] = d2
+
+        def q_d(g):
+            nc.vector.quantize_mx(
+                out=d2_code[:, g, :].bitcast(E4M3),
+                scales=d2_scale[:, g, :],
+                in_=d2_t[g][:].rearrange("p h t -> p (h t)"),
+            )
+
+        o0_t, o0_bank = {}, {}
+
+        def mm0(t, j, spare=False):
+            if spare:
+                bank = ps_wk.tile([P, H], F32, name="bank")
+            else:
+                bank = ps_o0.tile([P, H], F32, name="o0_bank_tile")
+            for g in range(NG):
+                u = NG * t + g
+                nc.tensor.matmul_mx(
+                    out=bank[:],
+                    lhsT=r_code[:, u % 4, P * j : P * (j + 1)].bitcast(E5M2),
+                    lhsT_scale=r_scale[:, u % 4, P * j : P * (j + 1)],
+                    rhs=d2_code[:, g, :].bitcast(E4M3),
+                    rhs_scale=d2_scale[:, g, :],
+                    start=(g == 0),
+                    stop=(g == NG - 1),
+                )
+            o0_bank[t, j] = bank
+
+        def ev0(t, j):
+            if t not in o0_t:
+                o0_t[t] = two.tile([P, 4, H], F32, name="o0_tile")
+            nc.vector.scalar_tensor_tensor(
+                out=o0_t[t][:, j, :], in0=o0_bank[t, j][:], scalar=-1.0, in1=rz_t[t][:, j, :], op0=ALU.mult, op1=ALU.mult
+            )
+
+        def st0(t, j0, j1):
+            dst = out_0[512 * t : 512 * (t + 1), :].rearrange("(p j) h -> p j h", j=4)
+            nc.sync.dma_start(out=dst[:, j0:j1, :], in_=o0_t[t][:, j0:j1, :])
+
+        acc = {}
+
+        def mm1(t, g):
+            u = NG * t + g
+            for r in range(4):
+                if t == 0:
+                    acc[g, r] = ps_acc.tile([P, H], F32, name="acc%d" % r)
+                nc.tensor.matmul_mx(
+                    out=acc[g, r][:],
+                    lhsT=t_code[:, slot(u), P * r : P * (r + 1)].bitcast(E5M2),
+                    lhsT_scale=t_scale[:, slot(u), P * r : P * (r + 1)],
+                    rhs=p_code[:, t, :].bitcast(E4M3),
+                    rhs_scale=p_scale[:, t, :],
+                    start=(t == 0),
+                    stop=(t == NT - 1),
+                )
+
+        o1_t = {}
+
+        def ev1(g, r):
+            if g not in o1_t:
+                o1_t[g] = two.tile([P, 4, H], F32, name="o1_tile")
+            nc.vector.scalar_tensor_tensor(
+                out=o1_t[g][:, r, :], in0=acc[g, r][:], scalar=-2.0, in1=d_sb[:, g, r, :], op0=ALU.mult, op1=ALU.mult
+            )
+
+        def st1(g, r0, r1):
+            dst = out_1[512 * g : 512 * (g + 1), :].rearrange("(m r) h -> m r h", r=4)
+            nc.sync.dma_start(out=dst[:, r0:r1, :], in_=o1_t[g][:, r0:r1, :])
+
+        load_s(0, 0, 1)
+        act(0, ACT.Tanh, 0, 1)
+        act(0, ACT.Square, 0, 1)
+        load_d(0)
+        make_d2(0)
+        load_s(0, 3, 4)
+        act(0, ACT.Tanh, 3, 4)
+        load_s(0, 1, 2)
+        act(0, ACT.Tanh, 1, 2)
+        act(0, ACT.Square, 1, 2)
+        act(0, ACT.Square, 3, 4)
+        load_g(0, 0, 512)
+        stt(0, 0, 1)
+        load_s(0, 2, 3)
+        act(0, ACT.Tanh, 2, 3)
+        act(0, ACT.Square, 2, 3)
+        stt(0, 1, 2)
+        tr(0, 0)
+        cp(0, 0, "s")
+        load_s(1)
+        act(1, ACT.Tanh, 2, 4)
+        q_d(0)
+        stt(0, 3, 4)
+        stt(0, 2, 3)
+        tr(0, 1)
+        il(0, 0, 4, "v")
+        load_d(1)
+        make_d2(1)
+        q_t(0)
+        q_d(1)
+        act(1, ACT.Tanh, 0, 2)
+        act(1, ACT.Square, 2, 4)
+        load_g(0, 512, 1024)
+        act(1, ACT.Square, 0, 2)
+        stt(1)
+        tr(1, 0)
+        cp(0, 1, "s")
+        tr(1, 1)
+        q_r(0)
+        load_s(2)
+        act(2, ACT.Tanh, 0, 2)
+        act(2, ACT.Tanh, 2, 4)
+        act(2, ACT.Square, 0, 2)
+        il(1, 1, 4, "v")
+        load_z(0)
+        load_rz(0)
+        make_p(0, 0)
+        make_p(0, 1)
+        act(2, ACT.Square, 2, 4)
+        cp(1, 1, "s")
+        cp(1, 0, "s")
+        q_r(1)
+        mm0(0, 0)
+        mm0(0, 1)
+        q_p(0)
+        il(1, 0, 1, "s")
+        q_t(1)
+        ev0(0, 0)
+        mm0(0, 2)
+        load_s(3)
+        act(3, ACT.Tanh, 0, 2)
+        act(3, ACT.Tanh, 2, 4)
+        act(3, ACT.Square, 0, 2)
+        load_g(1)
+        stt(2)
+        tr(2, 0)
+        tr(2, 1)
+        ev0(0, 1)
+        act(3, ACT.Square, 2, 4)
+        load_s(4)
+        act(4, ACT.Tanh, 0, 2)
+        act(4, ACT.Tanh, 2, 4)
+        cp(2, 0, "s")
+        stt(3)
+        il(3, 0, 2, "s")
+        act(4, ACT.Square, 0, 2)
+        ev0(0, 2)
+        il(3, 2, 4, "v")
+        cp(2, 1, "s")
+        mm0(0, 3)
+        ev0(0, 3)
+        il(2, 1, 4, "v")
+        load_rz(1)
+        load_z(1)
+        make_p(1, 0)
+        q_r(2)
+        make_p(1, 1)
+        tr(3, 0)
+        il(2, 0, 1, "s")
+        load_g(2)
+        act(4, ACT.Square, 2, 4)
+        stt(4)
+        q_p(1)
+        tr(3, 1)
+        cp(3, 1, "s")
+        cp(3, 0, "s")
+        q_r(3)
+        tr(4, 0)
+        tr(4, 1)
+        load_s(5)
+        act(5, ACT.Tanh, 2, 4)
+        act(5, ACT.Square, 2, 4)
+        act(5, ACT.Tanh, 0, 2)
+        act(5, ACT.Square, 0, 2)
+        cp(4, 0, "s")
+        q_t(3)
+        il(4, 0, 2, "s")
+        q_t(2)
+        cp(4, 1, "s")
+        load_rz(2)
+        load_z(2)
+        make_p(2, 0)
+        load_s(6)
+        act(6, ACT.Tanh, 0, 2)
+        load_s(7)
+        act(7, ACT.Tanh, 0, 2)
+        mm0(1, 0)
+        ev0(1, 0)
+        mm0(1, 1)
+        mm0(1, 2)
+        make_p(2, 1)
+        ev0(1, 1)
+        stt(5)
+        il(4, 2, 4, "v")
+        mm0(1, 3)
+        q_r(4)
+        ev0(1, 2)
+        q_p(2)
+        mm1(0, 0)
+        tr(5, 0)
+        mm1(1, 0)
+        tr(5, 1)
+        q_t(4)
+        mm1(2, 0)
+        load_z(3)
+        load_rz(3)
+        make_p(3, 0)
+        make_p(3, 1)
+        act(6, ACT.Tanh, 2, 4)
+        act(6, ACT.Square, 0, 2)
+        act(7, ACT.Tanh, 2, 4)
+        load_g(3)
+        act(6, ACT.Square, 2, 4)
+        stt(6)
+        cp(5, 0, "s")
+        tr(6, 0)
+        cp(5, 1, "s")
+        tr(6, 1)
+        ev0(1, 3)
+        q_r(5)
+        mm0(2, 0)
+        mm0(2, 1)
+        act(7, ACT.Square, 2, 4)
+        il(5, 3, 4, "v")
+        act(7, ACT.Square, 0, 2)
+        stt(7)
+        il(6, 0, 4, "s")
+        q_t(6)
+        cp(6, 0, "s")
+        tr(7, 0)
+        cp(6, 1, "s")
+        tr(7, 1)
+        cp(7, 1, "s")
+        q_p(3)
+        mm1(3, 0)
+        st0(0, 0, 4)
+        ev0(2, 1)
+        ev0(2, 0)
+        mm0(2, 2)
+        mm0(2, 3)
+        q_r(6)
+        ev1(0, 0)
+        ev1(0, 1)
+        ev1(0, 2)
+        st0(1, 0, 4)
+        ev1(0, 3)
+        st1(0, 0, 4)
+        mm1(0, 1)
+        cp(7, 0, "s")
+        q_r(7)
+        il(5, 0, 3, "s")
+        q_t(5)
+        ev0(2, 2)
+        ev0(2, 3)
+        st0(2, 0, 4)
+        il(7, 2, 4, "v")
+        il(7, 0, 2, "s")
+        mm0(3, 0, spare=True)
+        mm0(3, 1, spare=True)
+        ev0(3, 1)
+        q_t(7)
+        ev0(3, 0)
+        st0(3, 0, 2)
+        mm1(1, 1)
+        mm1(2, 1)
+        mm1(3, 1)
+        ev1(1, 0)
+        ev1(1, 1)
+        st1(1, 0, 2)
+        ev1(1, 3)
+        ev1(1, 2)
+        st1(1, 2, 4)
+        mm0(3, 2)
+        ev0(3, 2)
+        st0(3, 2, 3)
+        mm0(3, 3)
+        ev0(3, 3)
+        st0(3, 3, 4)

@@ -20,437 +20,365 @@ ALU = mybir.AluOpType
 P = 128
 NT = B // 512
 NG = R // 512
-NU = NT * NG
+ROWS = 4 * NT
+SHARES = (0, 128, 0, 0)
+LATE = 11
+Q30 = 14
+AHEAD = 4
+P_STEPS = (5, 7, 9, 12)
+VECTOR_COPIES = 0
 
 
 def tile_dedicomdecoder_v_kernel(tc, z_i, z_j, w_r, d_w, rz_in, scores, grad_out, out_0, out_1):
     nc = tc.nc
     with ExitStack() as ctx:
         keep = ctx.enter_context(tc.tile_pool(name="keep", bufs=1))
-        s_pool = ctx.enter_context(tc.tile_pool(name="s_pool", bufs=5))
-        three = ctx.enter_context(tc.tile_pool(name="three", bufs=3))
-        two = ctx.enter_context(tc.tile_pool(name="two", bufs=2))
-        ps_wk = ctx.enter_context(tc.psum_pool(name="ps_wk", bufs=2))
+        ring = ctx.enter_context(tc.tile_pool(name="ring", bufs=2))
+        ps_tr = ctx.enter_context(tc.psum_pool(name="ps_tr", bufs=2))
         ps_o0 = ctx.enter_context(tc.psum_pool(name="ps_o0", bufs=2))
         ps_acc = ctx.enter_context(tc.psum_pool(name="ps_acc", bufs=1))
         ctx.enter_context(tc.manual_schedule())
 
-        s_t, g_t, z_t, rz_t = {}, {}, {}, {}
+        def token_rows(hbm, t):
+            return hbm[512 * t : 512 * (t + 1), :].rearrange("(p j) n -> p j n", j=4)
 
-        def load_s(u, j0=0, j1=4):
-            t, g = divmod(u, NG)
-            if u not in s_t:
-                s_t[u] = s_pool.tile([P, 4, 512], F32, name="s_tile")
-            src = scores[512 * t : 512 * (t + 1), 512 * g : 512 * (g + 1)].rearrange("(p j) n -> p j n", j=4)
-            nc.sync.dma_start(out=s_t[u][:, j0:j1, :], in_=src[:, j0:j1, :])
+        s_t, g_t, z_t, rz_t, d_t = {}, {}, {}, {}, {}
+
+        def load_s(k0, k1):
+            if k0 % 2 == 0:
+                s_t[k0 // 2] = ring.tile([P, 2, R], F32, name="s_rows", bufs=4)
+            nc.sync.dma_start(
+                out=s_t[k0 // 2][:, k0 % 2 : k0 % 2 + k1 - k0, :],
+                in_=token_rows(scores, k0 // 4)[:, k0 % 4 : k0 % 4 + k1 - k0, :],
+            )
+
+        def load_g(k):
+            g_t[k // 2] = ring.tile([P, 2, R], BF16, name="g_rows", bufs=5)
+            nc.sync.dma_start(out=g_t[k // 2][:], in_=token_rows(grad_out, k // 4)[:, k % 4 : k % 4 + 2, :])
 
         def load_d(g):
-            src = d_w[512 * g : 512 * (g + 1), :].rearrange("(p j) h -> p j h", j=4)
-            nc.sync.dma_start(out=d_sb[:, g, :, :], in_=src)
-
-        def load_g(t, c0=0, c1=1024):
-            if t not in g_t:
-                g_t[t] = three.tile([P, 4, R], BF16, name="g_tile")
-            src = grad_out[512 * t : 512 * (t + 1), :].rearrange("(p j) n -> p j n", j=4)
-            nc.sync.dma_start(out=g_t[t][:, :, c0:c1], in_=src[:, :, c0:c1])
+            d_t[g] = keep.tile([P, 4, H], BF16, name="d_rows%d" % g)
+            nc.sync.dma_start(out=d_t[g][:], in_=token_rows(d_w, g))
 
         def load_z(t):
-            z_t[t] = two.tile([P, 4, H], BF16, name="z_tile")
-            nc.sync.dma_start(out=z_t[t][:], in_=z_i[512 * t : 512 * (t + 1), :].rearrange("(p j) n -> p j n", j=4))
+            z_t[t] = ring.tile([P, 4, H], BF16, name="z_rows")
+            nc.sync.dma_start(out=z_t[t][:], in_=token_rows(z_i, t))
 
-        def load_rz(t):
-            rz_t[t] = keep.tile([P, 4, H], F32, name="rz_tile%d" % t)
-            nc.sync.dma_start(out=rz_t[t][:], in_=rz_in[512 * t : 512 * (t + 1), :].rearrange("(p j) n -> p j n", j=4))
+        def load_rz(t, half):
+            if half == 0:
+                rz_t[t] = ring.tile([P, 4, H], F32, name="rz_rows", bufs=3)
+            rows = slice(2 * half, 2 * half + 2)
+            nc.sync.dma_start(out=rz_t[t][:, rows, :], in_=token_rows(rz_in, t)[:, rows, :])
 
         ident = keep.tile([P, P], F32, name="ident")
         make_identity(nc, ident[:])
-        warm = keep.tile([P, 1], F32, name="warm")
-        nc.vector.memset(warm[:], 0.0)
-        warm2 = keep.tile([P, 1], F32, name="warm2")
-        nc.scalar.activation(out=warm2[:], in_=warm[:], func=ACT.Tanh)
 
-        d_sb = keep.tile([P, NG, 4, H], BF16, name="d_sb")
         d2_code = keep.tile([P, NG, H], U32, name="d2_code", align_bytes=64)
         d2_scale = keep.tile([P, NG, H], U8, name="d2_scale", align_bytes=64)
         p_code = keep.tile([P, NT, H], U32, name="p_code", align_bytes=64)
         p_scale = keep.tile([P, NT, H], U8, name="p_scale", align_bytes=64)
-        t_code = keep.tile([P, NT + 2, 512], U32, name="t_code", align_bytes=64)
-        t_scale = keep.tile([P, NT + 2, 512], U8, name="t_scale", align_bytes=64)
-        r_code = keep.tile([P, 4, 512], U32, name="r_code", align_bytes=64)
-        r_scale = keep.tile([P, 4, 512], U8, name="r_scale", align_bytes=64)
+        tok_code = keep.tile([P, NT, NG, 512], U32, name="tok_code", align_bytes=64)
+        tok_scale = keep.tile([P, NT, NG, 512], U8, name="tok_scale", align_bytes=64)
 
-        def act(u, func, j0, j1):
-            s = s_t[u][:, j0:j1, :]
-            nc.scalar.activation(out=s, in_=s, func=func, scale=0.5)
+        def cells(k):
+            if k < ROWS - 4:
+                return [(k, 0), (k, 1)]
+            g, pair = divmod(k - (ROWS - 4), 2)
+            return [(ROWS - 4 + 2 * pair, g), (ROWS - 4 + 2 * pair + 1, g)]
 
-        dz_t, dzi_t, dzr_t, p_t, tr_t = {}, {}, {}, {}, {}
+        def part(pair_tile, k):
+            (row, g), (row2, g2) = cells(k)
+            if row == row2:
+                return pair_tile[:, row % 2, :]
+            return pair_tile[:, :, 512 * g : 512 * (g + 1)]
 
-        def slot(u):
-            t, g = divmod(u, NG)
-            return t if g == 1 else NT + t % 2
+        def pair_of(k):
+            return cells(k)[0][0] // 2
 
-        def stt(u, j0=0, j1=4):
-            t, g = divmod(u, NG)
-            if u not in dz_t:
-                dz_t[u] = three.tile([P, 4, 512], BF16, name="dz", align_bytes=64)
-            j = slice(j0, j1)
+        def tanh(k):
+            s = part(s_t[pair_of(k)], k)
+            nc.scalar.activation(out=s, in_=s, func=ACT.Tanh, scale=0.5)
+
+        def square(k):
+            s = part(s_t[pair_of(k)], k)
+            nc.scalar.activation(out=s, in_=s, func=ACT.Square, scale=0.5)
+
+        dz_t, tok_t, rel_t, bank_t, rel_code, rel_scale, p_t, d2_t, rel_at = {}, {}, {}, {}, {}, {}, {}, {}, {}
+
+        def make_dz(k):
+            t, pair = divmod(pair_of(k), 2)
+            if k % 4 == 0:
+                dz_t[t] = ring.tile([P, 4, R], BF16, name="dz", bufs=3)
             nc.vector.scalar_tensor_tensor(
-                out=dz_t[u][:, j, :],
-                in0=s_t[u][:, j, :],
+                out=part(dz_t[t][:, 2 * pair : 2 * pair + 2, :], k),
+                in0=part(s_t[pair_of(k)], k),
                 scalar=0.25,
-                in1=g_t[t][:, j, 512 * g : 512 * (g + 1)],
+                in1=part(g_t[pair_of(k)], k),
                 op0=ALU.subtract,
                 op1=ALU.mult,
             )
 
-        def il(u, r0, r1, eng):
-            if r0 == r1:
+        def interleave(t, g, m0, m1, copy):
+            if m0 == m1:
                 return
-            if u not in dzi_t:
-                dzi_t[u] = two.tile([P, 4, P, 4], BF16, name="dzi", align_bytes=64)
-            dst = dzi_t[u][:, r0:r1, :, :].rearrange("p r m t -> p m t r")
-            src = dz_t[u][:].rearrange("p t (m r) -> p m t r", r=4)[:, :, :, r0:r1]
-            if eng == "s":
-                nc.scalar.copy(out=dst, in_=src)
-            else:
-                nc.vector.tensor_copy(out=dst, in_=src)
-
-        def q_t(u):
-            nc.vector.quantize_mx(
-                out=t_code[:, slot(u), :].bitcast(E5M2),
-                scales=t_scale[:, slot(u), :],
-                in_=dzi_t[u][:].rearrange("p r m t -> p (r m t)"),
+            if (t, g) not in tok_t:
+                tok_t[t, g] = ring.tile([P, 4, P, 4], BF16, name="tok", align_bytes=64, bufs=3)
+            copy(
+                out=tok_t[t, g][:, :, m0:m1, :].rearrange("p r m j -> p m j r"),
+                in_=dz_t[t][:, :, 512 * g : 512 * (g + 1)].rearrange("p j (m r) -> p m j r", r=4)[:, m0:m1, :, :],
             )
 
-        def tr(u, b):
-            words = dz_t[u][:].rearrange("p j n -> p (j n)").bitcast(F32)
-            bank = ps_wk.tile([P, 2, 2, P], F32, name="bank")
-            for jj in range(2):
-                w0 = 256 * (2 * b + jj)
+        def quantize_tok(t, g):
+            nc.vector.quantize_mx(
+                out=tok_code[:, t, g, :].bitcast(E5M2),
+                scales=tok_scale[:, t, g, :],
+                in_=tok_t[t, g][:].rearrange("p r m j -> p (r m j)"),
+            )
+
+        def transpose(k):
+            bank_t[k] = ps_tr.tile([P, 2, 2, P], F32, name="tr_bank")
+            for c, (row, g) in enumerate(cells(k)):
+                words = dz_t[row // 4][:, row % 4, :].bitcast(F32)
                 for h in range(2):
-                    nc.tensor.transpose(bank[:, jj, h, :], words[:, w0 + h : w0 + 256 : 2], ident[:])
-            tr_t[u, b] = bank
-            if u not in dzr_t:
-                dzr_t[u] = two.tile([P, 4, P, 4], BF16, name="dzr", align_bytes=64)
+                    nc.tensor.transpose(bank_t[k][:, c, h, :], words[:, 256 * g + h : 256 * (g + 1) : 2], ident[:])
 
-        def cp(u, b, eng):
-            src = tr_t[u, b][:].rearrange("m j h p -> m j p h")
-            dst = dzr_t[u][:].rearrange("m j p r -> m (j p r)").bitcast(F32)[:, 512 * b : 512 * (b + 1)]
-            dst = dst.rearrange("m (j p h) -> m j p h", j=2, h=2)
-            if eng == "s":
-                nc.scalar.copy(out=dst, in_=src)
-            else:
-                nc.vector.tensor_copy(out=dst, in_=src)
+        def copy_words(k):
+            rel_t[k] = ring.tile([P, NG, P, 2], F32, name="rel", align_bytes=64, bufs=3)
+            copy = nc.vector.tensor_copy if k < VECTOR_COPIES else nc.scalar.copy
+            copy(out=rel_t[k][:], in_=bank_t[k][:].rearrange("m g h p -> m g p h"))
 
-        def q_r(u, j0=0, j1=4):
+        def quantize_rel(k):
+            rel_code[k] = ring.tile([P, 2 * P], U32, name="rel_code", align_bytes=64, bufs=6)
+            rel_scale[k] = ring.tile([P, 2 * P], U8, name="rel_scale", align_bytes=64, bufs=6)
+            for c, cell in enumerate(cells(k)):
+                rel_at[cell] = (k, slice(P * c, P * (c + 1)))
             nc.vector.quantize_mx(
-                out=r_code[:, u % 4, P * j0 : P * j1].bitcast(E5M2),
-                scales=r_scale[:, u % 4, P * j0 : P * j1],
-                in_=dzr_t[u][:, j0:j1, :, :].rearrange("m j p r -> m (j p r)"),
+                out=rel_code[k][:].bitcast(E5M2),
+                scales=rel_scale[k][:],
+                in_=rel_t[k][:].rearrange("m g p h -> m (g p h)").bitcast(BF16),
             )
+
+        def by_four(ap):
+            return ap.rearrange("p j (c i) -> p c j i", i=4)
 
         def make_p(t, half):
-            if t not in p_t:
-                p_t[t] = two.tile([P, H, 4], BF16, name="p_tile", align_bytes=64)
+            if half == 0:
+                p_t[t] = ring.tile([P, H, 4], BF16, name="staged", align_bytes=64)
             cols = slice(256 * half, 256 * (half + 1))
             nc.vector.tensor_tensor(
-                out=p_t[t][:, cols, :].rearrange("p (c i) t -> p c t i", i=4),
-                in0=z_t[t][:, :, cols].rearrange("p t (c i) -> p c t i", i=4),
-                in1=rz_t[t][:, :, cols].rearrange("p t (c i) -> p c t i", i=4),
+                out=by_four(p_t[t][:, cols, :].rearrange("p c j -> p j c")),
+                in0=by_four(z_t[t][:, :, cols]),
+                in1=by_four(rz_t[t][:, :, cols]),
                 op=ALU.mult,
             )
 
-        def q_p(t):
+        def quantize_p(t):
             nc.vector.quantize_mx(
-                out=p_code[:, t, :].bitcast(E4M3),
-                scales=p_scale[:, t, :],
-                in_=p_t[t][:].rearrange("p h t -> p (h t)"),
+                out=p_code[:, t, :].bitcast(E4M3), scales=p_scale[:, t, :], in_=p_t[t][:].rearrange("p h j -> p (h j)")
             )
 
-        d2_t = {}
-
-        def make_d2(g, eng="v"):
-            d2 = two.tile([P, H, 4], BF16, name="d2", align_bytes=64)
-            v = d_sb[:, g, :, :].rearrange("p t (c i) -> p c t i", i=4)
-            if eng == "s":
-                nc.scalar.activation(out=d2[:].rearrange("p (c i) t -> p c t i", i=4), in_=v, func=ACT.Square)
-            else:
-                nc.vector.tensor_tensor(out=d2[:].rearrange("p (c i) t -> p c t i", i=4), in0=v, in1=v, op=ALU.mult)
-            d2_t[g] = d2
-
-        def q_d(g):
-            nc.vector.quantize_mx(
-                out=d2_code[:, g, :].bitcast(E4M3),
-                scales=d2_scale[:, g, :],
-                in_=d2_t[g][:].rearrange("p h t -> p (h t)"),
+        def make_d2(g):
+            d2_t[g] = ring.tile([P, H, 4], BF16, name="staged", align_bytes=64)
+            nc.vector.tensor_tensor(
+                out=by_four(d2_t[g][:].rearrange("p c j -> p j c")),
+                in0=by_four(d_t[g][:]),
+                in1=by_four(d_t[g][:]),
+                op=ALU.mult,
             )
 
-        o0_t, o0_bank = {}, {}
+        def quantize_d2(g):
+            nc.vector.quantize_mx(
+                out=d2_code[:, g, :].bitcast(E4M3), scales=d2_scale[:, g, :], in_=d2_t[g][:].rearrange("p h j -> p (h j)")
+            )
 
-        def mm0(t, j, spare=False):
-            if spare:
-                bank = ps_wk.tile([P, H], F32, name="bank")
-            else:
-                bank = ps_o0.tile([P, H], F32, name="o0_bank_tile")
+        o0_bank, o0_t, acc, o1_t = {}, {}, {}, {}
+
+        def matmul_0(k):
+            o0_bank[k] = ps_o0.tile([P, H], F32, name="o0_bank")
             for g in range(NG):
-                u = NG * t + g
+                step, cols = rel_at[k, g]
                 nc.tensor.matmul_mx(
-                    out=bank[:],
-                    lhsT=r_code[:, u % 4, P * j : P * (j + 1)].bitcast(E5M2),
-                    lhsT_scale=r_scale[:, u % 4, P * j : P * (j + 1)],
+                    out=o0_bank[k][:],
+                    lhsT=rel_code[step][:, cols].bitcast(E5M2),
+                    lhsT_scale=rel_scale[step][:, cols],
                     rhs=d2_code[:, g, :].bitcast(E4M3),
                     rhs_scale=d2_scale[:, g, :],
                     start=(g == 0),
                     stop=(g == NG - 1),
                 )
-            o0_bank[t, j] = bank
 
-        def ev0(t, j):
-            if t not in o0_t:
-                o0_t[t] = two.tile([P, 4, H], F32, name="o0_tile")
+        def finish_0(k):
+            t, j = divmod(k, 4)
+            if j % 2 == 0:
+                o0_t[k // 2] = ring.tile([P, 2, H], F32, name="out_rows", bufs=8)
             nc.vector.scalar_tensor_tensor(
-                out=o0_t[t][:, j, :], in0=o0_bank[t, j][:], scalar=-1.0, in1=rz_t[t][:, j, :], op0=ALU.mult, op1=ALU.mult
+                out=o0_t[k // 2][:, j % 2, :],
+                in0=o0_bank[k][:],
+                scalar=-1.0,
+                in1=rz_t[t][:, j, :],
+                op0=ALU.mult,
+                op1=ALU.mult,
             )
 
-        def st0(t, j0, j1):
-            dst = out_0[512 * t : 512 * (t + 1), :].rearrange("(p j) h -> p j h", j=4)
-            nc.sync.dma_start(out=dst[:, j0:j1, :], in_=o0_t[t][:, j0:j1, :])
-
-        acc = {}
-
-        def mm1(t, g):
-            u = NG * t + g
-            for r in range(4):
-                if t == 0:
-                    acc[g, r] = ps_acc.tile([P, H], F32, name="acc%d" % r)
-                nc.tensor.matmul_mx(
-                    out=acc[g, r][:],
-                    lhsT=t_code[:, slot(u), P * r : P * (r + 1)].bitcast(E5M2),
-                    lhsT_scale=t_scale[:, slot(u), P * r : P * (r + 1)],
-                    rhs=p_code[:, t, :].bitcast(E4M3),
-                    rhs_scale=p_scale[:, t, :],
-                    start=(t == 0),
-                    stop=(t == NT - 1),
-                )
-
-        o1_t = {}
-
-        def ev1(g, r):
-            if g not in o1_t:
-                o1_t[g] = two.tile([P, 4, H], F32, name="o1_tile")
-            nc.vector.scalar_tensor_tensor(
-                out=o1_t[g][:, r, :], in0=acc[g, r][:], scalar=-2.0, in1=d_sb[:, g, r, :], op0=ALU.mult, op1=ALU.mult
+        def store_0(k0, k1):
+            t, j = divmod(k0, 4)
+            nc.sync.dma_start(
+                out=token_rows(out_0, t)[:, j : j + k1 - k0, :], in_=o0_t[k0 // 2][:, k0 % 2 : k0 % 2 + k1 - k0, :]
             )
 
-        def st1(g, r0, r1):
-            dst = out_1[512 * g : 512 * (g + 1), :].rearrange("(m r) h -> m r h", r=4)
-            nc.sync.dma_start(out=dst[:, r0:r1, :], in_=o1_t[g][:, r0:r1, :])
+        def matmul_1(t, g, r):
+            if t == 0:
+                acc[g, r] = ps_acc.tile([P, H], F32, name="acc%d" % r)
+            nc.tensor.matmul_mx(
+                out=acc[g, r][:],
+                lhsT=tok_code[:, t, g, P * r : P * (r + 1)].bitcast(E5M2),
+                lhsT_scale=tok_scale[:, t, g, P * r : P * (r + 1)],
+                rhs=p_code[:, t, :].bitcast(E4M3),
+                rhs_scale=p_scale[:, t, :],
+                start=(t == 0),
+                stop=(t == NT - 1),
+            )
 
-        load_s(0, 0, 1)
-        act(0, ACT.Tanh, 0, 1)
-        act(0, ACT.Square, 0, 1)
+        def finish_1(g, r):
+            if r % 2 == 0:
+                o1_t[g, r // 2] = ring.tile([P, 2, H], F32, name="out_rows", bufs=8)
+            nc.vector.scalar_tensor_tensor(
+                out=o1_t[g, r // 2][:, r % 2, :],
+                in0=acc[g, r][:],
+                scalar=-2.0,
+                in1=d_t[g][:, r, :],
+                op0=ALU.mult,
+                op1=ALU.mult,
+            )
+
+        def store_1(g, r0, r1):
+            nc.sync.dma_start(
+                out=token_rows(out_1, g)[:, r0:r1, :], in_=o1_t[g, r0 // 2][:, r0 % 2 : r0 % 2 + r1 - r0, :]
+            )
+
+
+        def share(t, g):
+            interleave(t, g, 0, SHARES[t], nc.scalar.copy)
+            interleave(t, g, SHARES[t], P, nc.vector.tensor_copy)
+
+        def load_rest(t, piece):
+            if piece == 0:
+                load_z(t)
+            else:
+                load_rz(t, piece - 1)
+
+        def load_step(k):
+            row = cells(k)[0][0]
+            if row // 2 not in s_t:
+                s_t[row // 2] = ring.tile([P, 2, R], F32, name="s_rows", bufs=4)
+            pair = token_rows(scores, row // 4)[:, row % 4 // 2 * 2 : row % 4 // 2 * 2 + 2, :]
+            nc.sync.dma_start(out=part(s_t[row // 2], k), in_=part(pair, k))
+
+        last = NT - 1
+
+        load_s(0, 1)
         load_d(0)
-        make_d2(0)
-        load_s(0, 3, 4)
-        act(0, ACT.Tanh, 3, 4)
-        load_s(0, 1, 2)
-        act(0, ACT.Tanh, 1, 2)
-        act(0, ACT.Square, 1, 2)
-        act(0, ACT.Square, 3, 4)
-        load_g(0, 0, 512)
-        stt(0, 0, 1)
-        load_s(0, 2, 3)
-        act(0, ACT.Tanh, 2, 3)
-        act(0, ACT.Square, 2, 3)
-        stt(0, 1, 2)
-        tr(0, 0)
-        cp(0, 0, "s")
-        load_s(1)
-        act(1, ACT.Tanh, 2, 4)
-        q_d(0)
-        stt(0, 3, 4)
-        stt(0, 2, 3)
-        tr(0, 1)
-        il(0, 0, 4, "v")
+        load_s(1, 2)
+        load_g(0)
+        load_s(2, 3)
         load_d(1)
-        make_d2(1)
-        q_t(0)
-        q_d(1)
-        act(1, ACT.Tanh, 0, 2)
-        act(1, ACT.Square, 2, 4)
-        load_g(0, 512, 1024)
-        act(1, ACT.Square, 0, 2)
-        stt(1)
-        tr(1, 0)
-        cp(0, 1, "s")
-        tr(1, 1)
-        q_r(0)
-        load_s(2)
-        act(2, ACT.Tanh, 0, 2)
-        act(2, ACT.Tanh, 2, 4)
-        act(2, ACT.Square, 0, 2)
-        il(1, 1, 4, "v")
-        load_z(0)
-        load_rz(0)
-        make_p(0, 0)
-        make_p(0, 1)
-        act(2, ACT.Square, 2, 4)
-        cp(1, 1, "s")
-        cp(1, 0, "s")
-        q_r(1)
-        mm0(0, 0)
-        mm0(0, 1)
-        q_p(0)
-        il(1, 0, 1, "s")
-        q_t(1)
-        ev0(0, 0)
-        mm0(0, 2)
-        load_s(3)
-        act(3, ACT.Tanh, 0, 2)
-        act(3, ACT.Tanh, 2, 4)
-        act(3, ACT.Square, 0, 2)
-        load_g(1)
-        stt(2)
-        tr(2, 0)
-        tr(2, 1)
-        ev0(0, 1)
-        act(3, ACT.Square, 2, 4)
-        load_s(4)
-        act(4, ACT.Tanh, 0, 2)
-        act(4, ACT.Tanh, 2, 4)
-        cp(2, 0, "s")
-        stt(3)
-        il(3, 0, 2, "s")
-        act(4, ACT.Square, 0, 2)
-        ev0(0, 2)
-        il(3, 2, 4, "v")
-        cp(2, 1, "s")
-        mm0(0, 3)
-        ev0(0, 3)
-        il(2, 1, 4, "v")
-        load_rz(1)
-        load_z(1)
-        make_p(1, 0)
-        q_r(2)
-        make_p(1, 1)
-        tr(3, 0)
-        il(2, 0, 1, "s")
+        load_s(3, 4)
         load_g(2)
-        act(4, ACT.Square, 2, 4)
-        stt(4)
-        q_p(1)
-        tr(3, 1)
-        cp(3, 1, "s")
-        cp(3, 0, "s")
-        q_r(3)
-        tr(4, 0)
-        tr(4, 1)
-        load_s(5)
-        act(5, ACT.Tanh, 2, 4)
-        act(5, ACT.Square, 2, 4)
-        act(5, ACT.Tanh, 0, 2)
-        act(5, ACT.Square, 0, 2)
-        cp(4, 0, "s")
-        q_t(3)
-        il(4, 0, 2, "s")
-        q_t(2)
-        cp(4, 1, "s")
-        load_rz(2)
-        load_z(2)
-        make_p(2, 0)
-        load_s(6)
-        act(6, ACT.Tanh, 0, 2)
-        load_s(7)
-        act(7, ACT.Tanh, 0, 2)
-        mm0(1, 0)
-        ev0(1, 0)
-        mm0(1, 1)
-        mm0(1, 2)
-        make_p(2, 1)
-        ev0(1, 1)
-        stt(5)
-        il(4, 2, 4, "v")
-        mm0(1, 3)
-        q_r(4)
-        ev0(1, 2)
-        q_p(2)
-        mm1(0, 0)
-        tr(5, 0)
-        mm1(1, 0)
-        tr(5, 1)
-        q_t(4)
-        mm1(2, 0)
-        load_z(3)
-        load_rz(3)
-        make_p(3, 0)
-        make_p(3, 1)
-        act(6, ACT.Tanh, 2, 4)
-        act(6, ACT.Square, 0, 2)
-        act(7, ACT.Tanh, 2, 4)
-        load_g(3)
-        act(6, ACT.Square, 2, 4)
-        stt(6)
-        cp(5, 0, "s")
-        tr(6, 0)
-        cp(5, 1, "s")
-        tr(6, 1)
-        ev0(1, 3)
-        q_r(5)
-        mm0(2, 0)
-        mm0(2, 1)
-        act(7, ACT.Square, 2, 4)
-        il(5, 3, 4, "v")
-        act(7, ACT.Square, 0, 2)
-        stt(7)
-        il(6, 0, 4, "s")
-        q_t(6)
-        cp(6, 0, "s")
-        tr(7, 0)
-        cp(6, 1, "s")
-        tr(7, 1)
-        cp(7, 1, "s")
-        q_p(3)
-        mm1(3, 0)
-        st0(0, 0, 4)
-        ev0(2, 1)
-        ev0(2, 0)
-        mm0(2, 2)
-        mm0(2, 3)
-        q_r(6)
-        ev1(0, 0)
-        ev1(0, 1)
-        ev1(0, 2)
-        st0(1, 0, 4)
-        ev1(0, 3)
-        st1(0, 0, 4)
-        mm1(0, 1)
-        cp(7, 0, "s")
-        q_r(7)
-        il(5, 0, 3, "s")
-        q_t(5)
-        ev0(2, 2)
-        ev0(2, 3)
-        st0(2, 0, 4)
-        il(7, 2, 4, "v")
-        il(7, 0, 2, "s")
-        mm0(3, 0, spare=True)
-        mm0(3, 1, spare=True)
-        ev0(3, 1)
-        q_t(7)
-        ev0(3, 0)
-        st0(3, 0, 2)
-        mm1(1, 1)
-        mm1(2, 1)
-        mm1(3, 1)
-        ev1(1, 0)
-        ev1(1, 1)
-        st1(1, 0, 2)
-        ev1(1, 3)
-        ev1(1, 2)
-        st1(1, 2, 4)
-        mm0(3, 2)
-        ev0(3, 2)
-        st0(3, 2, 3)
-        mm0(3, 3)
-        ev0(3, 3)
-        st0(3, 3, 4)
+        rest = [(t, piece) for t in range(NT) for piece in range(3)]
+        make_d2(0)
+        tanh(0)
+        square(0)
+        tanh(1)
+        square(1)
+        quantize_d2(0)
+        for k in range(ROWS):
+            t, j = divmod(k, 4)
+            ahead = k + AHEAD
+            if ahead < ROWS:
+                load_step(ahead)
+                load_rest(*rest[k])
+                if cells(ahead)[0][0] % 2 == 0 and cells(ahead)[0][1] == 0:
+                    load_g(cells(ahead)[0][0])
+            if k >= ROWS - AHEAD:
+                store_0(2 * (k - ROWS + AHEAD), 2 * (k - ROWS + AHEAD) + 2)
+            make_dz(k)
+            transpose(k)
+            if k + 2 < ROWS:
+                tanh(k + 2)
+            if k >= 1:
+                copy_words(k - 1)
+            if k + 2 < ROWS:
+                square(k + 2)
+            if k == ROWS - 2:
+                share(last, 0)
+            if k in (LATE, LATE + 2):
+                interleave(1 + (k - LATE) // 2, 1, 0, P, nc.scalar.copy)
+            if t > 0 and j == 0:
+                share(t - 1, 0)
+            if k == 5:
+                interleave(0, 1, 0, P, nc.scalar.copy)
+            if k == 1:
+                make_d2(1)
+            if k == 2:
+                quantize_d2(1)
+            if k >= 3:
+                quantize_rel(k - 3)
+            if k >= 4:
+                matmul_0(k - 4)
+            if k >= 5:
+                finish_0(k - 5)
+            if t > 0 and j == (2 if t == 2 else 1):
+                quantize_tok(t - 1, 0)
+            if k == 7:
+                quantize_tok(0, 1)
+            if k in (LATE + 2, LATE + 4):
+                quantize_tok((k - LATE) // 2, 1)
+            for tp, first in enumerate(P_STEPS):
+                if k == first + 2:
+                    quantize_p(tp)
+            for tp, first in enumerate(P_STEPS):
+                if first <= k < first + 2:
+                    make_p(tp, k - first)
+            if t > 0 and j == (1 if t == last else 3):
+                for r in range(4):
+                    matmul_1(t - 1, 0, r)
+            if k == Q30:
+                quantize_tok(last, 0)
+                for r in range(4):
+                    matmul_1(last, 0, r)
+
+        store_0(ROWS - 8, ROWS - 6)
+        copy_words(ROWS - 1)
+        interleave(last, 1, 0, P, nc.scalar.copy)
+        quantize_rel(ROWS - 3)
+        quantize_rel(ROWS - 2)
+        matmul_0(ROWS - 4)
+        finish_0(ROWS - 5)
+        matmul_0(ROWS - 3)
+        store_0(ROWS - 6, ROWS - 4)
+        for r in range(2):
+            finish_1(0, r)
+            for tt in range(last):
+                matmul_1(tt, 1, r)
+        store_1(0, 0, 2)
+        quantize_rel(ROWS - 1)
+        for r in range(2):
+            finish_0(ROWS - 4 + r)
+            matmul_0(ROWS - 2 + r)
+        store_0(ROWS - 4, ROWS - 2)
+        finish_1(0, 2)
+        for tt in range(last):
+            matmul_1(tt, 1, 2)
+        finish_1(0, 3)
+        store_1(0, 2, 4)
+        quantize_tok(last, 1)
+        for r in range(3):
+            matmul_1(last, 1, r)
+        for tt in range(NT):
+            matmul_1(tt, 1, 3)
+        for r in range(2):
+            finish_0(ROWS - 2 + r)
+            store_0(ROWS - 2 + r, ROWS - 1 + r)
+        for r in range(4):
+            finish_1(1, r)
+            store_1(1, r, r + 1)

@@ -21,12 +21,8 @@ P = 128
 NT = B // 512
 NG = R // 512
 ROWS = 4 * NT
-SHARES = (0, 128, 0, 0)
-LATE = 11
-Q30 = 14
 AHEAD = 4
 P_STEPS = (5, 7, 9, 12)
-VECTOR_COPIES = 0
 
 
 def tile_dedicomdecoder_v_kernel(tc, z_i, z_j, w_r, d_w, rz_in, scores, grad_out, out_0, out_1):
@@ -34,8 +30,7 @@ def tile_dedicomdecoder_v_kernel(tc, z_i, z_j, w_r, d_w, rz_in, scores, grad_out
     with ExitStack() as ctx:
         keep = ctx.enter_context(tc.tile_pool(name="keep", bufs=1))
         ring = ctx.enter_context(tc.tile_pool(name="ring", bufs=2))
-        ps_tr = ctx.enter_context(tc.psum_pool(name="ps_tr", bufs=2))
-        ps_o0 = ctx.enter_context(tc.psum_pool(name="ps_o0", bufs=2))
+        ps_work = ctx.enter_context(tc.psum_pool(name="ps_work", bufs=1))
         ps_acc = ctx.enter_context(tc.psum_pool(name="ps_acc", bufs=1))
         ctx.enter_context(tc.manual_schedule())
 
@@ -72,6 +67,8 @@ def tile_dedicomdecoder_v_kernel(tc, z_i, z_j, w_r, d_w, rz_in, scores, grad_out
 
         ident = keep.tile([P, P], F32, name="ident")
         make_identity(nc, ident[:])
+        ident_bf = keep.tile([P, P], BF16, name="ident_bf")
+        make_identity(nc, ident_bf[:])
 
         d2_code = keep.tile([P, NG, H], U32, name="d2_code", align_bytes=64)
         d2_scale = keep.tile([P, NG, H], U8, name="d2_scale", align_bytes=64)
@@ -109,34 +106,65 @@ def tile_dedicomdecoder_v_kernel(tc, z_i, z_j, w_r, d_w, rz_in, scores, grad_out
             t, pair = divmod(pair_of(k), 2)
             if k % 4 == 0:
                 dz_t[t] = ring.tile([P, 4, R], BF16, name="dz", bufs=3)
+            grad = part(g_t[pair_of(k)], k)
+            if k in g_bank:
+                grad = g_bank[k][:] if k >= ROWS - 4 else g_bank[k][:].rearrange("p c n -> p (c n)")
             nc.vector.scalar_tensor_tensor(
                 out=part(dz_t[t][:, 2 * pair : 2 * pair + 2, :], k),
                 in0=part(s_t[pair_of(k)], k),
                 scalar=0.25,
-                in1=part(g_t[pair_of(k)], k),
+                in1=grad,
                 op0=ALU.subtract,
                 op1=ALU.mult,
             )
 
-        def interleave(t, g, m0, m1, copy):
-            if m0 == m1:
-                return
-            if (t, g) not in tok_t:
-                tok_t[t, g] = ring.tile([P, 4, P, 4], BF16, name="tok", align_bytes=64, bufs=3)
-            copy(
-                out=tok_t[t, g][:, :, m0:m1, :].rearrange("p r m j -> p m j r"),
-                in_=dz_t[t][:, :, 512 * g : 512 * (g + 1)].rearrange("p j (m r) -> p m j r", r=4)[:, m0:m1, :, :],
+        def tok_tile(t, g, half, tag):
+            tok_t[t, g, half] = ring.tile([P, 2, P, 4], BF16, name=tag, align_bytes=64)
+            return tok_t[t, g, half]
+
+        def tok_source(t, g, half):
+            by_r = dz_t[t][:, :, 512 * g : 512 * (g + 1)].rearrange("p j (m r) -> p r m j", r=4)
+            return by_r[:, 2 * half : 2 * half + 2, :, :]
+
+        def interleave_gpsimd(t, g, half):
+            nc.gpsimd.tensor_scalar(
+                out=tok_tile(t, g, half, "tok_g")[:],
+                in0=tok_source(t, g, half),
+                scalar1=1.0,
+                scalar2=-0.0,
+                op0=ALU.mult,
+                op1=ALU.add,
             )
 
-        def quantize_tok(t, g):
-            nc.vector.quantize_mx(
-                out=tok_code[:, t, g, :].bitcast(E5M2),
-                scales=tok_scale[:, t, g, :],
-                in_=tok_t[t, g][:].rearrange("p r m j -> p (r m j)"),
+        def interleave_scalar(t, g, half):
+            nc.scalar.copy(
+                out=tok_tile(t, g, half, "tok_s")[:].rearrange("p r m j -> p m j r"),
+                in_=tok_source(t, g, half).rearrange("p r m j -> p m j r"),
             )
+
+        def quantize_tok(t, g, half):
+            cols = slice(256 * half, 256 * (half + 1))
+            nc.vector.quantize_mx(
+                out=tok_code[:, t, g, cols].bitcast(E5M2),
+                scales=tok_scale[:, t, g, cols],
+                in_=tok_t[t, g, half][:].rearrange("p r m j -> p (r m j)"),
+            )
+
+        g_bank = {}
+
+        def stage_g(k):
+            g_bank[k] = ps_work.tile([P, 2, 512], BF16, name="g_bank")
+            for c, (row, g) in enumerate(cells(k)):
+                nc.tensor.matmul(
+                    out=g_bank[k][:, c, :],
+                    lhsT=ident_bf[:],
+                    rhs=g_t[row // 2][:, row % 2, 512 * g : 512 * (g + 1)],
+                    start=True,
+                    stop=True,
+                )
 
         def transpose(k):
-            bank_t[k] = ps_tr.tile([P, 2, 2, P], F32, name="tr_bank")
+            bank_t[k] = ps_work.tile([P, 2, 2, P], F32, name="tr_bank", bufs=2)
             for c, (row, g) in enumerate(cells(k)):
                 words = dz_t[row // 4][:, row % 4, :].bitcast(F32)
                 for h in range(2):
@@ -144,8 +172,7 @@ def tile_dedicomdecoder_v_kernel(tc, z_i, z_j, w_r, d_w, rz_in, scores, grad_out
 
         def copy_words(k):
             rel_t[k] = ring.tile([P, NG, P, 2], F32, name="rel", align_bytes=64, bufs=3)
-            copy = nc.vector.tensor_copy if k < VECTOR_COPIES else nc.scalar.copy
-            copy(out=rel_t[k][:], in_=bank_t[k][:].rearrange("m g h p -> m g p h"))
+            nc.scalar.copy(out=rel_t[k][:], in_=bank_t[k][:].rearrange("m g h p -> m g p h"))
 
         def quantize_rel(k):
             rel_code[k] = ring.tile([P, 2 * P], U32, name="rel_code", align_bytes=64, bufs=6)
@@ -193,8 +220,8 @@ def tile_dedicomdecoder_v_kernel(tc, z_i, z_j, w_r, d_w, rz_in, scores, grad_out
 
         o0_bank, o0_t, acc, o1_t = {}, {}, {}, {}
 
-        def matmul_0(k):
-            o0_bank[k] = ps_o0.tile([P, H], F32, name="o0_bank")
+        def matmul_0(k, tag="o0_bank"):
+            o0_bank[k] = ps_work.tile([P, H], F32, name=tag)
             for g in range(NG):
                 step, cols = rel_at[k, g]
                 nc.tensor.matmul_mx(
@@ -257,10 +284,6 @@ def tile_dedicomdecoder_v_kernel(tc, z_i, z_j, w_r, d_w, rz_in, scores, grad_out
             )
 
 
-        def share(t, g):
-            interleave(t, g, 0, SHARES[t], nc.scalar.copy)
-            interleave(t, g, SHARES[t], P, nc.vector.tensor_copy)
-
         def load_rest(t, piece):
             if piece == 0:
                 load_z(t)
@@ -275,14 +298,15 @@ def tile_dedicomdecoder_v_kernel(tc, z_i, z_j, w_r, d_w, rz_in, scores, grad_out
             nc.sync.dma_start(out=part(s_t[row // 2], k), in_=part(pair, k))
 
         last = NT - 1
+        halves = [(t, g, half) for t in range(NT) for g in range(NG) for half in range(2)]
 
-        load_s(0, 1)
+        load_step(0)
         load_d(0)
-        load_s(1, 2)
+        load_step(1)
         load_g(0)
-        load_s(2, 3)
+        load_step(2)
         load_d(1)
-        load_s(3, 4)
+        load_step(3)
         load_g(2)
         rest = [(t, piece) for t in range(NT) for piece in range(3)]
         make_d2(0)
@@ -302,6 +326,10 @@ def tile_dedicomdecoder_v_kernel(tc, z_i, z_j, w_r, d_w, rz_in, scores, grad_out
             if k >= ROWS - AHEAD:
                 store_0(2 * (k - ROWS + AHEAD), 2 * (k - ROWS + AHEAD) + 2)
             make_dz(k)
+            if k >= 4:
+                interleave_gpsimd(*halves[k - 4])
+            if 3 <= k < ROWS - 1:
+                stage_g(k + 1)
             transpose(k)
             if k + 2 < ROWS:
                 tanh(k + 2)
@@ -310,49 +338,46 @@ def tile_dedicomdecoder_v_kernel(tc, z_i, z_j, w_r, d_w, rz_in, scores, grad_out
             if k + 2 < ROWS:
                 square(k + 2)
             if k == ROWS - 2:
-                share(last, 0)
-            if k in (LATE, LATE + 2):
-                interleave(1 + (k - LATE) // 2, 1, 0, P, nc.scalar.copy)
-            if t > 0 and j == 0:
-                share(t - 1, 0)
-            if k == 5:
-                interleave(0, 1, 0, P, nc.scalar.copy)
+                interleave_scalar(last, 0, 0)
+                interleave_scalar(last, 0, 1)
+            if k >= 5:
+                finish_0(k - 5)
+            if k >= 4:
+                matmul_0(k - 4)
             if k == 1:
                 make_d2(1)
             if k == 2:
                 quantize_d2(1)
-            if k >= 3:
-                quantize_rel(k - 3)
-            if k >= 4:
-                matmul_0(k - 4)
-            if k >= 5:
-                finish_0(k - 5)
-            if t > 0 and j == (2 if t == 2 else 1):
-                quantize_tok(t - 1, 0)
-            if k == 7:
-                quantize_tok(0, 1)
-            if k in (LATE + 2, LATE + 4):
-                quantize_tok((k - LATE) // 2, 1)
             for tp, first in enumerate(P_STEPS):
                 if k == first + 2:
                     quantize_p(tp)
             for tp, first in enumerate(P_STEPS):
                 if first <= k < first + 2:
                     make_p(tp, k - first)
-            if t > 0 and j == (1 if t == last else 3):
+            if k >= 5:
+                quantize_tok(*halves[k - 5])
+            if k >= 3:
+                quantize_rel(k - 3)
+            if 0 < t < last and j == 3:
                 for r in range(4):
                     matmul_1(t - 1, 0, r)
-            if k == Q30:
-                quantize_tok(last, 0)
+            if k == ROWS - 2:
+                for r in range(4):
+                    matmul_1(last - 1, 0, r)
+            if k == ROWS - 1:
+                quantize_tok(last, 0, 0)
+                quantize_tok(last, 0, 1)
                 for r in range(4):
                     matmul_1(last, 0, r)
 
-        store_0(ROWS - 8, ROWS - 6)
         copy_words(ROWS - 1)
-        interleave(last, 1, 0, P, nc.scalar.copy)
+        interleave_scalar(last, 1, 0)
+        interleave_scalar(last, 1, 1)
+        store_0(ROWS - 8, ROWS - 6)
+        quantize_tok(last - 1, 1, 1)
         quantize_rel(ROWS - 3)
         quantize_rel(ROWS - 2)
-        matmul_0(ROWS - 4)
+        matmul_0(ROWS - 4, "g_bank")
         finish_0(ROWS - 5)
         matmul_0(ROWS - 3)
         store_0(ROWS - 6, ROWS - 4)
@@ -364,14 +389,15 @@ def tile_dedicomdecoder_v_kernel(tc, z_i, z_j, w_r, d_w, rz_in, scores, grad_out
         quantize_rel(ROWS - 1)
         for r in range(2):
             finish_0(ROWS - 4 + r)
-            matmul_0(ROWS - 2 + r)
+            matmul_0(ROWS - 2 + r, ("g_bank", "o0_bank")[r])
         store_0(ROWS - 4, ROWS - 2)
         finish_1(0, 2)
         for tt in range(last):
             matmul_1(tt, 1, 2)
         finish_1(0, 3)
         store_1(0, 2, 4)
-        quantize_tok(last, 1)
+        quantize_tok(last, 1, 0)
+        quantize_tok(last, 1, 1)
         for r in range(3):
             matmul_1(last, 1, r)
         for tt in range(NT):

@@ -21,8 +21,14 @@ P = 128
 NT = B // 512
 NG = R // 512
 ROWS = 4 * NT
-AHEAD = 4
-P_STEPS = (5, 7, 9, 12)
+AHEAD = 3
+S_LEAD = 1.5
+G_LEAD = 0.5
+GPSIMD_SHARE = 80
+VECTOR_COPIES = 0
+STAGE_FROM = 4
+PAIRS_FROM = 6
+P_STEPS = (5, 8, 10, 12)
 
 
 def tile_dedicomdecoder_v_kernel(tc, z_i, z_j, w_r, d_w, rz_in, scores, grad_out, out_0, out_1):
@@ -39,14 +45,6 @@ def tile_dedicomdecoder_v_kernel(tc, z_i, z_j, w_r, d_w, rz_in, scores, grad_out
 
         s_t, g_t, z_t, rz_t, d_t = {}, {}, {}, {}, {}
 
-        def load_s(k0, k1):
-            if k0 % 2 == 0:
-                s_t[k0 // 2] = ring.tile([P, 2, R], F32, name="s_rows", bufs=4)
-            nc.sync.dma_start(
-                out=s_t[k0 // 2][:, k0 % 2 : k0 % 2 + k1 - k0, :],
-                in_=token_rows(scores, k0 // 4)[:, k0 % 4 : k0 % 4 + k1 - k0, :],
-            )
-
         def load_g(k):
             g_t[k // 2] = ring.tile([P, 2, R], BF16, name="g_rows", bufs=5)
             nc.sync.dma_start(out=g_t[k // 2][:], in_=token_rows(grad_out, k // 4)[:, k % 4 : k % 4 + 2, :])
@@ -59,11 +57,9 @@ def tile_dedicomdecoder_v_kernel(tc, z_i, z_j, w_r, d_w, rz_in, scores, grad_out
             z_t[t] = ring.tile([P, 4, H], BF16, name="z_rows")
             nc.sync.dma_start(out=z_t[t][:], in_=token_rows(z_i, t))
 
-        def load_rz(t, half):
-            if half == 0:
-                rz_t[t] = ring.tile([P, 4, H], F32, name="rz_rows", bufs=3)
-            rows = slice(2 * half, 2 * half + 2)
-            nc.sync.dma_start(out=rz_t[t][:, rows, :], in_=token_rows(rz_in, t)[:, rows, :])
+        def load_rz(t):
+            rz_t[t] = ring.tile([P, 4, H], F32, name="rz_rows", bufs=3)
+            nc.sync.dma_start(out=rz_t[t][:], in_=token_rows(rz_in, t))
 
         ident = keep.tile([P, P], F32, name="ident")
         make_identity(nc, ident[:])
@@ -92,12 +88,14 @@ def tile_dedicomdecoder_v_kernel(tc, z_i, z_j, w_r, d_w, rz_in, scores, grad_out
         def pair_of(k):
             return cells(k)[0][0] // 2
 
-        def tanh(k):
+        def tanh(k, cols=None):
             s = part(s_t[pair_of(k)], k)
+            s = s[:, cols] if cols else s
             nc.scalar.activation(out=s, in_=s, func=ACT.Tanh, scale=0.5)
 
-        def square(k):
+        def square(k, cols=None):
             s = part(s_t[pair_of(k)], k)
+            s = s[:, cols] if cols else s
             nc.scalar.activation(out=s, in_=s, func=ACT.Square, scale=0.5)
 
         dz_t, tok_t, rel_t, bank_t, rel_code, rel_scale, p_t, d2_t, rel_at = {}, {}, {}, {}, {}, {}, {}, {}, {}
@@ -128,18 +126,19 @@ def tile_dedicomdecoder_v_kernel(tc, z_i, z_j, w_r, d_w, rz_in, scores, grad_out
 
         def interleave_gpsimd(t, g, half):
             nc.gpsimd.tensor_scalar(
-                out=tok_tile(t, g, half, "tok_g")[:],
-                in0=tok_source(t, g, half),
+                out=tok_tile(t, g, half, "tok_g")[:, :, :GPSIMD_SHARE, :],
+                in0=tok_source(t, g, half)[:, :, :GPSIMD_SHARE, :],
                 scalar1=1.0,
                 scalar2=-0.0,
                 op0=ALU.mult,
                 op1=ALU.add,
             )
 
-        def interleave_scalar(t, g, half):
+        def interleave_scalar(t, g, half, m0=0):
+            tile = tok_t[t, g, half] if m0 else tok_tile(t, g, half, "tok_s")
             nc.scalar.copy(
-                out=tok_tile(t, g, half, "tok_s")[:].rearrange("p r m j -> p m j r"),
-                in_=tok_source(t, g, half).rearrange("p r m j -> p m j r"),
+                out=tile[:, :, m0:, :].rearrange("p r m j -> p m j r"),
+                in_=tok_source(t, g, half)[:, :, m0:, :].rearrange("p r m j -> p m j r"),
             )
 
         def quantize_tok(t, g, half):
@@ -172,7 +171,8 @@ def tile_dedicomdecoder_v_kernel(tc, z_i, z_j, w_r, d_w, rz_in, scores, grad_out
 
         def copy_words(k):
             rel_t[k] = ring.tile([P, NG, P, 2], F32, name="rel", align_bytes=64, bufs=3)
-            nc.scalar.copy(out=rel_t[k][:], in_=bank_t[k][:].rearrange("m g h p -> m g p h"))
+            copy = nc.vector.tensor_copy if k < VECTOR_COPIES else nc.scalar.copy
+            copy(out=rel_t[k][:], in_=bank_t[k][:].rearrange("m g h p -> m g p h"))
 
         def quantize_rel(k):
             rel_code[k] = ring.tile([P, 2 * P], U32, name="rel_code", align_bytes=64, bufs=6)
@@ -284,62 +284,63 @@ def tile_dedicomdecoder_v_kernel(tc, z_i, z_j, w_r, d_w, rz_in, scores, grad_out
             )
 
 
-        def load_rest(t, piece):
-            if piece == 0:
-                load_z(t)
-            else:
-                load_rz(t, piece - 1)
-
         def load_step(k):
             row = cells(k)[0][0]
             if row // 2 not in s_t:
                 s_t[row // 2] = ring.tile([P, 2, R], F32, name="s_rows", bufs=4)
             pair = token_rows(scores, row // 4)[:, row % 4 // 2 * 2 : row % 4 // 2 * 2 + 2, :]
-            nc.sync.dma_start(out=part(s_t[row // 2], k), in_=part(pair, k))
+            if PAIRS_FROM <= k < ROWS - 4:
+                nc.sync.dma_start(out=s_t[row // 2][:], in_=pair)
+            else:
+                nc.sync.dma_start(out=part(s_t[row // 2], k), in_=part(pair, k))
 
         last = NT - 1
         halves = [(t, g, half) for t in range(NT) for g in range(NG) for half in range(2)]
 
-        load_step(0)
-        load_d(0)
-        load_step(1)
-        load_g(0)
-        load_step(2)
-        load_d(1)
-        load_step(3)
-        load_g(2)
-        rest = [(t, piece) for t in range(NT) for piece in range(3)]
+        loads = [(k - S_LEAD, load_step, (k,)) for k in range(ROWS) if k % 2 == 0 or not PAIRS_FROM <= k < ROWS - 4]
+        loads += [(2 * g - 1, load_d, (g,)) for g in range(NG)]
+        loads += [(k - G_LEAD, load_g, (cells(k)[0][0],)) for k in range(ROWS) if cells(k)[0][0] % 2 == 0 and cells(k)[0][1] == 0]
+        for t in range(NT):
+            loads += [(P_STEPS[t], load_rz, (t,)), (P_STEPS[t], load_z, (t,))]
+        loads = sorted(loads, key=lambda entry: entry[0])
+
+        def issue_loads(k):
+            for need, load, args in loads:
+                if k - 1 + AHEAD < need <= k + AHEAD or (k == 0 and need <= AHEAD):
+                    load(*args)
+
+        issue_loads(0)
         make_d2(0)
-        tanh(0)
-        square(0)
-        tanh(1)
-        square(1)
+        for k in range(2):
+            for func in (tanh, square):
+                func(k, slice(0, 512))
+                func(k, slice(512, R))
         quantize_d2(0)
         for k in range(ROWS):
             t, j = divmod(k, 4)
-            ahead = k + AHEAD
-            if ahead < ROWS:
-                load_step(ahead)
-                load_rest(*rest[k])
-                if cells(ahead)[0][0] % 2 == 0 and cells(ahead)[0][1] == 0:
-                    load_g(cells(ahead)[0][0])
-            if k >= ROWS - AHEAD:
-                store_0(2 * (k - ROWS + AHEAD), 2 * (k - ROWS + AHEAD) + 2)
+            if k > 0:
+                issue_loads(k)
+            if k >= ROWS - 4:
+                store_0(2 * (k - ROWS + 4), 2 * (k - ROWS + 4) + 2)
             make_dz(k)
             if k >= 4:
                 interleave_gpsimd(*halves[k - 4])
-            if 3 <= k < ROWS - 1:
+            if STAGE_FROM - 1 <= k < ROWS - 1:
                 stage_g(k + 1)
             transpose(k)
             if k + 2 < ROWS:
                 tanh(k + 2)
-            if k >= 1:
+            if k > VECTOR_COPIES:
                 copy_words(k - 1)
             if k + 2 < ROWS:
                 square(k + 2)
+            if k >= 4:
+                interleave_scalar(*halves[k - 4], GPSIMD_SHARE)
             if k == ROWS - 2:
                 interleave_scalar(last, 0, 0)
                 interleave_scalar(last, 0, 1)
+            if 1 <= k <= VECTOR_COPIES:
+                copy_words(k - 1)
             if k >= 5:
                 finish_0(k - 5)
             if k >= 4:

@@ -20,15 +20,17 @@ ALU = mybir.AluOpType
 P = 128
 NT = B // 512
 NG = R // 512
-ROWS = 4 * NT
+STEPS = 4 * NT
+LAST = NT - 1
 AHEAD = 3
 S_LEAD = 1.5
 G_LEAD = 0.5
-GPSIMD_SHARE = 80
-VECTOR_COPIES = 0
+PAIRS_FROM = 8
 STAGE_FROM = 4
-PAIRS_FROM = 6
-P_STEPS = (5, 8, 10, 12)
+SCALAR_FROM = 6
+GPSIMD_SHARE = 80
+P_STEPS = (4, 7, 10, 12)
+P_NEED = (3.6, 7, 10, 12)
 
 
 def tile_dedicomdecoder_v_kernel(tc, z_i, z_j, w_r, d_w, rz_in, scores, grad_out, out_0, out_1):
@@ -40,26 +42,51 @@ def tile_dedicomdecoder_v_kernel(tc, z_i, z_j, w_r, d_w, rz_in, scores, grad_out
         ps_acc = ctx.enter_context(tc.psum_pool(name="ps_acc", bufs=1))
         ctx.enter_context(tc.manual_schedule())
 
-        def token_rows(hbm, t):
+        def four_rows(hbm, t):
             return hbm[512 * t : 512 * (t + 1), :].rearrange("(p j) n -> p j n", j=4)
+
+        def cells(k):
+            if k < STEPS - 4:
+                return [(k, 0), (k, 1)]
+            g, pair = divmod(k - (STEPS - 4), 2)
+            return [(STEPS - 4 + 2 * pair, g), (STEPS - 4 + 2 * pair + 1, g)]
+
+        def pair_of(k):
+            return cells(k)[0][0] // 2
+
+        def part(pair_tile, k):
+            (row, g), (row2, g2) = cells(k)
+            if row == row2:
+                return pair_tile[:, row % 2, :]
+            return pair_tile[:, :, 512 * g : 512 * (g + 1)]
 
         s_t, g_t, z_t, rz_t, d_t = {}, {}, {}, {}, {}
 
-        def load_g(k):
-            g_t[k // 2] = ring.tile([P, 2, R], BF16, name="g_rows", bufs=5)
-            nc.sync.dma_start(out=g_t[k // 2][:], in_=token_rows(grad_out, k // 4)[:, k % 4 : k % 4 + 2, :])
+        def load_s(k):
+            pair = pair_of(k)
+            if pair not in s_t:
+                s_t[pair] = ring.tile([P, 2, R], F32, name="s_rows", bufs=4)
+            src = four_rows(scores, pair // 2)[:, pair % 2 * 2 : pair % 2 * 2 + 2, :]
+            if PAIRS_FROM <= k < STEPS - 4:
+                nc.sync.dma_start(out=s_t[pair][:], in_=src)
+            else:
+                nc.sync.dma_start(out=part(s_t[pair], k), in_=part(src, k))
+
+        def load_g(pair):
+            g_t[pair] = ring.tile([P, 2, R], BF16, name="g_rows", bufs=5)
+            nc.sync.dma_start(out=g_t[pair][:], in_=four_rows(grad_out, pair // 2)[:, pair % 2 * 2 : pair % 2 * 2 + 2, :])
 
         def load_d(g):
             d_t[g] = keep.tile([P, 4, H], BF16, name="d_rows%d" % g)
-            nc.sync.dma_start(out=d_t[g][:], in_=token_rows(d_w, g))
+            nc.sync.dma_start(out=d_t[g][:], in_=four_rows(d_w, g))
 
         def load_z(t):
             z_t[t] = ring.tile([P, 4, H], BF16, name="z_rows")
-            nc.sync.dma_start(out=z_t[t][:], in_=token_rows(z_i, t))
+            nc.sync.dma_start(out=z_t[t][:], in_=four_rows(z_i, t))
 
         def load_rz(t):
             rz_t[t] = ring.tile([P, 4, H], F32, name="rz_rows", bufs=3)
-            nc.sync.dma_start(out=rz_t[t][:], in_=token_rows(rz_in, t))
+            nc.sync.dma_start(out=rz_t[t][:], in_=four_rows(rz_in, t))
 
         ident = keep.tile([P, P], F32, name="ident")
         make_identity(nc, ident[:])
@@ -70,86 +97,12 @@ def tile_dedicomdecoder_v_kernel(tc, z_i, z_j, w_r, d_w, rz_in, scores, grad_out
         d2_scale = keep.tile([P, NG, H], U8, name="d2_scale", align_bytes=64)
         p_code = keep.tile([P, NT, H], U32, name="p_code", align_bytes=64)
         p_scale = keep.tile([P, NT, H], U8, name="p_scale", align_bytes=64)
-        tok_code = keep.tile([P, NT, NG, 512], U32, name="tok_code", align_bytes=64)
-        tok_scale = keep.tile([P, NT, NG, 512], U8, name="tok_scale", align_bytes=64)
 
-        def cells(k):
-            if k < ROWS - 4:
-                return [(k, 0), (k, 1)]
-            g, pair = divmod(k - (ROWS - 4), 2)
-            return [(ROWS - 4 + 2 * pair, g), (ROWS - 4 + 2 * pair + 1, g)]
+        def activate(func, k, cols=slice(None)):
+            s = part(s_t[pair_of(k)], k)[:, cols]
+            nc.scalar.activation(out=s, in_=s, func=func, scale=0.5)
 
-        def part(pair_tile, k):
-            (row, g), (row2, g2) = cells(k)
-            if row == row2:
-                return pair_tile[:, row % 2, :]
-            return pair_tile[:, :, 512 * g : 512 * (g + 1)]
-
-        def pair_of(k):
-            return cells(k)[0][0] // 2
-
-        def tanh(k, cols=None):
-            s = part(s_t[pair_of(k)], k)
-            s = s[:, cols] if cols else s
-            nc.scalar.activation(out=s, in_=s, func=ACT.Tanh, scale=0.5)
-
-        def square(k, cols=None):
-            s = part(s_t[pair_of(k)], k)
-            s = s[:, cols] if cols else s
-            nc.scalar.activation(out=s, in_=s, func=ACT.Square, scale=0.5)
-
-        dz_t, tok_t, rel_t, bank_t, rel_code, rel_scale, p_t, d2_t, rel_at = {}, {}, {}, {}, {}, {}, {}, {}, {}
-
-        def make_dz(k):
-            t, pair = divmod(pair_of(k), 2)
-            if k % 4 == 0:
-                dz_t[t] = ring.tile([P, 4, R], BF16, name="dz", bufs=3)
-            grad = part(g_t[pair_of(k)], k)
-            if k in g_bank:
-                grad = g_bank[k][:] if k >= ROWS - 4 else g_bank[k][:].rearrange("p c n -> p (c n)")
-            nc.vector.scalar_tensor_tensor(
-                out=part(dz_t[t][:, 2 * pair : 2 * pair + 2, :], k),
-                in0=part(s_t[pair_of(k)], k),
-                scalar=0.25,
-                in1=grad,
-                op0=ALU.subtract,
-                op1=ALU.mult,
-            )
-
-        def tok_tile(t, g, half, tag):
-            tok_t[t, g, half] = ring.tile([P, 2, P, 4], BF16, name=tag, align_bytes=64)
-            return tok_t[t, g, half]
-
-        def tok_source(t, g, half):
-            by_r = dz_t[t][:, :, 512 * g : 512 * (g + 1)].rearrange("p j (m r) -> p r m j", r=4)
-            return by_r[:, 2 * half : 2 * half + 2, :, :]
-
-        def interleave_gpsimd(t, g, half):
-            nc.gpsimd.tensor_scalar(
-                out=tok_tile(t, g, half, "tok_g")[:, :, :GPSIMD_SHARE, :],
-                in0=tok_source(t, g, half)[:, :, :GPSIMD_SHARE, :],
-                scalar1=1.0,
-                scalar2=-0.0,
-                op0=ALU.mult,
-                op1=ALU.add,
-            )
-
-        def interleave_scalar(t, g, half, m0=0):
-            tile = tok_t[t, g, half] if m0 else tok_tile(t, g, half, "tok_s")
-            nc.scalar.copy(
-                out=tile[:, :, m0:, :].rearrange("p r m j -> p m j r"),
-                in_=tok_source(t, g, half)[:, :, m0:, :].rearrange("p r m j -> p m j r"),
-            )
-
-        def quantize_tok(t, g, half):
-            cols = slice(256 * half, 256 * (half + 1))
-            nc.vector.quantize_mx(
-                out=tok_code[:, t, g, cols].bitcast(E5M2),
-                scales=tok_scale[:, t, g, cols],
-                in_=tok_t[t, g, half][:].rearrange("p r m j -> p (r m j)"),
-            )
-
-        g_bank = {}
+        dz_t, g_bank, tr_bank, p_t, d2_t = {}, {}, {}, {}, {}
 
         def stage_g(k):
             g_bank[k] = ps_work.tile([P, 2, 512], BF16, name="g_bank")
@@ -162,27 +115,73 @@ def tile_dedicomdecoder_v_kernel(tc, z_i, z_j, w_r, d_w, rz_in, scores, grad_out
                     stop=True,
                 )
 
+        def make_dz(k):
+            t, pair = divmod(pair_of(k), 2)
+            if k % 4 == 0:
+                dz_t[t] = ring.tile([P, 4, R], BF16, name="dz", bufs=3)
+            grad = part(g_t[pair_of(k)], k)
+            if k in g_bank:
+                grad = g_bank[k][:] if k >= STEPS - 4 else g_bank[k][:].rearrange("p c n -> p (c n)")
+            nc.vector.scalar_tensor_tensor(
+                out=part(dz_t[t][:, 2 * pair : 2 * pair + 2, :], k),
+                in0=part(s_t[pair_of(k)], k),
+                scalar=0.25,
+                in1=grad,
+                op0=ALU.subtract,
+                op1=ALU.mult,
+            )
+
+        batch_t, tok_at, rel_at, filled = {}, {}, {}, {}
+
+        def slot(batch, index):
+            if batch not in batch_t:
+                tag = "step_batch" if batch < STEPS + 1 else "late_batch"
+                batch_t[batch] = ring.tile([P, 2, 1024], BF16, name=tag, align_bytes=64)
+                filled[batch] = set()
+            filled[batch].add(index)
+            return batch_t[batch][:, index, :]
+
+        def tok_views(unit, batch, index, m0, m1):
+            t, g, half = unit
+            for r in range(2):
+                tok_at[t, g, 2 * half + r] = (batch, 256 * index + P * r)
+            dst = slot(batch, index).rearrange("p (r m j) -> p r m j", r=2, j=4)
+            src = dz_t[t][:, :, 512 * g : 512 * (g + 1)].rearrange("p j (m r) -> p r m j", r=4)
+            return dst[:, :, m0:m1, :], src[:, 2 * half : 2 * half + 2, m0:m1, :]
+
+        def interleave_gpsimd(unit, batch):
+            dst, src = tok_views(unit, batch, 0, 0, GPSIMD_SHARE)
+            nc.gpsimd.tensor_scalar(out=dst, in0=src, scalar1=1.0, scalar2=-0.0, op0=ALU.mult, op1=ALU.add)
+
+        def interleave(copy, unit, batch, index, m0=0):
+            dst, src = tok_views(unit, batch, index, m0, P)
+            copy(out=dst.rearrange("p r m j -> p m j r"), in_=src.rearrange("p r m j -> p m j r"))
+
         def transpose(k):
-            bank_t[k] = ps_work.tile([P, 2, 2, P], F32, name="tr_bank", bufs=2)
+            tr_bank[k] = ps_work.tile([P, 2, 2, P], F32, name="tr_bank", bufs=2)
             for c, (row, g) in enumerate(cells(k)):
                 words = dz_t[row // 4][:, row % 4, :].bitcast(F32)
                 for h in range(2):
-                    nc.tensor.transpose(bank_t[k][:, c, h, :], words[:, 256 * g + h : 256 * (g + 1) : 2], ident[:])
+                    nc.tensor.transpose(tr_bank[k][:, c, h, :], words[:, 256 * g + h : 256 * (g + 1) : 2], ident[:])
 
-        def copy_words(k):
-            rel_t[k] = ring.tile([P, NG, P, 2], F32, name="rel", align_bytes=64, bufs=3)
-            copy = nc.vector.tensor_copy if k < VECTOR_COPIES else nc.scalar.copy
-            copy(out=rel_t[k][:], in_=bank_t[k][:].rearrange("m g h p -> m g p h"))
-
-        def quantize_rel(k):
-            rel_code[k] = ring.tile([P, 2 * P], U32, name="rel_code", align_bytes=64, bufs=6)
-            rel_scale[k] = ring.tile([P, 2 * P], U8, name="rel_scale", align_bytes=64, bufs=6)
+        def copy_words(k, batch, index=1):
             for c, cell in enumerate(cells(k)):
-                rel_at[cell] = (k, slice(P * c, P * (c + 1)))
+                rel_at[cell] = (batch, 256 * index + P * c)
+            nc.scalar.copy(
+                out=slot(batch, index).bitcast(F32).rearrange("m (c p h) -> m c p h", c=2, h=2),
+                in_=tr_bank[k][:].rearrange("m c h p -> m c p h"),
+            )
+
+        dz_code, dz_scale = {}, {}
+
+        def quantize_dz(batch):
+            first, end = min(filled[batch]), max(filled[batch]) + 1
+            dz_code[batch] = keep.tile([P, 512], U32, name="dz_code%d" % batch, align_bytes=64)
+            dz_scale[batch] = keep.tile([P, 512], U8, name="dz_scale%d" % batch, align_bytes=64)
             nc.vector.quantize_mx(
-                out=rel_code[k][:].bitcast(E5M2),
-                scales=rel_scale[k][:],
-                in_=rel_t[k][:].rearrange("m g p h -> m (g p h)").bitcast(BF16),
+                out=dz_code[batch][:, 256 * first : 256 * end].bitcast(E5M2),
+                scales=dz_scale[batch][:, 256 * first : 256 * end],
+                in_=batch_t[batch][:, first:end, :].rearrange("p i n -> p (i n)"),
             )
 
         def by_four(ap):
@@ -218,52 +217,59 @@ def tile_dedicomdecoder_v_kernel(tc, z_i, z_j, w_r, d_w, rz_in, scores, grad_out
                 out=d2_code[:, g, :].bitcast(E4M3), scales=d2_scale[:, g, :], in_=d2_t[g][:].rearrange("p h j -> p (h j)")
             )
 
+        def stationary(place):
+            batch, col = place
+            return dz_code[batch][:, col : col + P].bitcast(E5M2), dz_scale[batch][:, col : col + P]
+
         o0_bank, o0_t, acc, o1_t = {}, {}, {}, {}
 
-        def matmul_0(k, tag="o0_bank"):
-            o0_bank[k] = ps_work.tile([P, H], F32, name=tag)
+        def matmul_0(row, tag="o0_bank"):
+            o0_bank[row] = ps_work.tile([P, H], F32, name=tag)
             for g in range(NG):
-                step, cols = rel_at[k, g]
+                code, scale = stationary(rel_at[row, g])
                 nc.tensor.matmul_mx(
-                    out=o0_bank[k][:],
-                    lhsT=rel_code[step][:, cols].bitcast(E5M2),
-                    lhsT_scale=rel_scale[step][:, cols],
+                    out=o0_bank[row][:],
+                    lhsT=code,
+                    lhsT_scale=scale,
                     rhs=d2_code[:, g, :].bitcast(E4M3),
                     rhs_scale=d2_scale[:, g, :],
                     start=(g == 0),
                     stop=(g == NG - 1),
                 )
 
-        def finish_0(k):
-            t, j = divmod(k, 4)
+        def finish_0(row):
+            t, j = divmod(row, 4)
             if j % 2 == 0:
-                o0_t[k // 2] = ring.tile([P, 2, H], F32, name="out_rows", bufs=8)
+                o0_t[row // 2] = ring.tile([P, 2, H], F32, name="out_rows", bufs=8)
             nc.vector.scalar_tensor_tensor(
-                out=o0_t[k // 2][:, j % 2, :],
-                in0=o0_bank[k][:],
+                out=o0_t[row // 2][:, j % 2, :],
+                in0=o0_bank[row][:],
                 scalar=-1.0,
                 in1=rz_t[t][:, j, :],
                 op0=ALU.mult,
                 op1=ALU.mult,
             )
 
-        def store_0(k0, k1):
-            t, j = divmod(k0, 4)
+        def store_0(row, count):
+            t, j = divmod(row, 4)
             nc.sync.dma_start(
-                out=token_rows(out_0, t)[:, j : j + k1 - k0, :], in_=o0_t[k0 // 2][:, k0 % 2 : k0 % 2 + k1 - k0, :]
+                out=four_rows(out_0, t)[:, j : j + count, :], in_=o0_t[row // 2][:, row % 2 : row % 2 + count, :]
             )
 
         def matmul_1(t, g, r):
-            if t == 0:
+            if t == 0 and g == 1 and r >= 2:
+                acc[g, r] = ps_work.tile([P, H], F32, name="tr_bank", bufs=2)
+            elif t == 0:
                 acc[g, r] = ps_acc.tile([P, H], F32, name="acc%d" % r)
+            code, scale = stationary(tok_at[t, g, r])
             nc.tensor.matmul_mx(
                 out=acc[g, r][:],
-                lhsT=tok_code[:, t, g, P * r : P * (r + 1)].bitcast(E5M2),
-                lhsT_scale=tok_scale[:, t, g, P * r : P * (r + 1)],
+                lhsT=code,
+                lhsT_scale=scale,
                 rhs=p_code[:, t, :].bitcast(E4M3),
                 rhs_scale=p_scale[:, t, :],
                 start=(t == 0),
-                stop=(t == NT - 1),
+                stop=(t == LAST),
             )
 
         def finish_1(g, r):
@@ -278,134 +284,123 @@ def tile_dedicomdecoder_v_kernel(tc, z_i, z_j, w_r, d_w, rz_in, scores, grad_out
                 op1=ALU.mult,
             )
 
-        def store_1(g, r0, r1):
+        def store_1(g, r, count):
             nc.sync.dma_start(
-                out=token_rows(out_1, g)[:, r0:r1, :], in_=o1_t[g, r0 // 2][:, r0 % 2 : r0 % 2 + r1 - r0, :]
+                out=four_rows(out_1, g)[:, r : r + count, :], in_=o1_t[g, r // 2][:, r % 2 : r % 2 + count, :]
             )
 
-
-        def load_step(k):
-            row = cells(k)[0][0]
-            if row // 2 not in s_t:
-                s_t[row // 2] = ring.tile([P, 2, R], F32, name="s_rows", bufs=4)
-            pair = token_rows(scores, row // 4)[:, row % 4 // 2 * 2 : row % 4 // 2 * 2 + 2, :]
-            if PAIRS_FROM <= k < ROWS - 4:
-                nc.sync.dma_start(out=s_t[row // 2][:], in_=pair)
-            else:
-                nc.sync.dma_start(out=part(s_t[row // 2], k), in_=part(pair, k))
-
-        last = NT - 1
-        halves = [(t, g, half) for t in range(NT) for g in range(NG) for half in range(2)]
-
-        loads = [(k - S_LEAD, load_step, (k,)) for k in range(ROWS) if k % 2 == 0 or not PAIRS_FROM <= k < ROWS - 4]
-        loads += [(2 * g - 1, load_d, (g,)) for g in range(NG)]
-        loads += [(k - G_LEAD, load_g, (cells(k)[0][0],)) for k in range(ROWS) if cells(k)[0][0] % 2 == 0 and cells(k)[0][1] == 0]
+        loads = [(k - S_LEAD, load_s, k) for k in range(STEPS) if k % 2 == 0 or not PAIRS_FROM <= k < STEPS - 4]
+        loads += [(2 * g - 1, load_d, g) for g in range(NG)]
+        loads += [(min(k for k in range(STEPS) if pair_of(k) == pair) - G_LEAD, load_g, pair) for pair in range(2 * NT)]
         for t in range(NT):
-            loads += [(P_STEPS[t], load_rz, (t,)), (P_STEPS[t], load_z, (t,))]
+            loads += [(P_NEED[t], load_rz, t), (P_NEED[t], load_z, t)]
         loads = sorted(loads, key=lambda entry: entry[0])
 
-        def issue_loads(k):
-            for need, load, args in loads:
-                if k - 1 + AHEAD < need <= k + AHEAD or (k == 0 and need <= AHEAD):
-                    load(*args)
+        def issue_loads(after, until):
+            for need, load, arg in loads:
+                if after < need <= until:
+                    load(arg)
 
-        issue_loads(0)
+        def gpsimd_unit(k):
+            if k == STEPS - 2:
+                return (LAST, 0, 0)
+            if k == STEPS - 1:
+                return (LAST - 1, 1, 0)
+            return (k // 4 - 1, k % 4 // 2, k % 2) if k >= 4 else None
+
+        late_a, late_b, late_c, late_d = STEPS + 1, STEPS + 2, STEPS + 3, STEPS + 4
+
+        issue_loads(-2, AHEAD)
         make_d2(0)
         for k in range(2):
-            for func in (tanh, square):
-                func(k, slice(0, 512))
-                func(k, slice(512, R))
+            for func in (ACT.Tanh, ACT.Square):
+                activate(func, k, slice(0, 512))
+                activate(func, k, slice(512, R))
         quantize_d2(0)
-        for k in range(ROWS):
-            t, j = divmod(k, 4)
-            if k > 0:
-                issue_loads(k)
-            if k >= ROWS - 4:
-                store_0(2 * (k - ROWS + 4), 2 * (k - ROWS + 4) + 2)
+        for k in range(STEPS):
+            issue_loads(k + AHEAD, k + 1 + AHEAD)
+            if k >= STEPS - 4:
+                store_0(2 * (k - STEPS + 4), 2)
+            unit = gpsimd_unit(k)
             make_dz(k)
-            if k >= 4:
-                interleave_gpsimd(*halves[k - 4])
-            if STAGE_FROM - 1 <= k < ROWS - 1:
+            if unit:
+                interleave_gpsimd(unit, k + 1)
+            if STAGE_FROM <= k + 1 < STEPS:
                 stage_g(k + 1)
-            transpose(k)
-            if k + 2 < ROWS:
-                tanh(k + 2)
-            if k > VECTOR_COPIES:
-                copy_words(k - 1)
-            if k + 2 < ROWS:
-                square(k + 2)
-            if k >= 4:
-                interleave_scalar(*halves[k - 4], GPSIMD_SHARE)
-            if k == ROWS - 2:
-                interleave_scalar(last, 0, 0)
-                interleave_scalar(last, 0, 1)
-            if 1 <= k <= VECTOR_COPIES:
-                copy_words(k - 1)
+            if k == STEPS - 2:
+                interleave(nc.scalar.copy, (LAST, 0, 1), late_a, 0)
+            if k + 2 < STEPS:
+                activate(ACT.Tanh, k + 2)
+            if k >= 1:
+                copy_words(k - 1, k + 1)
+            if unit and k >= SCALAR_FROM:
+                interleave(nc.scalar.copy, unit, k + 1, 0, GPSIMD_SHARE)
+            if k + 2 < STEPS:
+                activate(ACT.Square, k + 2)
+            if k == STEPS - 1:
+                interleave(nc.scalar.copy, (LAST - 1, 1, 1), late_b, 0)
             if k >= 5:
                 finish_0(k - 5)
+            if k == STEPS - 1:
+                transpose(k)
             if k >= 4:
                 matmul_0(k - 4)
+            if k < STEPS - 1:
+                transpose(k)
+            jobs = []
             if k == 1:
-                make_d2(1)
-            if k == 2:
-                quantize_d2(1)
-            for tp, first in enumerate(P_STEPS):
-                if k == first + 2:
-                    quantize_p(tp)
-            for tp, first in enumerate(P_STEPS):
-                if first <= k < first + 2:
-                    make_p(tp, k - first)
-            if k >= 5:
-                quantize_tok(*halves[k - 5])
-            if k >= 3:
-                quantize_rel(k - 3)
-            if 0 < t < last and j == 3:
+                jobs.append((make_d2, 1))
+            if k == 3:
+                jobs.append((quantize_d2, 1))
+            if k == STEPS - 1:
+                jobs.append((quantize_dz, late_a))
+            if unit and k < SCALAR_FROM:
+                jobs.append((interleave, nc.vector.tensor_copy, unit, k + 1, 0, GPSIMD_SHARE))
+            jobs += [(quantize_p, t) for t, first in enumerate(P_STEPS) if k == first + 2]
+            jobs += [(make_p, t, k - first) for t, first in enumerate(P_STEPS) if first <= k < first + 2]
+            if k >= 2:
+                jobs.insert(max(len(jobs) - 1, 0), (quantize_dz, k))
+            for job, *args in jobs:
+                job(*args)
+            if k in (7, 11, 14, 15):
                 for r in range(4):
-                    matmul_1(t - 1, 0, r)
-            if k == ROWS - 2:
-                for r in range(4):
-                    matmul_1(last - 1, 0, r)
-            if k == ROWS - 1:
-                quantize_tok(last, 0, 0)
-                quantize_tok(last, 0, 1)
-                for r in range(4):
-                    matmul_1(last, 0, r)
+                    matmul_1((7, 11, 14, 15).index(k), 0, r)
 
-        copy_words(ROWS - 1)
-        interleave_scalar(last, 1, 0)
-        interleave_scalar(last, 1, 1)
-        store_0(ROWS - 8, ROWS - 6)
-        quantize_tok(last - 1, 1, 1)
-        quantize_rel(ROWS - 3)
-        quantize_rel(ROWS - 2)
-        matmul_0(ROWS - 4, "g_bank")
-        finish_0(ROWS - 5)
-        matmul_0(ROWS - 3)
-        store_0(ROWS - 6, ROWS - 4)
-        for r in range(2):
-            finish_1(0, r)
-            for tt in range(last):
-                matmul_1(tt, 1, r)
+        copy_words(STEPS - 1, late_b)
+        interleave(nc.scalar.copy, (LAST, 1, 0), late_c, 0)
+        interleave(nc.scalar.copy, (LAST, 1, 1), late_c, 1)
+        store_0(STEPS - 8, 2)
+        quantize_dz(STEPS)
+        finish_0(STEPS - 5)
+        store_0(STEPS - 6, 2)
+        matmul_0(STEPS - 4, "g_bank")
+        matmul_0(STEPS - 3)
+        for r in (2, 3):
+            for t in range(LAST - 1):
+                matmul_1(t, 1, r)
+        finish_1(0, 0)
+        finish_1(0, 1)
         store_1(0, 0, 2)
-        quantize_rel(ROWS - 1)
+        quantize_dz(late_b)
         for r in range(2):
-            finish_0(ROWS - 4 + r)
-            matmul_0(ROWS - 2 + r, ("g_bank", "o0_bank")[r])
-        store_0(ROWS - 4, ROWS - 2)
+            finish_0(STEPS - 4 + r)
+            matmul_0(STEPS - 2 + r, ("g_bank", "o0_bank")[r])
+        store_0(STEPS - 4, 2)
+        for r in (2, 3):
+            matmul_1(LAST - 1, 1, r)
+        for t in range(LAST):
+            matmul_1(t, 1, 0)
         finish_1(0, 2)
-        for tt in range(last):
-            matmul_1(tt, 1, 2)
         finish_1(0, 3)
-        store_1(0, 2, 4)
-        quantize_tok(last, 1, 0)
-        quantize_tok(last, 1, 1)
-        for r in range(3):
-            matmul_1(last, 1, r)
-        for tt in range(NT):
-            matmul_1(tt, 1, 3)
+        store_1(0, 2, 2)
+        quantize_dz(late_c)
+        for r in (2, 3, 0):
+            matmul_1(LAST, 1, r)
+        for t in range(NT):
+            matmul_1(t, 1, 1)
         for r in range(2):
-            finish_0(ROWS - 2 + r)
-            store_0(ROWS - 2 + r, ROWS - 1 + r)
-        for r in range(4):
+            finish_0(STEPS - 2 + r)
+        store_0(STEPS - 2, 2)
+        for r in (2, 3, 0, 1):
             finish_1(1, r)
-            store_1(1, r, r + 1)
+            store_1(1, r, 1)

@@ -184,17 +184,17 @@ def tile_dedicomdecoder_v_kernel(tc, z_i, z_j, w_r, d_w, rz_in, scores, grad_out
                 in_=batch_t[batch][:, first:end, :].rearrange("p i n -> p (i n)"),
             )
 
-        def by_four(ap):
-            return ap.rearrange("p j (c i) -> p c j i", i=4)
+        def by_two(ap):
+            return ap.rearrange("p j (c i) -> p c j i", i=2)
 
         def make_p(t, half):
             if half == 0:
                 p_t[t] = ring.tile([P, H, 4], BF16, name="staged", align_bytes=64)
             cols = slice(256 * half, 256 * (half + 1))
             nc.vector.tensor_tensor(
-                out=by_four(p_t[t][:, cols, :].rearrange("p c j -> p j c")),
-                in0=by_four(z_t[t][:, :, cols]),
-                in1=by_four(rz_t[t][:, :, cols]),
+                out=by_two(p_t[t][:, cols, :].rearrange("p c j -> p j c")),
+                in0=by_two(z_t[t][:, :, cols]),
+                in1=by_two(rz_t[t][:, :, cols]),
                 op=ALU.mult,
             )
 
@@ -206,9 +206,9 @@ def tile_dedicomdecoder_v_kernel(tc, z_i, z_j, w_r, d_w, rz_in, scores, grad_out
         def make_d2(g):
             d2_t[g] = ring.tile([P, H, 4], BF16, name="staged", align_bytes=64)
             nc.vector.tensor_tensor(
-                out=by_four(d2_t[g][:].rearrange("p c j -> p j c")),
-                in0=by_four(d_t[g][:]),
-                in1=by_four(d_t[g][:]),
+                out=by_two(d2_t[g][:].rearrange("p c j -> p j c")),
+                in0=by_two(d_t[g][:]),
+                in1=by_two(d_t[g][:]),
                 op=ALU.mult,
             )
 

@@ -272,22 +272,20 @@ def tile_dedicomdecoder_v_kernel(tc, z_i, z_j, w_r, d_w, rz_in, scores, grad_out
                 stop=(t == LAST),
             )
 
-        def finish_1(g, r):
+        def finish_1(g, r, cols=slice(0, H)):
             if r % 2 == 0:
                 o1_t[g, r // 2] = ring.tile([P, 2, H], F32, name="out_rows", bufs=8)
             nc.vector.scalar_tensor_tensor(
-                out=o1_t[g, r // 2][:, r % 2, :],
-                in0=acc[g, r][:],
+                out=o1_t[g, r // 2][:, r % 2, cols],
+                in0=acc[g, r][:, cols],
                 scalar=-2.0,
-                in1=d_t[g][:, r, :],
+                in1=d_t[g][:, r, cols],
                 op0=ALU.mult,
                 op1=ALU.mult,
             )
 
-        def store_1(g, r, count):
-            nc.sync.dma_start(
-                out=four_rows(out_1, g)[:, r : r + count, :], in_=o1_t[g, r // 2][:, r % 2 : r % 2 + count, :]
-            )
+        def store_1(g, r, cols=slice(0, H)):
+            nc.sync.dma_start(out=four_rows(out_1, g)[:, r, cols], in_=o1_t[g, r // 2][:, r % 2, cols])
 
         loads = [(k - S_LEAD, load_s, k) for k in range(STEPS) if k % 2 == 0 or not PAIRS_FROM <= k < STEPS - 4]
         loads += [(2 * g - 1, load_d, g) for g in range(NG)]
@@ -370,29 +368,30 @@ def tile_dedicomdecoder_v_kernel(tc, z_i, z_j, w_r, d_w, rz_in, scores, grad_out
         interleave(nc.scalar.copy, (LAST, 1, 0), late_c, 0)
         interleave(nc.scalar.copy, (LAST, 1, 1), late_c, 1)
         store_0(STEPS - 8, 2)
+        store_0(STEPS - 6, 1)
         quantize_dz(STEPS)
         finish_0(STEPS - 5)
-        store_0(STEPS - 6, 2)
+        store_0(STEPS - 5, 1)
         matmul_0(STEPS - 4, "g_bank")
         matmul_0(STEPS - 3)
         for r in (2, 3):
             for t in range(LAST - 1):
                 matmul_1(t, 1, r)
-        finish_1(0, 0)
-        finish_1(0, 1)
-        store_1(0, 0, 2)
+        for r in range(2):
+            finish_1(0, r)
+            store_1(0, r)
         quantize_dz(late_b)
         for r in range(2):
             finish_0(STEPS - 4 + r)
+            store_0(STEPS - 4 + r, 1)
             matmul_0(STEPS - 2 + r, ("g_bank", "o0_bank")[r])
-        store_0(STEPS - 4, 2)
         for r in (2, 3):
             matmul_1(LAST - 1, 1, r)
         for t in range(LAST):
             matmul_1(t, 1, 0)
-        finish_1(0, 2)
-        finish_1(0, 3)
-        store_1(0, 2, 2)
+        for r in (2, 3):
+            finish_1(0, r)
+            store_1(0, r)
         quantize_dz(late_c)
         for r in (2, 3, 0):
             matmul_1(LAST, 1, r)
@@ -400,7 +399,10 @@ def tile_dedicomdecoder_v_kernel(tc, z_i, z_j, w_r, d_w, rz_in, scores, grad_out
             matmul_1(t, 1, 1)
         for r in range(2):
             finish_0(STEPS - 2 + r)
-        store_0(STEPS - 2, 2)
-        for r in (2, 3, 0, 1):
+            store_0(STEPS - 2 + r, 1)
+        for r in (2, 3, 0):
             finish_1(1, r)
-            store_1(1, r, 1)
+            store_1(1, r)
+        for cols in (slice(0, 256), slice(256, H)):
+            finish_1(1, 1, cols)
+            store_1(1, 1, cols)

@@ -151,7 +151,7 @@ def tile_dedicomdecoder_v_kernel(tc, z_i, z_j, w_r, d_w, rz_in, scores, grad_out
 
         def interleave_gpsimd(unit, batch):
             dst, src = tok_views(unit, batch, 0, 0, GPSIMD_SHARE)
-            nc.gpsimd.tensor_scalar(out=dst, in0=src, scalar1=1.0, scalar2=-0.0, op0=ALU.mult, op1=ALU.add)
+            nc.gpsimd.tensor_copy(out=dst, in_=src)
 
         def interleave(copy, unit, batch, index, m0=0):
             dst, src = tok_views(unit, batch, index, m0, P)

@@ -20,17 +20,9 @@ ALU = mybir.AluOpType
 P = 128
 NT = B // 512
 NG = R // 512
-STEPS = 4 * NT
 LAST = NT - 1
-AHEAD = 3
-S_LEAD = 1.5
-G_LEAD = 0.5
-PAIRS_FROM = 8
-STAGE_FROM = 4
-SCALAR_FROM = 6
-GPSIMD_SHARE = 80
-P_STEPS = (4, 7, 10, 12)
-P_NEED = (3.6, 7, 10, 12)
+UNITS = [(t, g) for t in range(1, NT) for g in range(NG)]
+GPSIMD_COLS = 240
 
 
 def tile_dedicomdecoder_v_kernel(tc, z_i, z_j, w_r, d_w, rz_in, scores, grad_out, out_0, out_1):
@@ -38,53 +30,40 @@ def tile_dedicomdecoder_v_kernel(tc, z_i, z_j, w_r, d_w, rz_in, scores, grad_out
     with ExitStack() as ctx:
         keep = ctx.enter_context(tc.tile_pool(name="keep", bufs=1))
         ring = ctx.enter_context(tc.tile_pool(name="ring", bufs=2))
-        ps_work = ctx.enter_context(tc.psum_pool(name="ps_work", bufs=1))
-        ps_acc = ctx.enter_context(tc.psum_pool(name="ps_acc", bufs=1))
+        psum = ctx.enter_context(tc.psum_pool(name="psum", bufs=1))
         ctx.enter_context(tc.manual_schedule())
 
         def four_rows(hbm, t):
             return hbm[512 * t : 512 * (t + 1), :].rearrange("(p j) n -> p j n", j=4)
 
-        def cells(k):
-            if k < STEPS - 4:
-                return [(k, 0), (k, 1)]
-            g, pair = divmod(k - (STEPS - 4), 2)
-            return [(STEPS - 4 + 2 * pair, g), (STEPS - 4 + 2 * pair + 1, g)]
-
-        def pair_of(k):
-            return cells(k)[0][0] // 2
-
-        def part(pair_tile, k):
-            (row, g), (row2, g2) = cells(k)
-            if row == row2:
-                return pair_tile[:, row % 2, :]
-            return pair_tile[:, :, 512 * g : 512 * (g + 1)]
-
         s_t, g_t, z_t, rz_t, d_t = {}, {}, {}, {}, {}
 
-        def load_s(k):
-            pair = pair_of(k)
-            if pair not in s_t:
-                s_t[pair] = ring.tile([P, 2, R], F32, name="s_rows", bufs=4)
-            src = four_rows(scores, pair // 2)[:, pair % 2 * 2 : pair % 2 * 2 + 2, :]
-            if PAIRS_FROM <= k < STEPS - 4:
-                nc.sync.dma_start(out=s_t[pair][:], in_=src)
-            else:
-                nc.sync.dma_start(out=part(s_t[pair], k), in_=part(src, k))
+        def load_s_row(j):
+            if j % 2 == 0:
+                s_t[0, j // 2] = ring.tile([P, 2, R], F32, name="s_in", bufs=4)
+            nc.sync.dma_start(out=s_t[0, j // 2][:, j % 2, :], in_=four_rows(scores, 0)[:, j, :])
 
-        def load_g(pair):
-            g_t[pair] = ring.tile([P, 2, R], BF16, name="g_rows", bufs=5)
-            nc.sync.dma_start(out=g_t[pair][:], in_=four_rows(grad_out, pair // 2)[:, pair % 2 * 2 : pair % 2 * 2 + 2, :])
+        def load_g_rows(u):
+            g_t[0, u] = ring.tile([P, 2, R], BF16, name="g_in", bufs=4)
+            nc.sync.dma_start(out=g_t[0, u][:], in_=four_rows(grad_out, 0)[:, 2 * u : 2 * u + 2, :])
+
+        def load_s(unit):
+            t, g = unit
+            s_t[unit] = ring.tile([P, 4, 512], F32, name="s_in", bufs=4)
+            nc.sync.dma_start(out=s_t[unit][:], in_=four_rows(scores, t)[:, :, 512 * g : 512 * (g + 1)])
+
+        def load_g(unit):
+            t, g = unit
+            g_t[unit] = ring.tile([P, 4, 512], BF16, name="g_in", bufs=4)
+            nc.sync.dma_start(out=g_t[unit][:], in_=four_rows(grad_out, t)[:, :, 512 * g : 512 * (g + 1)])
 
         def load_d(g):
             d_t[g] = keep.tile([P, 4, H], BF16, name="d_rows%d" % g)
             nc.sync.dma_start(out=d_t[g][:], in_=four_rows(d_w, g))
 
-        def load_z(t):
+        def load_z_rz(t):
             z_t[t] = ring.tile([P, 4, H], BF16, name="z_rows")
             nc.sync.dma_start(out=z_t[t][:], in_=four_rows(z_i, t))
-
-        def load_rz(t):
             rz_t[t] = ring.tile([P, 4, H], F32, name="rz_rows", bufs=3)
             nc.sync.dma_start(out=rz_t[t][:], in_=four_rows(rz_in, t))
 
@@ -93,316 +72,367 @@ def tile_dedicomdecoder_v_kernel(tc, z_i, z_j, w_r, d_w, rz_in, scores, grad_out
         ident_bf = keep.tile([P, P], BF16, name="ident_bf")
         make_identity(nc, ident_bf[:])
 
-        d2_code = keep.tile([P, NG, H], U32, name="d2_code", align_bytes=64)
-        d2_scale = keep.tile([P, NG, H], U8, name="d2_scale", align_bytes=64)
-        p_code = keep.tile([P, NT, H], U32, name="p_code", align_bytes=64)
-        p_scale = keep.tile([P, NT, H], U8, name="p_scale", align_bytes=64)
+        codes, scales = {}, {}
 
-        def activate(func, k, cols=slice(None)):
-            s = part(s_t[pair_of(k)], k)[:, cols]
-            nc.scalar.activation(out=s, in_=s, func=func, scale=0.5)
-
-        dz_t, g_bank, tr_bank, p_t, d2_t = {}, {}, {}, {}, {}
-
-        def stage_g(k):
-            g_bank[k] = ps_work.tile([P, 2, 512], BF16, name="g_bank")
-            for c, (row, g) in enumerate(cells(k)):
-                nc.tensor.matmul(
-                    out=g_bank[k][:, c, :],
-                    lhsT=ident_bf[:],
-                    rhs=g_t[row // 2][:, row % 2, 512 * g : 512 * (g + 1)],
-                    start=True,
-                    stop=True,
-                )
-
-        def make_dz(k):
-            t, pair = divmod(pair_of(k), 2)
-            if k % 4 == 0:
-                dz_t[t] = ring.tile([P, 4, R], BF16, name="dz", bufs=3)
-            grad = part(g_t[pair_of(k)], k)
-            if k in g_bank:
-                grad = g_bank[k][:] if k >= STEPS - 4 else g_bank[k][:].rearrange("p c n -> p (c n)")
-            nc.vector.scalar_tensor_tensor(
-                out=part(dz_t[t][:, 2 * pair : 2 * pair + 2, :], k),
-                in0=part(s_t[pair_of(k)], k),
-                scalar=0.25,
-                in1=grad,
-                op0=ALU.subtract,
-                op1=ALU.mult,
-            )
-
-        batch_t, tok_at, rel_at, filled = {}, {}, {}, {}
-
-        def slot(batch, index):
-            if batch not in batch_t:
-                tag = "step_batch" if batch < STEPS + 1 else "late_batch"
-                batch_t[batch] = ring.tile([P, 2, 1024], BF16, name=tag, align_bytes=64)
-                filled[batch] = set()
-            filled[batch].add(index)
-            return batch_t[batch][:, index, :]
-
-        def tok_views(unit, batch, index, m0, m1):
-            t, g, half = unit
-            for r in range(2):
-                tok_at[t, g, 2 * half + r] = (batch, 256 * index + P * r)
-            dst = slot(batch, index).rearrange("p (r m j) -> p r m j", r=2, j=4)
-            src = dz_t[t][:, :, 512 * g : 512 * (g + 1)].rearrange("p j (m r) -> p r m j", r=4)
-            return dst[:, :, m0:m1, :], src[:, 2 * half : 2 * half + 2, m0:m1, :]
-
-        def interleave_gpsimd(unit, batch):
-            dst, src = tok_views(unit, batch, 0, 0, GPSIMD_SHARE)
-            nc.gpsimd.tensor_copy(out=dst, in_=src)
-
-        def interleave(copy, unit, batch, index, m0=0):
-            dst, src = tok_views(unit, batch, index, m0, P)
-            copy(out=dst.rearrange("p r m j -> p m j r"), in_=src.rearrange("p r m j -> p m j r"))
-
-        def transpose(k):
-            tr_bank[k] = ps_work.tile([P, 2, 2, P], F32, name="tr_bank", bufs=2)
-            for c, (row, g) in enumerate(cells(k)):
-                words = dz_t[row // 4][:, row % 4, :].bitcast(F32)
-                for h in range(2):
-                    nc.tensor.transpose(tr_bank[k][:, c, h, :], words[:, 256 * g + h : 256 * (g + 1) : 2], ident[:])
-
-        def copy_words(k, batch, index=1):
-            for c, cell in enumerate(cells(k)):
-                rel_at[cell] = (batch, 256 * index + P * c)
-            nc.scalar.copy(
-                out=slot(batch, index).bitcast(F32).rearrange("m (c p h) -> m c p h", c=2, h=2),
-                in_=tr_bank[k][:].rearrange("m c h p -> m c p h"),
-            )
-
-        dz_code, dz_scale = {}, {}
-
-        def quantize_dz(batch):
-            first, end = min(filled[batch]), max(filled[batch]) + 1
-            dz_code[batch] = keep.tile([P, 512], U32, name="dz_code%d" % batch, align_bytes=64)
-            dz_scale[batch] = keep.tile([P, 512], U8, name="dz_scale%d" % batch, align_bytes=64)
-            nc.vector.quantize_mx(
-                out=dz_code[batch][:, 256 * first : 256 * end].bitcast(E5M2),
-                scales=dz_scale[batch][:, 256 * first : 256 * end],
-                in_=batch_t[batch][:, first:end, :].rearrange("p i n -> p (i n)"),
-            )
+        def quantize(key, staged, fmt):
+            codes[key] = keep.tile([P, 512], U32, name="code_%s%d%d" % key, align_bytes=64)
+            scales[key] = keep.tile([P, 512], U8, name="scale_%s%d%d" % key, align_bytes=64)
+            nc.vector.quantize_mx(out=codes[key][:].bitcast(fmt), scales=scales[key][:], in_=staged[:])
 
         def by_two(ap):
             return ap.rearrange("p j (c i) -> p c j i", i=2)
 
-        def make_p(t, half):
-            if half == 0:
-                p_t[t] = ring.tile([P, H, 4], BF16, name="staged", align_bytes=64)
-            cols = slice(256 * half, 256 * (half + 1))
-            nc.vector.tensor_tensor(
-                out=by_two(p_t[t][:, cols, :].rearrange("p c j -> p j c")),
-                in0=by_two(z_t[t][:, :, cols]),
-                in1=by_two(rz_t[t][:, :, cols]),
-                op=ALU.mult,
-            )
+        tok_t, rel_t, tr_bank, x_t, g_bank, p_t = {}, {}, {}, {}, {}, {}
 
-        def quantize_p(t):
-            nc.vector.quantize_mx(
-                out=p_code[:, t, :].bitcast(E4M3), scales=p_scale[:, t, :], in_=p_t[t][:].rearrange("p h j -> p (h j)")
-            )
+        def shared_stage():
+            return keep.tile([P, 2048], BF16, name="shared_stage", align_bytes=64)
 
         def make_d2(g):
-            d2_t[g] = ring.tile([P, H, 4], BF16, name="staged", align_bytes=64)
+            tok_t["d", g] = shared_stage()
             nc.vector.tensor_tensor(
-                out=by_two(d2_t[g][:].rearrange("p c j -> p j c")),
+                out=by_two(tok_t["d", g][:].rearrange("p (c j) -> p j c", j=4)),
                 in0=by_two(d_t[g][:]),
                 in1=by_two(d_t[g][:]),
                 op=ALU.mult,
             )
 
         def quantize_d2(g):
-            nc.vector.quantize_mx(
-                out=d2_code[:, g, :].bitcast(E4M3), scales=d2_scale[:, g, :], in_=d2_t[g][:].rearrange("p h j -> p (h j)")
+            quantize(("d", g, 0), tok_t["d", g], E4M3)
+
+        dz_rows = keep.tile([P, 4, R], BF16, name="dz_rows")
+
+        def activate_row(func, j, cols=slice(None)):
+            s = s_t[0, j // 2][:, j % 2, cols]
+            nc.scalar.activation(out=s, in_=s, func=func, scale=0.5)
+
+        def dz_row(j):
+            nc.vector.scalar_tensor_tensor(
+                out=dz_rows[:, j, :],
+                in0=s_t[0, j // 2][:, j % 2, :],
+                scalar=0.25,
+                in1=g_t[0, j // 2][:, j % 2, :],
+                op0=ALU.subtract,
+                op1=ALU.mult,
             )
 
-        def stationary(place):
-            batch, col = place
-            return dz_code[batch][:, col : col + P].bitcast(E5M2), dz_scale[batch][:, col : col + P]
-
-        o0_bank, o0_t, acc, o1_t = {}, {}, {}, {}
-
-        def matmul_0(row, tag="o0_bank"):
-            o0_bank[row] = ps_work.tile([P, H], F32, name=tag)
+        def transpose_row(j):
+            tr_bank[0, j] = psum.tile([P, NG, 2, P], F32, name="tr_bank", bufs=2)
+            words = dz_rows[:, j, :].bitcast(F32)
             for g in range(NG):
-                code, scale = stationary(rel_at[row, g])
-                nc.tensor.matmul_mx(
-                    out=o0_bank[row][:],
-                    lhsT=code,
-                    lhsT_scale=scale,
-                    rhs=d2_code[:, g, :].bitcast(E4M3),
-                    rhs_scale=d2_scale[:, g, :],
-                    start=(g == 0),
-                    stop=(g == NG - 1),
+                for h in range(2):
+                    nc.tensor.transpose(tr_bank[0, j][:, g, h, :], words[:, 256 * g + h : 256 * (g + 1) : 2], ident[:])
+
+        def copy_row(j):
+            if j % 2 == 0:
+                rel_t[0, j // 2] = ring.tile([P, 2048], BF16, name="rel", align_bytes=64)
+            nc.vector.tensor_copy(
+                out=rel_t[0, j // 2][:, 1024 * (j % 2) : 1024 * (j % 2 + 1)]
+                .bitcast(F32)
+                .rearrange("q (g p h) -> q g p h", g=NG, h=2),
+                in_=tr_bank[0, j][:].rearrange("q g h p -> q g p h"),
+            )
+
+        def regroup(g):
+            tok_t[0, g] = shared_stage()
+            nc.gpsimd.tensor_copy(
+                out=tok_t[0, g][:].rearrange("p (t q j) -> p t q j", t=4, j=4),
+                in_=dz_rows[:, :, 512 * g : 512 * (g + 1)].rearrange("p j (q t) -> p t q j", t=4),
+            )
+
+        def tanh(unit, u):
+            if u == 0:
+                x_t[unit] = ring.tile([P, 2, 2, P, 2, 2], F32, name="x_half")
+            nc.scalar.activation(
+                out=x_t[unit][:, u].rearrange("p h q b e -> p q h b e"),
+                in_=s_t[unit][:, 2 * u : 2 * u + 2, :].rearrange("p e (q h b) -> p q h b e", h=2, b=2),
+                func=ACT.Tanh,
+                scale=0.5,
+            )
+
+        def squares(unit):
+            return s_t[unit][:].rearrange("p j n -> p (j n)").rearrange("p (t q j) -> p t q j", t=4, j=4)
+
+        def square(unit, h):
+            nc.scalar.activation(
+                out=squares(unit)[:, 2 * h : 2 * h + 2].rearrange("p b q (u e) -> p q b u e", u=2),
+                in_=x_t[unit][:, :, h].rearrange("p u q b e -> p q b u e"),
+                func=ACT.Square,
+                scale=0.5,
+            )
+
+        def activate(unit):
+            for u in range(2):
+                tanh(unit, u)
+            for h in range(2):
+                square(unit, h)
+
+        def stage_g(unit, h):
+            g_bank[unit, h] = psum.tile([P, 4, P, 2], BF16, name="g_bank")
+            pairs = g_t[unit][:].rearrange("p j (q h b) -> p j h q b", h=2, b=2)
+            for u in range(2):
+                nc.tensor.matmul(
+                    out=g_bank[unit, h][:, 2 * u : 2 * u + 2],
+                    lhsT=ident_bf[:],
+                    rhs=pairs[:, 2 * u : 2 * u + 2, h],
+                    start=True,
+                    stop=True,
                 )
 
-        def finish_0(row):
-            t, j = divmod(row, 4)
-            if j % 2 == 0:
-                o0_t[row // 2] = ring.tile([P, 2, H], F32, name="out_rows", bufs=8)
-            nc.vector.scalar_tensor_tensor(
-                out=o0_t[row // 2][:, j % 2, :],
-                in0=o0_bank[row][:],
-                scalar=-1.0,
-                in1=rz_t[t][:, j, :],
-                op0=ALU.mult,
-                op1=ALU.mult,
+        def make_dz(unit, h):
+            if h == 0:
+                tok_t[unit] = ring.tile([P, 2048], BF16, name="tok", bufs=3, align_bytes=64)
+            for b in range(2):
+                nc.vector.scalar_tensor_tensor(
+                    out=tok_t[unit][:].rearrange("p (t q j) -> p t q j", t=4, j=4)[:, 2 * h + b],
+                    in0=squares(unit)[:, 2 * h + b],
+                    scalar=0.25,
+                    in1=g_bank[unit, h][:, :, :, b].rearrange("p j q -> p q j"),
+                    op0=ALU.subtract,
+                    op1=ALU.mult,
+                )
+
+        def transpose(unit, places=range(4)):
+            words = tok_t[unit][:].bitcast(F32).rearrange("p (t q u) -> p t u q", t=4, u=2)
+            for u in range(2):
+                if 0 in places:
+                    tr_bank[unit, u] = psum.tile([P, 4, P], F32, name="tr_bank", bufs=2)
+                for t in places:
+                    nc.tensor.transpose(tr_bank[unit, u][:, t, :], words[:, t, u, :], ident[:])
+
+        def copy_out(unit, u, copy):
+            if u == 0:
+                rel_t[unit] = ring.tile([P, 2048], BF16, name="rel", align_bytes=64)
+            copy(
+                out=rel_t[unit][:, 1024 * u : 1024 * (u + 1)].rearrange("q (e p t) -> q e p t", e=2, t=4),
+                in_=tr_bank[unit, u][:].bitcast(BF16).rearrange("q t (p e) -> q e p t", e=2),
             )
 
-        def store_0(row, count):
-            t, j = divmod(row, 4)
-            nc.sync.dma_start(
-                out=four_rows(out_0, t)[:, j : j + count, :], in_=o0_t[row // 2][:, row % 2 : row % 2 + count, :]
+        def quantize_tok(unit):
+            quantize(("tok",) + unit, tok_t[unit], E5M2)
+
+        def quantize_rel(unit):
+            quantize(("rel",) + unit, rel_t[unit], E5M2)
+
+        def p_gpsimd(t):
+            p_t[t] = shared_stage()
+            cols = slice(0, GPSIMD_COLS)
+            nc.gpsimd.tensor_tensor(
+                out=p_t[t][:].rearrange("p (c j) -> p c j", j=4)[:, cols, :],
+                in0=z_t[t][:, :, cols].rearrange("p j c -> p c j"),
+                in1=rz_t[t][:, :, cols].rearrange("p j c -> p c j"),
+                op=ALU.mult,
             )
 
-        def matmul_1(t, g, r):
-            if t == 0 and g == 1 and r >= 2:
-                acc[g, r] = ps_work.tile([P, H], F32, name="tr_bank", bufs=2)
-            elif t == 0:
-                acc[g, r] = ps_acc.tile([P, H], F32, name="acc%d" % r)
-            code, scale = stationary(tok_at[t, g, r])
+        def p_vector(t):
+            cols = slice(GPSIMD_COLS, H)
+            nc.vector.tensor_tensor(
+                out=by_two(p_t[t][:].rearrange("p (c j) -> p j c", j=4)[:, :, cols]),
+                in0=by_two(z_t[t][:, :, cols]),
+                in1=by_two(rz_t[t][:, :, cols]),
+                op=ALU.mult,
+            )
+
+        def quantize_rel_half(unit, u):
+            key = ("rel",) + unit
+            if u == 0:
+                codes[key] = keep.tile([P, 512], U32, name="code_%s%d%d" % key, align_bytes=64)
+                scales[key] = keep.tile([P, 512], U8, name="scale_%s%d%d" % key, align_bytes=64)
+            cols = slice(256 * u, 256 * (u + 1))
+            nc.vector.quantize_mx(
+                out=codes[key][:, cols].bitcast(E5M2),
+                scales=scales[key][:, cols],
+                in_=rel_t[unit][:, 1024 * u : 1024 * (u + 1)],
+            )
+
+        def quantize_p(t):
+            quantize(("p", t, 0), p_t[t], E4M3)
+
+        def pass_mx(bank, key, col, moving, start, stop):
             nc.tensor.matmul_mx(
-                out=acc[g, r][:],
-                lhsT=code,
-                lhsT_scale=scale,
-                rhs=p_code[:, t, :].bitcast(E4M3),
-                rhs_scale=p_scale[:, t, :],
-                start=(t == 0),
-                stop=(t == LAST),
+                out=bank[:],
+                lhsT=codes[key][:, col : col + P].bitcast(E5M2),
+                lhsT_scale=scales[key][:, col : col + P],
+                rhs=codes[moving][:].bitcast(E4M3),
+                rhs_scale=scales[moving][:],
+                start=start,
+                stop=stop,
             )
 
-        def finish_1(g, r, cols=slice(0, H)):
-            if r % 2 == 0:
-                o1_t[g, r // 2] = ring.tile([P, 2, H], F32, name="out_rows", bufs=8)
+        o0_bank, o1_bank, out_t = {}, {}, {}
+
+        def new_bank(tag):
+            return psum.tile([P, H], F32, name=tag, bufs=2 if tag in ("o_bank", "tr_bank") else 1)
+
+        def matmul_0(row, groups=range(NG), tag="o_bank"):
+            t, j = divmod(row, 4)
+            for g in groups:
+                if g == 0:
+                    o0_bank[row] = new_bank(tag)
+                if t == 0:
+                    key, col = ("rel", 0, j // 2), 256 * (j % 2) + P * g
+                else:
+                    key, col = ("rel", t, g), P * j
+                pass_mx(o0_bank[row], key, col, ("d", g, 0), g == 0, g == NG - 1)
+
+        def matmul_1(g, r, tiles, tag=None):
+            for t in tiles:
+                first = (g, r) not in o1_bank
+                if first:
+                    o1_bank[g, r] = new_bank(tag)
+                pass_mx(o1_bank[g, r], ("tok", t, g), P * r, ("p", t, 0), first, t == LAST)
+
+        def finish(key, bank, factor, other):
+            out_t[key] = ring.tile([P, H], F32, name="out_row", bufs=14)
             nc.vector.scalar_tensor_tensor(
-                out=o1_t[g, r // 2][:, r % 2, cols],
-                in0=acc[g, r][:, cols],
-                scalar=-2.0,
-                in1=d_t[g][:, r, cols],
-                op0=ALU.mult,
-                op1=ALU.mult,
+                out=out_t[key][:], in0=bank[:], scalar=factor, in1=other, op0=ALU.mult, op1=ALU.mult
             )
 
-        def store_1(g, r, cols=slice(0, H)):
-            nc.sync.dma_start(out=four_rows(out_1, g)[:, r, cols], in_=o1_t[g, r // 2][:, r % 2, cols])
+        def finish_0(row):
+            finish((0, row), o0_bank[row], -1.0, rz_t[row // 4][:, row % 4, :])
 
-        loads = [(k - S_LEAD, load_s, k) for k in range(STEPS) if k % 2 == 0 or not PAIRS_FROM <= k < STEPS - 4]
-        loads += [(2 * g - 1, load_d, g) for g in range(NG)]
-        loads += [(min(k for k in range(STEPS) if pair_of(k) == pair) - G_LEAD, load_g, pair) for pair in range(2 * NT)]
-        for t in range(NT):
-            loads += [(P_NEED[t], load_rz, t), (P_NEED[t], load_z, t)]
-        loads = sorted(loads, key=lambda entry: entry[0])
+        def finish_1(g, r):
+            finish((1, 4 * g + r), o1_bank[g, r], -2.0, d_t[g][:, r, :])
 
-        def issue_loads(after, until):
-            for need, load, arg in loads:
-                if after < need <= until:
-                    load(arg)
+        def store(which, row):
+            nc.sync.dma_start(out=four_rows((out_0, out_1)[which], row // 4)[:, row % 4, :], in_=out_t[which, row][:])
 
-        def gpsimd_unit(k):
-            if k == STEPS - 2:
-                return (LAST, 0, 0)
-            if k == STEPS - 1:
-                return (LAST - 1, 1, 0)
-            return (k // 4 - 1, k % 4 // 2, k % 2) if k >= 4 else None
-
-        late_a, late_b, late_c, late_d = STEPS + 1, STEPS + 2, STEPS + 3, STEPS + 4
-
-        issue_loads(-2, AHEAD)
+        load_s_row(0)
+        load_d(0)
+        load_s_row(1)
+        load_g_rows(0)
+        load_s_row(2)
+        load_g_rows(1)
+        load_s_row(3)
+        load_d(1)
+        load_s(UNITS[0])
+        load_g(UNITS[0])
+        load_s(UNITS[1])
+        load_g(UNITS[1])
+        load_z_rz(0)
         make_d2(0)
-        for k in range(2):
+        for j in range(4):
             for func in (ACT.Tanh, ACT.Square):
-                activate(func, k, slice(0, 512))
-                activate(func, k, slice(512, R))
+                activate_row(func, j, slice(0, 512))
+                activate_row(func, j, slice(512, R))
+        activate(UNITS[0])
+        dz_row(0)
+        transpose_row(0)
         quantize_d2(0)
-        for k in range(STEPS):
-            issue_loads(k + AHEAD, k + 1 + AHEAD)
-            if k >= STEPS - 4:
-                store_0(2 * (k - STEPS + 4), 2)
-            unit = gpsimd_unit(k)
-            make_dz(k)
-            if unit:
-                interleave_gpsimd(unit, k + 1)
-            if STAGE_FROM <= k + 1 < STEPS:
-                stage_g(k + 1)
-            if k == STEPS - 2:
-                interleave(nc.scalar.copy, (LAST, 0, 1), late_a, 0)
-            if k + 2 < STEPS:
-                activate(ACT.Tanh, k + 2)
-            if k >= 1:
-                copy_words(k - 1, k + 1)
-            if unit and k >= SCALAR_FROM:
-                interleave(nc.scalar.copy, unit, k + 1, 0, GPSIMD_SHARE)
-            if k + 2 < STEPS:
-                activate(ACT.Square, k + 2)
-            if k == STEPS - 1:
-                interleave(nc.scalar.copy, (LAST - 1, 1, 1), late_b, 0)
-            if k >= 5:
-                finish_0(k - 5)
-            if k == STEPS - 1:
-                transpose(k)
-            if k >= 4:
-                matmul_0(k - 4)
-            if k < STEPS - 1:
-                transpose(k)
-            jobs = []
-            if k == 1:
-                jobs.append((make_d2, 1))
-            if k == 3:
-                jobs.append((quantize_d2, 1))
-            if k == STEPS - 1:
-                jobs.append((quantize_dz, late_a))
-            if unit and k < SCALAR_FROM:
-                jobs.append((interleave, nc.vector.tensor_copy, unit, k + 1, 0, GPSIMD_SHARE))
-            jobs += [(quantize_p, t) for t, first in enumerate(P_STEPS) if k == first + 2]
-            jobs += [(make_p, t, k - first) for t, first in enumerate(P_STEPS) if first <= k < first + 2]
-            if k >= 2:
-                jobs.insert(max(len(jobs) - 1, 0), (quantize_dz, k))
-            for job, *args in jobs:
-                job(*args)
-            if k in (7, 11, 14, 15):
-                for r in range(4):
-                    matmul_1((7, 11, 14, 15).index(k), 0, r)
+        dz_row(1)
+        transpose_row(1)
+        copy_row(0)
+        dz_row(2)
+        transpose_row(2)
+        copy_row(1)
+        make_d2(1)
+        dz_row(3)
+        transpose_row(3)
+        stage_g(UNITS[0], 0)
+        load_s(UNITS[2])
+        load_g(UNITS[2])
+        load_z_rz(1)
+        load_s(UNITS[3])
+        quantize_rel((0, 0))
+        quantize_d2(1)
+        regroup(0)
+        copy_row(2)
+        make_dz(UNITS[0], 0)
+        stage_g(UNITS[0], 1)
+        copy_row(3)
+        make_dz(UNITS[0], 1)
+        transpose(UNITS[0])
+        stage_g(UNITS[1], 0)
+        quantize_tok(UNITS[0])
+        quantize_rel((0, 1))
+        quantize_tok((0, 0))
 
-        copy_words(STEPS - 1, late_b)
-        interleave(nc.scalar.copy, (LAST, 1, 0), late_c, 0)
-        interleave(nc.scalar.copy, (LAST, 1, 1), late_c, 1)
-        store_0(STEPS - 8, 2)
-        store_0(STEPS - 6, 1)
-        quantize_dz(STEPS)
-        finish_0(STEPS - 5)
-        store_0(STEPS - 5, 1)
-        matmul_0(STEPS - 4, "g_bank")
-        matmul_0(STEPS - 3)
-        for r in (2, 3):
-            for t in range(LAST - 1):
-                matmul_1(t, 1, r)
-        for r in range(2):
+        for i in range(1, 5):
+            unit, t = UNITS[i], i - 1
+            activate(unit)
+            for u in range(2):
+                copy_out(UNITS[i - 1], u, nc.scalar.copy)
+            p_gpsimd(t)
+            for row in (2 * t, 2 * t + 1):
+                matmul_0(row)
+            if t >= 1:
+                for r in range(3):
+                    matmul_1(0, r, [t - 1], "acc%d" % r)
+            make_dz(unit, 0)
+            stage_g(unit, 1)
+            for row in (2 * t, 2 * t + 1):
+                finish_0(row)
+            make_dz(unit, 1)
+            transpose(unit)
+            stage_g(UNITS[i + 1], 0)
+            if i + 2 < len(UNITS):
+                load_g(UNITS[i + 2])
+            quantize_tok(unit)
+            p_vector(t)
+            if t + 2 < NT:
+                load_z_rz(t + 2)
+            if i + 3 < len(UNITS):
+                load_s(UNITS[i + 3])
+            quantize_rel(UNITS[i - 1])
+            quantize_p(t)
+        for row in range(8):
+            store(0, row)
+
+        unit = UNITS[5]
+        activate(unit)
+        for u in range(2):
+            copy_out(UNITS[4], u, nc.scalar.copy)
+        regroup(1)
+        matmul_0(8)
+        matmul_0(9)
+        for r in range(3):
+            matmul_1(0, r, [LAST])
+        for row in (8, 9):
+            finish_0(row)
+            store(0, row)
+        matmul_0(10)
+        matmul_0(11)
+        finish_1(0, 0)
+        store(1, 0)
+        make_dz(unit, 0)
+        stage_g(unit, 1)
+        matmul_1(1, 0, (1, 2), "acc0")
+        for row in (10, 11):
+            finish_0(row)
+            store(0, row)
+        matmul_1(0, 3, range(NT), "o_bank")
+        for r in (1, 2):
             finish_1(0, r)
-            store_1(0, r)
-        quantize_dz(late_b)
-        for r in range(2):
-            finish_0(STEPS - 4 + r)
-            store_0(STEPS - 4 + r, 1)
-            matmul_0(STEPS - 2 + r, ("g_bank", "o0_bank")[r])
-        for r in (2, 3):
-            matmul_1(LAST - 1, 1, r)
-        for t in range(LAST):
-            matmul_1(t, 1, 0)
-        for r in (2, 3):
-            finish_1(0, r)
-            store_1(0, r)
-        quantize_dz(late_c)
-        for r in (2, 3, 0):
-            matmul_1(LAST, 1, r)
-        for t in range(NT):
-            matmul_1(t, 1, 1)
-        for r in range(2):
-            finish_0(STEPS - 2 + r)
-            store_0(STEPS - 2 + r, 1)
-        for r in (2, 3, 0):
+            store(1, r)
+        quantize_tok((0, 1))
+        transpose(unit, (0, 1))
+        for r in (1, 2):
+            matmul_1(1, r, (1, 2), "acc%d" % r)
+        make_dz(unit, 1)
+        transpose(unit, (2, 3))
+        for r in range(3):
+            matmul_1(1, r, [0])
+        matmul_1(1, 3, range(LAST), "g_bank")
+        finish_1(0, 3)
+        store(1, 3)
+        quantize_tok(unit)
+        quantize_rel(UNITS[4])
+        for r in range(4):
+            matmul_1(1, r, [LAST])
+        matmul_0(12, [0])
+        matmul_0(13, [0])
+        copy_out(unit, 0, nc.scalar.copy)
+        copy_out(unit, 1, nc.vector.tensor_copy)
+        quantize_rel_half(unit, 0)
+        finish_1(1, 0)
+        store(1, 4)
+        quantize_rel_half(unit, 1)
+        matmul_0(12, [1])
+        matmul_0(13, [1])
+        matmul_0(14, tag="tr_bank")
+        matmul_0(15, tag="tr_bank")
+        for r in (1, 2, 3):
             finish_1(1, r)
-            store_1(1, r)
-        for cols in (slice(0, 256), slice(256, H)):
-            finish_1(1, 1, cols)
-            store_1(1, 1, cols)
+            store(1, 4 + r)
+        for row in range(12, 16):
+            finish_0(row)
+            store(0, row)

@@ -22,7 +22,7 @@ NT = B // 512
 NG = R // 512
 LAST = NT - 1
 UNITS = [(t, g) for t in range(1, NT) for g in range(NG)]
-GPSIMD_COLS = 240
+GPSIMD_COLS = 224
 
 
 def tile_dedicomdecoder_v_kernel(tc, z_i, z_j, w_r, d_w, rz_in, scores, grad_out, out_0, out_1):
@@ -40,22 +40,32 @@ def tile_dedicomdecoder_v_kernel(tc, z_i, z_j, w_r, d_w, rz_in, scores, grad_out
 
         def load_s_row(j):
             if j % 2 == 0:
-                s_t[0, j // 2] = ring.tile([P, 2, R], F32, name="s_in", bufs=4)
+                s_t[0, j // 2] = ring.tile([P, 2, R], F32, name="s_in", bufs=6)
             nc.sync.dma_start(out=s_t[0, j // 2][:, j % 2, :], in_=four_rows(scores, 0)[:, j, :])
 
         def load_g_rows(u):
-            g_t[0, u] = ring.tile([P, 2, R], BF16, name="g_in", bufs=4)
-            nc.sync.dma_start(out=g_t[0, u][:], in_=four_rows(grad_out, 0)[:, 2 * u : 2 * u + 2, :])
+            if u == 0:
+                g_t[0] = ring.tile([P, 4, R], BF16, name="g_in")
+            nc.sync.dma_start(out=g_t[0][:, 2 * u : 2 * u + 2, :], in_=four_rows(grad_out, 0)[:, 2 * u : 2 * u + 2, :])
 
-        def load_s(unit):
+        s_at = {}
+
+        def load_s(t, u):
+            s_t[t, u] = ring.tile([P, 2, R], F32, name="s_in", bufs=6)
+            nc.sync.dma_start(out=s_t[t, u][:], in_=four_rows(scores, t)[:, 2 * u : 2 * u + 2, :])
+            for g in range(NG):
+                s_at[(t, g), u] = s_t[t, u][:, :, 512 * g : 512 * (g + 1)]
+
+        def load_s_unit(unit):
             t, g = unit
-            s_t[unit] = ring.tile([P, 4, 512], F32, name="s_in", bufs=4)
+            s_t[unit] = ring.tile([P, 4, 512], F32, name="s_in", bufs=6)
             nc.sync.dma_start(out=s_t[unit][:], in_=four_rows(scores, t)[:, :, 512 * g : 512 * (g + 1)])
+            for u in range(2):
+                s_at[unit, u] = s_t[unit][:, 2 * u : 2 * u + 2, :]
 
-        def load_g(unit):
-            t, g = unit
-            g_t[unit] = ring.tile([P, 4, 512], BF16, name="g_in", bufs=4)
-            nc.sync.dma_start(out=g_t[unit][:], in_=four_rows(grad_out, t)[:, :, 512 * g : 512 * (g + 1)])
+        def load_g(t):
+            g_t[t] = ring.tile([P, 4, R], BF16, name="g_in")
+            nc.sync.dma_start(out=g_t[t][:], in_=four_rows(grad_out, t))
 
         def load_d(g):
             d_t[g] = keep.tile([P, 4, H], BF16, name="d_rows%d" % g)
@@ -74,9 +84,16 @@ def tile_dedicomdecoder_v_kernel(tc, z_i, z_j, w_r, d_w, rz_in, scores, grad_out
 
         codes, scales = {}, {}
 
+        def new_codes(key):
+            if key[0] == "rel":
+                codes[key] = ring.tile([P, 512], U32, name="code_rel", bufs=4, align_bytes=64)
+                scales[key] = ring.tile([P, 512], U8, name="scale_rel", bufs=4, align_bytes=64)
+            else:
+                codes[key] = keep.tile([P, 512], U32, name="code_%s%d%d" % key, align_bytes=64)
+                scales[key] = keep.tile([P, 512], U8, name="scale_%s%d%d" % key, align_bytes=64)
+
         def quantize(key, staged, fmt):
-            codes[key] = keep.tile([P, 512], U32, name="code_%s%d%d" % key, align_bytes=64)
-            scales[key] = keep.tile([P, 512], U8, name="scale_%s%d%d" % key, align_bytes=64)
+            new_codes(key)
             nc.vector.quantize_mx(out=codes[key][:].bitcast(fmt), scales=scales[key][:], in_=staged[:])
 
         def by_two(ap):
@@ -110,13 +127,13 @@ def tile_dedicomdecoder_v_kernel(tc, z_i, z_j, w_r, d_w, rz_in, scores, grad_out
                 out=dz_rows[:, j, :],
                 in0=s_t[0, j // 2][:, j % 2, :],
                 scalar=0.25,
-                in1=g_t[0, j // 2][:, j % 2, :],
+                in1=g_t[0][:, j, :],
                 op0=ALU.subtract,
                 op1=ALU.mult,
             )
 
         def transpose_row(j):
-            tr_bank[0, j] = psum.tile([P, NG, 2, P], F32, name="tr_bank", bufs=2)
+            tr_bank[0, j] = psum.tile([P, NG, 2, P], F32, name="work_bank", bufs=2)
             words = dz_rows[:, j, :].bitcast(F32)
             for g in range(NG):
                 for h in range(2):
@@ -132,29 +149,33 @@ def tile_dedicomdecoder_v_kernel(tc, z_i, z_j, w_r, d_w, rz_in, scores, grad_out
                 in_=tr_bank[0, j][:].rearrange("q g h p -> q g p h"),
             )
 
-        def regroup(g):
-            tok_t[0, g] = shared_stage()
-            nc.gpsimd.tensor_copy(
-                out=tok_t[0, g][:].rearrange("p (t q j) -> p t q j", t=4, j=4),
-                in_=dz_rows[:, :, 512 * g : 512 * (g + 1)].rearrange("p j (q t) -> p t q j", t=4),
+        def regroup(g, copy, places=slice(0, 4)):
+            if (0, g) not in tok_t:
+                tok_t[0, g] = shared_stage()
+            copy(
+                out=tok_t[0, g][:].rearrange("p (t q j) -> p t q j", t=4, j=4)[:, places],
+                in_=dz_rows[:, :, 512 * g : 512 * (g + 1)].rearrange("p j (q t) -> p t q j", t=4)[:, places],
             )
+
+        def group(unit):
+            return slice(512 * unit[1], 512 * (unit[1] + 1))
 
         def tanh(unit, u):
             if u == 0:
-                x_t[unit] = ring.tile([P, 2, 2, P, 2, 2], F32, name="x_half")
+                x_t[unit] = keep.tile([P, 2, 2, P, 2, 2], F32, name="x_half")
             nc.scalar.activation(
                 out=x_t[unit][:, u].rearrange("p h q b e -> p q h b e"),
-                in_=s_t[unit][:, 2 * u : 2 * u + 2, :].rearrange("p e (q h b) -> p q h b e", h=2, b=2),
+                in_=s_at[unit, u].rearrange("p e (q h b) -> p q h b e", h=2, b=2),
                 func=ACT.Tanh,
                 scale=0.5,
             )
 
-        def squares(unit):
-            return s_t[unit][:].rearrange("p j n -> p (j n)").rearrange("p (t q j) -> p t q j", t=4, j=4)
+        def squares(unit, h):
+            return s_at[unit, h].rearrange("p b (q j) -> p b q j", j=4)
 
         def square(unit, h):
             nc.scalar.activation(
-                out=squares(unit)[:, 2 * h : 2 * h + 2].rearrange("p b q (u e) -> p q b u e", u=2),
+                out=squares(unit, h).rearrange("p b q (u e) -> p q b u e", u=2),
                 in_=x_t[unit][:, :, h].rearrange("p u q b e -> p q b u e"),
                 func=ACT.Square,
                 scale=0.5,
@@ -167,8 +188,8 @@ def tile_dedicomdecoder_v_kernel(tc, z_i, z_j, w_r, d_w, rz_in, scores, grad_out
                 square(unit, h)
 
         def stage_g(unit, h):
-            g_bank[unit, h] = psum.tile([P, 4, P, 2], BF16, name="g_bank")
-            pairs = g_t[unit][:].rearrange("p j (q h b) -> p j h q b", h=2, b=2)
+            g_bank[unit, h] = psum.tile([P, 4, P, 2], BF16, name="g_bank", bufs=2)
+            pairs = g_t[unit[0]][:, :, group(unit)].rearrange("p j (q h b) -> p j h q b", h=2, b=2)
             for u in range(2):
                 nc.tensor.matmul(
                     out=g_bank[unit, h][:, 2 * u : 2 * u + 2],
@@ -178,13 +199,13 @@ def tile_dedicomdecoder_v_kernel(tc, z_i, z_j, w_r, d_w, rz_in, scores, grad_out
                     stop=True,
                 )
 
-        def make_dz(unit, h):
-            if h == 0:
+        def make_dz(unit, h, places=range(2)):
+            if unit not in tok_t:
                 tok_t[unit] = ring.tile([P, 2048], BF16, name="tok", bufs=3, align_bytes=64)
-            for b in range(2):
+            for b in places:
                 nc.vector.scalar_tensor_tensor(
                     out=tok_t[unit][:].rearrange("p (t q j) -> p t q j", t=4, j=4)[:, 2 * h + b],
-                    in0=squares(unit)[:, 2 * h + b],
+                    in0=squares(unit, h)[:, b],
                     scalar=0.25,
                     in1=g_bank[unit, h][:, :, :, b].rearrange("p j q -> p q j"),
                     op0=ALU.subtract,
@@ -195,7 +216,7 @@ def tile_dedicomdecoder_v_kernel(tc, z_i, z_j, w_r, d_w, rz_in, scores, grad_out
             words = tok_t[unit][:].bitcast(F32).rearrange("p (t q u) -> p t u q", t=4, u=2)
             for u in range(2):
                 if 0 in places:
-                    tr_bank[unit, u] = psum.tile([P, 4, P], F32, name="tr_bank", bufs=2)
+                    tr_bank[unit, u] = psum.tile([P, 4, P], F32, name="work_bank", bufs=2)
                 for t in places:
                     nc.tensor.transpose(tr_bank[unit, u][:, t, :], words[:, t, u, :], ident[:])
 
@@ -232,18 +253,6 @@ def tile_dedicomdecoder_v_kernel(tc, z_i, z_j, w_r, d_w, rz_in, scores, grad_out
                 op=ALU.mult,
             )
 
-        def quantize_rel_half(unit, u):
-            key = ("rel",) + unit
-            if u == 0:
-                codes[key] = keep.tile([P, 512], U32, name="code_%s%d%d" % key, align_bytes=64)
-                scales[key] = keep.tile([P, 512], U8, name="scale_%s%d%d" % key, align_bytes=64)
-            cols = slice(256 * u, 256 * (u + 1))
-            nc.vector.quantize_mx(
-                out=codes[key][:, cols].bitcast(E5M2),
-                scales=scales[key][:, cols],
-                in_=rel_t[unit][:, 1024 * u : 1024 * (u + 1)],
-            )
-
         def quantize_p(t):
             quantize(("p", t, 0), p_t[t], E4M3)
 
@@ -261,9 +270,9 @@ def tile_dedicomdecoder_v_kernel(tc, z_i, z_j, w_r, d_w, rz_in, scores, grad_out
         o0_bank, o1_bank, out_t = {}, {}, {}
 
         def new_bank(tag):
-            return psum.tile([P, H], F32, name=tag, bufs=2 if tag in ("o_bank", "tr_bank") else 1)
+            return psum.tile([P, H], F32, name=tag, bufs=2 if tag in ("work_bank", "g_bank") else 1)
 
-        def matmul_0(row, groups=range(NG), tag="o_bank"):
+        def matmul_0(row, groups=range(NG), tag="work_bank"):
             t, j = divmod(row, 4)
             for g in groups:
                 if g == 0:
@@ -304,11 +313,12 @@ def tile_dedicomdecoder_v_kernel(tc, z_i, z_j, w_r, d_w, rz_in, scores, grad_out
         load_g_rows(1)
         load_s_row(3)
         load_d(1)
-        load_s(UNITS[0])
-        load_g(UNITS[0])
-        load_s(UNITS[1])
-        load_g(UNITS[1])
+        load_s_unit(UNITS[0])
+        load_g(1)
+        load_s_unit(UNITS[1])
         load_z_rz(0)
+        for u in range(2):
+            load_s(2, u)
         make_d2(0)
         for j in range(4):
             for func in (ACT.Tanh, ACT.Square):
@@ -327,21 +337,22 @@ def tile_dedicomdecoder_v_kernel(tc, z_i, z_j, w_r, d_w, rz_in, scores, grad_out
         make_d2(1)
         dz_row(3)
         transpose_row(3)
-        stage_g(UNITS[0], 0)
-        load_s(UNITS[2])
-        load_g(UNITS[2])
+        for h in range(2):
+            stage_g(UNITS[0], h)
+        load_g(2)
         load_z_rz(1)
-        load_s(UNITS[3])
+        load_s(LAST, 0)
         quantize_rel((0, 0))
         quantize_d2(1)
-        regroup(0)
+        regroup(0, nc.gpsimd.tensor_copy, slice(0, 3))
         copy_row(2)
         make_dz(UNITS[0], 0)
-        stage_g(UNITS[0], 1)
+        stage_g(UNITS[1], 0)
         copy_row(3)
         make_dz(UNITS[0], 1)
         transpose(UNITS[0])
-        stage_g(UNITS[1], 0)
+        stage_g(UNITS[1], 1)
+        regroup(0, nc.vector.tensor_copy, slice(3, 4))
         quantize_tok(UNITS[0])
         quantize_rel((0, 1))
         quantize_tok((0, 0))
@@ -355,23 +366,23 @@ def tile_dedicomdecoder_v_kernel(tc, z_i, z_j, w_r, d_w, rz_in, scores, grad_out
             for row in (2 * t, 2 * t + 1):
                 matmul_0(row)
             if t >= 1:
-                for r in range(3):
+                for r in range(4):
                     matmul_1(0, r, [t - 1], "acc%d" % r)
             make_dz(unit, 0)
-            stage_g(unit, 1)
+            stage_g(UNITS[i + 1], 0)
+            make_dz(unit, 1, [0])
             for row in (2 * t, 2 * t + 1):
                 finish_0(row)
-            make_dz(unit, 1)
+            make_dz(unit, 1, [1])
             transpose(unit)
-            stage_g(UNITS[i + 1], 0)
-            if i + 2 < len(UNITS):
-                load_g(UNITS[i + 2])
+            stage_g(UNITS[i + 1], 1)
             quantize_tok(unit)
             p_vector(t)
             if t + 2 < NT:
                 load_z_rz(t + 2)
-            if i + 3 < len(UNITS):
-                load_s(UNITS[i + 3])
+            if i == 1:
+                load_s(LAST, 1)
+                load_g(LAST)
             quantize_rel(UNITS[i - 1])
             quantize_p(t)
         for row in range(8):
@@ -381,56 +392,51 @@ def tile_dedicomdecoder_v_kernel(tc, z_i, z_j, w_r, d_w, rz_in, scores, grad_out
         activate(unit)
         for u in range(2):
             copy_out(UNITS[4], u, nc.scalar.copy)
-        regroup(1)
-        matmul_0(8)
-        matmul_0(9)
-        for r in range(3):
+        regroup(1, nc.gpsimd.tensor_copy)
+        for r in range(4):
             matmul_1(0, r, [LAST])
-        for row in (8, 9):
-            finish_0(row)
-            store(0, row)
-        matmul_0(10)
-        matmul_0(11)
-        finish_1(0, 0)
-        store(1, 0)
         make_dz(unit, 0)
-        stage_g(unit, 1)
-        matmul_1(1, 0, (1, 2), "acc0")
-        for row in (10, 11):
-            finish_0(row)
-            store(0, row)
-        matmul_1(0, 3, range(NT), "o_bank")
-        for r in (1, 2):
+        matmul_0(8, tag="g_bank")
+        for r in range(2):
             finish_1(0, r)
             store(1, r)
-        quantize_tok((0, 1))
-        transpose(unit, (0, 1))
-        for r in (1, 2):
             matmul_1(1, r, (1, 2), "acc%d" % r)
         make_dz(unit, 1)
-        transpose(unit, (2, 3))
-        for r in range(3):
-            matmul_1(1, r, [0])
-        matmul_1(1, 3, range(LAST), "g_bank")
-        finish_1(0, 3)
-        store(1, 3)
+        transpose(unit)
+        matmul_0(9, tag="g_bank")
+        for u in range(2):
+            copy_out(unit, u, nc.scalar.copy)
+        finish_0(8)
+        store(0, 8)
+        matmul_0(10, tag="g_bank")
         quantize_tok(unit)
+        quantize_tok((0, 1))
         quantize_rel(UNITS[4])
-        for r in range(4):
-            matmul_1(1, r, [LAST])
-        matmul_0(12, [0])
-        matmul_0(13, [0])
-        copy_out(unit, 0, nc.scalar.copy)
-        copy_out(unit, 1, nc.vector.tensor_copy)
-        quantize_rel_half(unit, 0)
+        for r in range(2):
+            matmul_1(1, r, (0, LAST))
+        for r in (2, 3):
+            finish_1(0, r)
+            store(1, r)
+        finish_0(9)
+        store(0, 9)
+        matmul_0(11, tag="g_bank")
+        for r in (2, 3):
+            matmul_1(1, r, range(NT), "acc%d" % r)
+        finish_0(10)
+        store(0, 10)
+        matmul_0(12, [0], tag="g_bank")
         finish_1(1, 0)
         store(1, 4)
-        quantize_rel_half(unit, 1)
+        quantize_rel(unit)
+        finish_0(11)
+        store(0, 11)
+        finish_1(1, 1)
+        store(1, 5)
         matmul_0(12, [1])
-        matmul_0(13, [1])
-        matmul_0(14, tag="tr_bank")
-        matmul_0(15, tag="tr_bank")
-        for r in (1, 2, 3):
+        matmul_0(13, tag="g_bank")
+        matmul_0(14)
+        matmul_0(15)
+        for r in (2, 3):
             finish_1(1, r)
             store(1, 4 + r)
         for row in range(12, 16):

@@ -238,9 +238,9 @@ def tile_dedicomdecoder_v_kernel(tc, z_i, z_j, w_r, d_w, rz_in, scores, grad_out
             p_t[t] = shared_stage()
             cols = slice(0, GPSIMD_COLS)
             nc.gpsimd.tensor_tensor(
-                out=p_t[t][:].rearrange("p (c j) -> p c j", j=4)[:, cols, :],
-                in0=z_t[t][:, :, cols].rearrange("p j c -> p c j"),
-                in1=rz_t[t][:, :, cols].rearrange("p j c -> p c j"),
+                out=by_two(p_t[t][:].rearrange("p (c j) -> p j c", j=4)[:, :, cols]),
+                in0=by_two(z_t[t][:, :, cols]),
+                in1=by_two(rz_t[t][:, :, cols]),
                 op=ALU.mult,
             )
 

@@ -22,7 +22,7 @@ NT = B // 512
 NG = R // 512
 LAST = NT - 1
 UNITS = [(t, g) for t in range(1, NT) for g in range(NG)]
-GPSIMD_COLS = 224
+GPSIMD_COLS = 288
 
 
 def tile_dedicomdecoder_v_kernel(tc, z_i, z_j, w_r, d_w, rz_in, scores, grad_out, out_0, out_1):
@@ -40,7 +40,7 @@ def tile_dedicomdecoder_v_kernel(tc, z_i, z_j, w_r, d_w, rz_in, scores, grad_out
 
         def load_s_row(j):
             if j % 2 == 0:
-                s_t[0, j // 2] = ring.tile([P, 2, R], F32, name="s_in", bufs=6)
+                s_t[0, j // 2] = ring.tile([P, 2, R], F32, name="s_in", bufs=5)
             nc.sync.dma_start(out=s_t[0, j // 2][:, j % 2, :], in_=four_rows(scores, 0)[:, j, :])
 
         def load_g_rows(u):
@@ -50,15 +50,9 @@ def tile_dedicomdecoder_v_kernel(tc, z_i, z_j, w_r, d_w, rz_in, scores, grad_out
 
         s_at = {}
 
-        def load_s(t, u):
-            s_t[t, u] = ring.tile([P, 2, R], F32, name="s_in", bufs=6)
-            nc.sync.dma_start(out=s_t[t, u][:], in_=four_rows(scores, t)[:, 2 * u : 2 * u + 2, :])
-            for g in range(NG):
-                s_at[(t, g), u] = s_t[t, u][:, :, 512 * g : 512 * (g + 1)]
-
-        def load_s_unit(unit):
+        def load_s(unit):
             t, g = unit
-            s_t[unit] = ring.tile([P, 4, 512], F32, name="s_in", bufs=6)
+            s_t[unit] = ring.tile([P, 4, 512], F32, name="s_in", bufs=5)
             nc.sync.dma_start(out=s_t[unit][:], in_=four_rows(scores, t)[:, :, 512 * g : 512 * (g + 1)])
             for u in range(2):
                 s_at[unit, u] = s_t[unit][:, 2 * u : 2 * u + 2, :]
@@ -162,7 +156,7 @@ def tile_dedicomdecoder_v_kernel(tc, z_i, z_j, w_r, d_w, rz_in, scores, grad_out
 
         def tanh(unit, u):
             if u == 0:
-                x_t[unit] = keep.tile([P, 2, 2, P, 2, 2], F32, name="x_half")
+                x_t[unit] = ring.tile([P, 2, 2, P, 2, 2], F32, name="x_half")
             nc.scalar.activation(
                 out=x_t[unit][:, u].rearrange("p h q b e -> p q h b e"),
                 in_=s_at[unit, u].rearrange("p e (q h b) -> p q h b e", h=2, b=2),
@@ -171,11 +165,11 @@ def tile_dedicomdecoder_v_kernel(tc, z_i, z_j, w_r, d_w, rz_in, scores, grad_out
             )
 
         def squares(unit, h):
-            return s_at[unit, h].rearrange("p b (q j) -> p b q j", j=4)
+            return s_at[unit, h].rearrange("p b (q j) -> p (b q) j", j=4)
 
         def square(unit, h):
             nc.scalar.activation(
-                out=squares(unit, h).rearrange("p b q (u e) -> p q b u e", u=2),
+                out=squares(unit, h).rearrange("p (b q) (u e) -> p q b u e", b=2, u=2),
                 in_=x_t[unit][:, :, h].rearrange("p u q b e -> p q b u e"),
                 func=ACT.Square,
                 scale=0.5,
@@ -187,30 +181,37 @@ def tile_dedicomdecoder_v_kernel(tc, z_i, z_j, w_r, d_w, rz_in, scores, grad_out
             for h in range(2):
                 square(unit, h)
 
+        def scalar_round(i):
+            for u in range(2):
+                tanh(UNITS[i], u)
+            square(UNITS[i], 0)
+            for u in range(2):
+                copy_out(UNITS[i - 1], u, nc.scalar.copy)
+            square(UNITS[i], 1)
+
         def stage_g(unit, h):
-            g_bank[unit, h] = psum.tile([P, 4, P, 2], BF16, name="g_bank", bufs=2)
-            pairs = g_t[unit[0]][:, :, group(unit)].rearrange("p j (q h b) -> p j h q b", h=2, b=2)
+            g_bank[unit, h] = psum.tile([P, 4, 2, P], BF16, name="g_bank", bufs=2)
+            places = g_t[unit[0]][:, :, group(unit)].rearrange("p j (q t) -> p j t q", t=4)
             for u in range(2):
                 nc.tensor.matmul(
                     out=g_bank[unit, h][:, 2 * u : 2 * u + 2],
                     lhsT=ident_bf[:],
-                    rhs=pairs[:, 2 * u : 2 * u + 2, h],
+                    rhs=places[:, 2 * u : 2 * u + 2, 2 * h : 2 * h + 2],
                     start=True,
                     stop=True,
                 )
 
-        def make_dz(unit, h, places=range(2)):
+        def make_dz(unit, h):
             if unit not in tok_t:
                 tok_t[unit] = ring.tile([P, 2048], BF16, name="tok", bufs=3, align_bytes=64)
-            for b in places:
-                nc.vector.scalar_tensor_tensor(
-                    out=tok_t[unit][:].rearrange("p (t q j) -> p t q j", t=4, j=4)[:, 2 * h + b],
-                    in0=squares(unit, h)[:, b],
-                    scalar=0.25,
-                    in1=g_bank[unit, h][:, :, :, b].rearrange("p j q -> p q j"),
-                    op0=ALU.subtract,
-                    op1=ALU.mult,
-                )
+            nc.vector.scalar_tensor_tensor(
+                out=tok_t[unit][:, 1024 * h : 1024 * (h + 1)].rearrange("p (c j) -> p c j", j=4),
+                in0=squares(unit, h),
+                scalar=0.25,
+                in1=g_bank[unit, h][:].rearrange("p j b q -> p (b q) j"),
+                op0=ALU.subtract,
+                op1=ALU.mult,
+            )
 
         def transpose(unit, places=range(4)):
             words = tok_t[unit][:].bitcast(F32).rearrange("p (t q u) -> p t u q", t=4, u=2)
@@ -296,11 +297,16 @@ def tile_dedicomdecoder_v_kernel(tc, z_i, z_j, w_r, d_w, rz_in, scores, grad_out
                 out=out_t[key][:], in0=bank[:], scalar=factor, in1=other, op0=ALU.mult, op1=ALU.mult
             )
 
-        def finish_0(row):
-            finish((0, row), o0_bank[row], -1.0, rz_t[row // 4][:, row % 4, :])
+        def finish_aside(key, bank, factor, other):
+            out_t[key] = ring.tile([P, H], F32, name="out_row", bufs=14)
+            nc.scalar.mul(out=out_t[key][:], in_=bank[:], mul=factor)
+            nc.gpsimd.tensor_tensor(out=out_t[key][:], in0=out_t[key][:], in1=other, op=ALU.mult)
 
-        def finish_1(g, r):
-            finish((1, 4 * g + r), o1_bank[g, r], -2.0, d_t[g][:, r, :])
+        def finish_0(row, how=finish):
+            how((0, row), o0_bank[row], -1.0, rz_t[row // 4][:, row % 4, :])
+
+        def finish_1(g, r, how=finish):
+            how((1, 4 * g + r), o1_bank[g, r], -2.0, d_t[g][:, r, :])
 
         def store(which, row):
             nc.sync.dma_start(out=four_rows((out_0, out_1)[which], row // 4)[:, row % 4, :], in_=out_t[which, row][:])
@@ -313,12 +319,11 @@ def tile_dedicomdecoder_v_kernel(tc, z_i, z_j, w_r, d_w, rz_in, scores, grad_out
         load_g_rows(1)
         load_s_row(3)
         load_d(1)
-        load_s_unit(UNITS[0])
+        load_s(UNITS[0])
         load_g(1)
-        load_s_unit(UNITS[1])
+        load_s(UNITS[1])
         load_z_rz(0)
-        for u in range(2):
-            load_s(2, u)
+        load_s(UNITS[2])
         make_d2(0)
         for j in range(4):
             for func in (ACT.Tanh, ACT.Square):
@@ -341,7 +346,7 @@ def tile_dedicomdecoder_v_kernel(tc, z_i, z_j, w_r, d_w, rz_in, scores, grad_out
             stage_g(UNITS[0], h)
         load_g(2)
         load_z_rz(1)
-        load_s(LAST, 0)
+        load_s(UNITS[3])
         quantize_rel((0, 0))
         quantize_d2(1)
         regroup(0, nc.gpsimd.tensor_copy, slice(0, 3))
@@ -359,86 +364,89 @@ def tile_dedicomdecoder_v_kernel(tc, z_i, z_j, w_r, d_w, rz_in, scores, grad_out
 
         for i in range(1, 5):
             unit, t = UNITS[i], i - 1
-            activate(unit)
-            for u in range(2):
-                copy_out(UNITS[i - 1], u, nc.scalar.copy)
+            rows = (2 * t, 2 * t + 1)
+            scalar_round(i)
             p_gpsimd(t)
-            for row in (2 * t, 2 * t + 1):
-                matmul_0(row)
+            matmul_0(rows[0])
             if t >= 1:
-                for r in range(4):
+                for r in range(2):
+                    matmul_1(0, r, [t - 1], "acc%d" % r)
+            matmul_0(rows[1])
+            if t >= 1:
+                for r in range(2, 4):
                     matmul_1(0, r, [t - 1], "acc%d" % r)
             make_dz(unit, 0)
             stage_g(UNITS[i + 1], 0)
-            make_dz(unit, 1, [0])
-            for row in (2 * t, 2 * t + 1):
+            for row in rows:
                 finish_0(row)
-            make_dz(unit, 1, [1])
-            transpose(unit)
+            transpose(unit, (0, 1))
+            make_dz(unit, 1)
+            transpose(unit, (2, 3))
             stage_g(UNITS[i + 1], 1)
-            quantize_tok(unit)
             p_vector(t)
             if t + 2 < NT:
                 load_z_rz(t + 2)
+                load_s(UNITS[i + 3])
             if i == 1:
-                load_s(LAST, 1)
                 load_g(LAST)
+            quantize_tok(unit)
             quantize_rel(UNITS[i - 1])
             quantize_p(t)
         for row in range(8):
             store(0, row)
 
         unit = UNITS[5]
-        activate(unit)
-        for u in range(2):
-            copy_out(UNITS[4], u, nc.scalar.copy)
+        scalar_round(5)
         regroup(1, nc.gpsimd.tensor_copy)
-        for r in range(4):
+        matmul_0(8)
+        matmul_1(0, 0, [LAST])
+        matmul_0(9)
+        for r in range(1, 4):
             matmul_1(0, r, [LAST])
         make_dz(unit, 0)
-        matmul_0(8, tag="g_bank")
+        matmul_0(10, tag="g_bank")
+        for r in range(2):
+            finish_0(8 + r)
+            store(0, 8 + r)
+        transpose(unit, (0, 1))
+        finish_1(0, 2, finish_aside)
+        matmul_1(1, 2, (1, 2), "acc2")
+        make_dz(unit, 1)
+        transpose(unit, (2, 3))
         for r in range(2):
             finish_1(0, r)
             store(1, r)
             matmul_1(1, r, (1, 2), "acc%d" % r)
-        make_dz(unit, 1)
-        transpose(unit)
-        matmul_0(9, tag="g_bank")
+        matmul_0(11, tag="g_bank")
         for u in range(2):
             copy_out(unit, u, nc.scalar.copy)
-        finish_0(8)
-        store(0, 8)
-        matmul_0(10, tag="g_bank")
-        quantize_tok(unit)
+        finish_1(0, 3)
+        store(1, 3)
+        store(1, 2)
+        matmul_1(1, 3, (1, 2), "acc3")
         quantize_tok((0, 1))
+        quantize_tok(unit)
         quantize_rel(UNITS[4])
-        for r in range(2):
+        for r in range(4):
             matmul_1(1, r, (0, LAST))
-        for r in (2, 3):
-            finish_1(0, r)
-            store(1, r)
-        finish_0(9)
-        store(0, 9)
-        matmul_0(11, tag="g_bank")
-        for r in (2, 3):
-            matmul_1(1, r, range(NT), "acc%d" % r)
-        finish_0(10)
-        store(0, 10)
-        matmul_0(12, [0], tag="g_bank")
-        finish_1(1, 0)
-        store(1, 4)
+        for row in (10, 11):
+            finish_0(row)
+            store(0, row)
+            matmul_0(row + 2, [0], tag="g_bank")
         quantize_rel(unit)
-        finish_0(11)
-        store(0, 11)
-        finish_1(1, 1)
-        store(1, 5)
+        for r in range(2):
+            finish_1(1, r, finish_aside)
         matmul_0(12, [1])
-        matmul_0(13, tag="g_bank")
+        matmul_0(13, [1])
         matmul_0(14)
         matmul_0(15)
-        for r in (2, 3):
-            finish_1(1, r)
-            store(1, 4 + r)
+        finish_1(1, 2)
+        store(1, 6)
+        finish_1(1, 3)
+        store(1, 7)
+        store(1, 4)
         for row in range(12, 16):
             finish_0(row)
             store(0, row)
+            if row == 12:
+                store(1, 5)

@@ -22,7 +22,7 @@ NT = B // 512
 NG = R // 512
 LAST = NT - 1
 UNITS = [(t, g) for t in range(1, NT) for g in range(NG)]
-GPSIMD_COLS = 288
+GPSIMD_COLS = 224
 
 
 def tile_dedicomdecoder_v_kernel(tc, z_i, z_j, w_r, d_w, rz_in, scores, grad_out, out_0, out_1):
@@ -165,11 +165,11 @@ def tile_dedicomdecoder_v_kernel(tc, z_i, z_j, w_r, d_w, rz_in, scores, grad_out
             )
 
         def squares(unit, h):
-            return s_at[unit, h].rearrange("p b (q j) -> p (b q) j", j=4)
+            return s_at[unit, h].rearrange("p b (q j) -> p b q j", j=4)
 
         def square(unit, h):
             nc.scalar.activation(
-                out=squares(unit, h).rearrange("p (b q) (u e) -> p q b u e", b=2, u=2),
+                out=squares(unit, h).rearrange("p b q (u e) -> p q b u e", u=2),
                 in_=x_t[unit][:, :, h].rearrange("p u q b e -> p q b u e"),
                 func=ACT.Square,
                 scale=0.5,
@@ -190,13 +190,13 @@ def tile_dedicomdecoder_v_kernel(tc, z_i, z_j, w_r, d_w, rz_in, scores, grad_out
             square(UNITS[i], 1)
 
         def stage_g(unit, h):
-            g_bank[unit, h] = psum.tile([P, 4, 2, P], BF16, name="g_bank", bufs=2)
-            places = g_t[unit[0]][:, :, group(unit)].rearrange("p j (q t) -> p j t q", t=4)
+            g_bank[unit, h] = psum.tile([P, 4, P, 2], BF16, name="g_bank", bufs=2)
+            pairs = g_t[unit[0]][:, :, group(unit)].rearrange("p j (q h b) -> p j h q b", h=2, b=2)
             for u in range(2):
                 nc.tensor.matmul(
                     out=g_bank[unit, h][:, 2 * u : 2 * u + 2],
                     lhsT=ident_bf[:],
-                    rhs=places[:, 2 * u : 2 * u + 2, 2 * h : 2 * h + 2],
+                    rhs=pairs[:, 2 * u : 2 * u + 2, h],
                     start=True,
                     stop=True,
                 )
@@ -204,14 +204,15 @@ def tile_dedicomdecoder_v_kernel(tc, z_i, z_j, w_r, d_w, rz_in, scores, grad_out
         def make_dz(unit, h):
             if unit not in tok_t:
                 tok_t[unit] = ring.tile([P, 2048], BF16, name="tok", bufs=3, align_bytes=64)
-            nc.vector.scalar_tensor_tensor(
-                out=tok_t[unit][:, 1024 * h : 1024 * (h + 1)].rearrange("p (c j) -> p c j", j=4),
-                in0=squares(unit, h),
-                scalar=0.25,
-                in1=g_bank[unit, h][:].rearrange("p j b q -> p (b q) j"),
-                op0=ALU.subtract,
-                op1=ALU.mult,
-            )
+            for b in range(2):
+                nc.vector.scalar_tensor_tensor(
+                    out=tok_t[unit][:].rearrange("p (t q j) -> p t q j", t=4, j=4)[:, 2 * h + b],
+                    in0=squares(unit, h)[:, b],
+                    scalar=0.25,
+                    in1=g_bank[unit, h][:, :, :, b].rearrange("p j q -> p q j"),
+                    op0=ALU.subtract,
+                    op1=ALU.mult,
+                )
 
         def transpose(unit, places=range(4)):
             words = tok_t[unit][:].bitcast(F32).rearrange("p (t q u) -> p t u q", t=4, u=2)
@@ -291,25 +292,36 @@ def tile_dedicomdecoder_v_kernel(tc, z_i, z_j, w_r, d_w, rz_in, scores, grad_out
                     o1_bank[g, r] = new_bank(tag)
                 pass_mx(o1_bank[g, r], ("tok", t, g), P * r, ("p", t, 0), first, t == LAST)
 
-        def finish(key, bank, factor, other):
-            out_t[key] = ring.tile([P, H], F32, name="out_row", bufs=14)
+        def out_row(which, row):
+            if (which, row // 2) not in out_t:
+                out_t[which, row // 2] = ring.tile([P, 2, H], F32, name="out_rows", bufs=7)
+            return out_t[which, row // 2][:, row % 2, :]
+
+        def finish(key, bank, factor, other, cols=slice(0, H)):
             nc.vector.scalar_tensor_tensor(
-                out=out_t[key][:], in0=bank[:], scalar=factor, in1=other, op0=ALU.mult, op1=ALU.mult
+                out=out_row(*key)[:, cols],
+                in0=bank[:, cols],
+                scalar=factor,
+                in1=other[:, cols],
+                op0=ALU.mult,
+                op1=ALU.mult,
             )
 
         def finish_aside(key, bank, factor, other):
-            out_t[key] = ring.tile([P, H], F32, name="out_row", bufs=14)
-            nc.scalar.mul(out=out_t[key][:], in_=bank[:], mul=factor)
-            nc.gpsimd.tensor_tensor(out=out_t[key][:], in0=out_t[key][:], in1=other, op=ALU.mult)
+            nc.scalar.mul(out=out_row(*key), in_=bank[:], mul=factor)
+            nc.gpsimd.tensor_tensor(out=out_row(*key), in0=out_row(*key), in1=other, op=ALU.mult)
 
-        def finish_0(row, how=finish):
-            how((0, row), o0_bank[row], -1.0, rz_t[row // 4][:, row % 4, :])
+        def finish_0(row, cols=slice(0, H)):
+            finish((0, row), o0_bank[row], -1.0, rz_t[row // 4][:, row % 4, :], cols)
 
         def finish_1(g, r, how=finish):
             how((1, 4 * g + r), o1_bank[g, r], -2.0, d_t[g][:, r, :])
 
-        def store(which, row):
-            nc.sync.dma_start(out=four_rows((out_0, out_1)[which], row // 4)[:, row % 4, :], in_=out_t[which, row][:])
+        def store(which, row, count=2, cols=slice(0, H)):
+            nc.sync.dma_start(
+                out=four_rows((out_0, out_1)[which], row // 4)[:, row % 4 : row % 4 + count, cols],
+                in_=out_t[which, row // 2][:, row % 2 : row % 2 + count, cols],
+            )
 
         load_s_row(0)
         load_d(0)
@@ -318,8 +330,8 @@ def tile_dedicomdecoder_v_kernel(tc, z_i, z_j, w_r, d_w, rz_in, scores, grad_out
         load_s_row(2)
         load_g_rows(1)
         load_s_row(3)
-        load_d(1)
         load_s(UNITS[0])
+        load_d(1)
         load_g(1)
         load_s(UNITS[1])
         load_z_rz(0)
@@ -339,9 +351,9 @@ def tile_dedicomdecoder_v_kernel(tc, z_i, z_j, w_r, d_w, rz_in, scores, grad_out
         dz_row(2)
         transpose_row(2)
         copy_row(1)
-        make_d2(1)
         dz_row(3)
         transpose_row(3)
+        make_d2(1)
         for h in range(2):
             stage_g(UNITS[0], h)
         load_g(2)
@@ -354,8 +366,9 @@ def tile_dedicomdecoder_v_kernel(tc, z_i, z_j, w_r, d_w, rz_in, scores, grad_out
         make_dz(UNITS[0], 0)
         stage_g(UNITS[1], 0)
         copy_row(3)
+        transpose(UNITS[0], (0, 1))
         make_dz(UNITS[0], 1)
-        transpose(UNITS[0])
+        transpose(UNITS[0], (2, 3))
         stage_g(UNITS[1], 1)
         regroup(0, nc.vector.tensor_copy, slice(3, 4))
         quantize_tok(UNITS[0])
@@ -392,7 +405,7 @@ def tile_dedicomdecoder_v_kernel(tc, z_i, z_j, w_r, d_w, rz_in, scores, grad_out
             quantize_tok(unit)
             quantize_rel(UNITS[i - 1])
             quantize_p(t)
-        for row in range(8):
+        for row in range(0, 8, 2):
             store(0, row)
 
         unit = UNITS[5]
@@ -405,25 +418,22 @@ def tile_dedicomdecoder_v_kernel(tc, z_i, z_j, w_r, d_w, rz_in, scores, grad_out
             matmul_1(0, r, [LAST])
         make_dz(unit, 0)
         matmul_0(10, tag="g_bank")
-        for r in range(2):
-            finish_0(8 + r)
-            store(0, 8 + r)
+        for row in (8, 9):
+            finish_0(row)
+        store(0, 8)
         transpose(unit, (0, 1))
-        finish_1(0, 2, finish_aside)
-        matmul_1(1, 2, (1, 2), "acc2")
         make_dz(unit, 1)
         transpose(unit, (2, 3))
-        for r in range(2):
+        finish_1(0, 3, finish_aside)
+        matmul_1(1, 3, (1, 2), "acc3")
+        for r in range(3):
             finish_1(0, r)
-            store(1, r)
             matmul_1(1, r, (1, 2), "acc%d" % r)
+        store(1, 0)
+        store(1, 2)
         matmul_0(11, tag="g_bank")
         for u in range(2):
             copy_out(unit, u, nc.scalar.copy)
-        finish_1(0, 3)
-        store(1, 3)
-        store(1, 2)
-        matmul_1(1, 3, (1, 2), "acc3")
         quantize_tok((0, 1))
         quantize_tok(unit)
         quantize_rel(UNITS[4])
@@ -431,22 +441,22 @@ def tile_dedicomdecoder_v_kernel(tc, z_i, z_j, w_r, d_w, rz_in, scores, grad_out
             matmul_1(1, r, (0, LAST))
         for row in (10, 11):
             finish_0(row)
-            store(0, row)
             matmul_0(row + 2, [0], tag="g_bank")
+        store(0, 10)
+        finish_1(1, 0)
         quantize_rel(unit)
-        for r in range(2):
-            finish_1(1, r, finish_aside)
+        finish_1(1, 1)
+        store(1, 4)
         matmul_0(12, [1])
         matmul_0(13, [1])
         matmul_0(14)
         matmul_0(15)
-        finish_1(1, 2)
-        store(1, 6)
-        finish_1(1, 3)
-        store(1, 7)
-        store(1, 4)
-        for row in range(12, 16):
+        for r in (2, 3):
+            finish_1(1, r)
+            store(1, 4 + r, 1)
+        for row in range(12, 15):
             finish_0(row)
-            store(0, row)
-            if row == 12:
-                store(1, 5)
+            store(0, row, 1)
+        for cols in (slice(0, 256), slice(256, H)):
+            finish_0(15, cols)
+            store(0, 15, 1, cols)

@@ -127,7 +127,7 @@ def tile_dedicomdecoder_v_kernel(tc, z_i, z_j, w_r, d_w, rz_in, scores, grad_out
             )
 
         def transpose_row(j):
-            tr_bank[0, j] = psum.tile([P, NG, 2, P], F32, name="work_bank", bufs=2)
+            tr_bank[0, j] = psum.tile([P, NG, 2, P], F32, name="tr_bank", bufs=2)
             words = dz_rows[:, j, :].bitcast(F32)
             for g in range(NG):
                 for h in range(2):
@@ -190,7 +190,7 @@ def tile_dedicomdecoder_v_kernel(tc, z_i, z_j, w_r, d_w, rz_in, scores, grad_out
             square(UNITS[i], 1)
 
         def stage_g(unit, h):
-            g_bank[unit, h] = psum.tile([P, 4, P, 2], BF16, name="g_bank", bufs=2)
+            g_bank[unit, h] = psum.tile([P, 4, P, 2], BF16, name="ring_bank", bufs=3)
             pairs = g_t[unit[0]][:, :, group(unit)].rearrange("p j (q h b) -> p j h q b", h=2, b=2)
             for u in range(2):
                 nc.tensor.matmul(
@@ -218,7 +218,7 @@ def tile_dedicomdecoder_v_kernel(tc, z_i, z_j, w_r, d_w, rz_in, scores, grad_out
             words = tok_t[unit][:].bitcast(F32).rearrange("p (t q u) -> p t u q", t=4, u=2)
             for u in range(2):
                 if 0 in places:
-                    tr_bank[unit, u] = psum.tile([P, 4, P], F32, name="work_bank", bufs=2)
+                    tr_bank[unit, u] = psum.tile([P, 4, P], F32, name="tr_bank", bufs=2)
                 for t in places:
                     nc.tensor.transpose(tr_bank[unit, u][:, t, :], words[:, t, u, :], ident[:])
 
@@ -269,12 +269,12 @@ def tile_dedicomdecoder_v_kernel(tc, z_i, z_j, w_r, d_w, rz_in, scores, grad_out
                 stop=stop,
             )
 
-        o0_bank, o1_bank, out_t = {}, {}, {}
+        o0_bank, o1_bank, o1_done, out_t = {}, {}, {}, {}
 
         def new_bank(tag):
-            return psum.tile([P, H], F32, name=tag, bufs=2 if tag in ("work_bank", "g_bank") else 1)
+            return psum.tile([P, H], F32, name=tag, bufs={"tr_bank": 2, "ring_bank": 3}.get(tag, 1))
 
-        def matmul_0(row, groups=range(NG), tag="work_bank"):
+        def matmul_0(row, groups=range(NG), tag="ring_bank"):
             t, j = divmod(row, 4)
             for g in groups:
                 if g == 0:
@@ -287,10 +287,11 @@ def tile_dedicomdecoder_v_kernel(tc, z_i, z_j, w_r, d_w, rz_in, scores, grad_out
 
         def matmul_1(g, r, tiles, tag=None):
             for t in tiles:
-                first = (g, r) not in o1_bank
-                if first:
+                done = o1_done.setdefault((g, r), [])
+                if not done:
                     o1_bank[g, r] = new_bank(tag)
-                pass_mx(o1_bank[g, r], ("tok", t, g), P * r, ("p", t, 0), first, t == LAST)
+                done.append(t)
+                pass_mx(o1_bank[g, r], ("tok", t, g), P * r, ("p", t, 0), len(done) == 1, len(done) == NT)
 
         def out_row(which, row):
             if (which, row // 2) not in out_t:
@@ -307,15 +308,23 @@ def tile_dedicomdecoder_v_kernel(tc, z_i, z_j, w_r, d_w, rz_in, scores, grad_out
                 op1=ALU.mult,
             )
 
-        def finish_aside(key, bank, factor, other):
-            nc.scalar.mul(out=out_row(*key), in_=bank[:], mul=factor)
-            nc.gpsimd.tensor_tensor(out=out_row(*key), in0=out_row(*key), in1=other, op=ALU.mult)
+        aside_t = {}
+
+        def copy_aside(g, r):
+            nc.scalar.mul(out=out_row(1, 4 * g + r), in_=o1_bank[g, r][:], mul=-2.0)
+
+        def finish_aside(g, r, held):
+            aside_t[g, r] = held
+            nc.gpsimd.tensor_tensor(out=held, in0=out_row(1, 4 * g + r), in1=d_t[g][:, r, :], op=ALU.mult)
+
+        def store_aside(g, r, queue):
+            queue.dma_start(out=four_rows(out_1, g)[:, r, :], in_=aside_t[g, r])
 
         def finish_0(row, cols=slice(0, H)):
             finish((0, row), o0_bank[row], -1.0, rz_t[row // 4][:, row % 4, :], cols)
 
-        def finish_1(g, r, how=finish):
-            how((1, 4 * g + r), o1_bank[g, r], -2.0, d_t[g][:, r, :])
+        def finish_1(g, r):
+            finish((1, 4 * g + r), o1_bank[g, r], -2.0, d_t[g][:, r, :])
 
         def store(which, row, count=2, cols=slice(0, H)):
             nc.sync.dma_start(
@@ -365,6 +374,7 @@ def tile_dedicomdecoder_v_kernel(tc, z_i, z_j, w_r, d_w, rz_in, scores, grad_out
         copy_row(2)
         make_dz(UNITS[0], 0)
         stage_g(UNITS[1], 0)
+        matmul_0(0)
         copy_row(3)
         transpose(UNITS[0], (0, 1))
         make_dz(UNITS[0], 1)
@@ -377,80 +387,81 @@ def tile_dedicomdecoder_v_kernel(tc, z_i, z_j, w_r, d_w, rz_in, scores, grad_out
 
         for i in range(1, 5):
             unit, t = UNITS[i], i - 1
-            rows = (2 * t, 2 * t + 1)
             scalar_round(i)
             p_gpsimd(t)
-            matmul_0(rows[0])
-            if t >= 1:
-                for r in range(2):
-                    matmul_1(0, r, [t - 1], "acc%d" % r)
-            matmul_0(rows[1])
-            if t >= 1:
-                for r in range(2, 4):
-                    matmul_1(0, r, [t - 1], "acc%d" % r)
             make_dz(unit, 0)
+            matmul_0(2 * t + 1)
+            finish_0(2 * t)
             stage_g(UNITS[i + 1], 0)
-            for row in rows:
-                finish_0(row)
-            transpose(unit, (0, 1))
             make_dz(unit, 1)
-            transpose(unit, (2, 3))
-            stage_g(UNITS[i + 1], 1)
+            transpose(unit)
+            finish_0(2 * t + 1)
             p_vector(t)
             if t + 2 < NT:
                 load_z_rz(t + 2)
                 load_s(UNITS[i + 3])
             if i == 1:
                 load_g(LAST)
-            quantize_tok(unit)
             quantize_rel(UNITS[i - 1])
+            matmul_0(2 * t + 2)
+            stage_g(UNITS[i + 1], 1)
+            quantize_tok(unit)
             quantize_p(t)
+            for r in range(3):
+                matmul_1(0, r, [t], "acc%d" % r)
         for row in range(0, 8, 2):
             store(0, row)
 
         unit = UNITS[5]
         scalar_round(5)
         regroup(1, nc.gpsimd.tensor_copy)
-        matmul_0(8)
-        matmul_1(0, 0, [LAST])
-        matmul_0(9)
-        for r in range(1, 4):
-            matmul_1(0, r, [LAST])
         make_dz(unit, 0)
-        matmul_0(10, tag="g_bank")
-        for row in (8, 9):
-            finish_0(row)
-        store(0, 8)
-        transpose(unit, (0, 1))
-        make_dz(unit, 1)
-        transpose(unit, (2, 3))
-        finish_1(0, 3, finish_aside)
-        matmul_1(1, 3, (1, 2), "acc3")
+        matmul_1(0, 3, range(NT), "ring_bank")
+        finish_0(8)
+        store(0, 8, 1)
+        matmul_0(9)
         for r in range(3):
             finish_1(0, r)
             matmul_1(1, r, (1, 2), "acc%d" % r)
-        store(1, 0)
-        store(1, 2)
-        matmul_0(11, tag="g_bank")
+            if r == 1:
+                store(1, 0)
+                transpose(unit, (0, 1))
+        store(1, 2, 1)
+        make_dz(unit, 1)
+        transpose(unit, (2, 3))
+        copy_aside(0, 3)
+        matmul_0(10)
+        matmul_0(11)
         for u in range(2):
             copy_out(unit, u, nc.scalar.copy)
-        quantize_tok((0, 1))
         quantize_tok(unit)
-        quantize_rel(UNITS[4])
-        for r in range(4):
-            matmul_1(1, r, (0, LAST))
+        quantize_tok((0, 1))
+        finish_aside(0, 3, shared_stage()[:].bitcast(F32)[:, :H])
+        for r in range(3):
+            matmul_1(1, r, (LAST,))
+        for r in range(3):
+            matmul_1(1, r, (0,))
+        finish_0(9)
+        store(0, 9, 1)
+        matmul_1(1, 3, (1, 2, 0, LAST), "ring_bank")
         for row in (10, 11):
             finish_0(row)
-            matmul_0(row + 2, [0], tag="g_bank")
-        store(0, 10)
-        finish_1(1, 0)
+            store(0, row, 1)
+        store_aside(0, 3, nc.sync)
+        for r in range(2):
+            copy_aside(1, r)
+        quantize_rel(UNITS[4])
+        for row in (12, 13):
+            matmul_0(row, [0])
         quantize_rel(unit)
-        finish_1(1, 1)
-        store(1, 4)
-        matmul_0(12, [1])
-        matmul_0(13, [1])
-        matmul_0(14)
-        matmul_0(15)
+        for row in (12, 13):
+            matmul_0(row, [1])
+        for row in (14, 15):
+            matmul_0(row, tag="tr_bank")
+        for r in range(2):
+            held = ring.tile([P, 2048], BF16, name="rel", align_bytes=64)
+            finish_aside(1, r, held[:].bitcast(F32)[:, :H])
+            store_aside(1, r, nc.scalar)
         for r in (2, 3):
             finish_1(1, r)
             store(1, 4 + r, 1)

@@ -23,6 +23,7 @@ NG = R // 512
 LAST = NT - 1
 UNITS = [(t, g) for t in range(1, NT) for g in range(NG)]
 GPSIMD_COLS = 224
+RING = 3
 
 
 def tile_dedicomdecoder_v_kernel(tc, z_i, z_j, w_r, d_w, rz_in, scores, grad_out, out_0, out_1):
@@ -53,9 +54,13 @@ def tile_dedicomdecoder_v_kernel(tc, z_i, z_j, w_r, d_w, rz_in, scores, grad_out
         def load_s(unit):
             t, g = unit
             s_t[unit] = ring.tile([P, 4, 512], F32, name="s_in", bufs=5)
-            nc.sync.dma_start(out=s_t[unit][:], in_=four_rows(scores, t)[:, :, 512 * g : 512 * (g + 1)])
+            src = four_rows(scores, t)[:, :, 512 * g : 512 * (g + 1)]
             for u in range(2):
                 s_at[unit, u] = s_t[unit][:, 2 * u : 2 * u + 2, :]
+                if unit == UNITS[-1]:
+                    nc.sync.dma_start(out=s_at[unit, u], in_=src[:, 2 * u : 2 * u + 2, :])
+            if unit != UNITS[-1]:
+                nc.sync.dma_start(out=s_t[unit][:], in_=src)
 
         def load_g(t):
             g_t[t] = ring.tile([P, 4, R], BF16, name="g_in")
@@ -95,8 +100,17 @@ def tile_dedicomdecoder_v_kernel(tc, z_i, z_j, w_r, d_w, rz_in, scores, grad_out
 
         tok_t, rel_t, tr_bank, x_t, g_bank, p_t = {}, {}, {}, {}, {}, {}
 
+        ring_uses = []
+
+        def next_in_ring():
+            ring_uses.append("ring_bank%d" % (len(ring_uses) % RING))
+            return ring_uses[-1]
+
         def shared_stage():
             return keep.tile([P, 2048], BF16, name="shared_stage", align_bytes=64)
+
+        def rel_stage():
+            return ring.tile([P, 2048], BF16, name="rel", align_bytes=64)
 
         def make_d2(g):
             tok_t["d", g] = shared_stage()
@@ -127,16 +141,16 @@ def tile_dedicomdecoder_v_kernel(tc, z_i, z_j, w_r, d_w, rz_in, scores, grad_out
             )
 
         def transpose_row(j):
-            tr_bank[0, j] = psum.tile([P, NG, 2, P], F32, name="tr_bank", bufs=2)
+            tr_bank[0, j] = psum.tile([P, NG, 2, P], F32, name="tr_bank%d" % (j % 2))
             words = dz_rows[:, j, :].bitcast(F32)
             for g in range(NG):
                 for h in range(2):
                     nc.tensor.transpose(tr_bank[0, j][:, g, h, :], words[:, 256 * g + h : 256 * (g + 1) : 2], ident[:])
 
-        def copy_row(j):
+        def copy_row(j, copy):
             if j % 2 == 0:
-                rel_t[0, j // 2] = ring.tile([P, 2048], BF16, name="rel", align_bytes=64)
-            nc.vector.tensor_copy(
+                rel_t[0, j // 2] = rel_stage()
+            copy(
                 out=rel_t[0, j // 2][:, 1024 * (j % 2) : 1024 * (j % 2 + 1)]
                 .bitcast(F32)
                 .rearrange("q (g p h) -> q g p h", g=NG, h=2),
@@ -157,12 +171,9 @@ def tile_dedicomdecoder_v_kernel(tc, z_i, z_j, w_r, d_w, rz_in, scores, grad_out
         def tanh(unit, u):
             if u == 0:
                 x_t[unit] = ring.tile([P, 2, 2, P, 2, 2], F32, name="x_half")
-            nc.scalar.activation(
-                out=x_t[unit][:, u].rearrange("p h q b e -> p q h b e"),
-                in_=s_at[unit, u].rearrange("p e (q h b) -> p q h b e", h=2, b=2),
-                func=ACT.Tanh,
-                scale=0.5,
-            )
+            pairs = s_at[unit, u].rearrange("p e (q h b) -> p h q b e", h=2, b=2)
+            for h in range(2):
+                nc.scalar.activation(out=x_t[unit][:, u, h], in_=pairs[:, h], func=ACT.Tanh, scale=0.5)
 
         def squares(unit, h):
             return s_at[unit, h].rearrange("p b (q j) -> p b q j", j=4)
@@ -182,15 +193,12 @@ def tile_dedicomdecoder_v_kernel(tc, z_i, z_j, w_r, d_w, rz_in, scores, grad_out
                 square(unit, h)
 
         def scalar_round(i):
-            for u in range(2):
-                tanh(UNITS[i], u)
-            square(UNITS[i], 0)
+            activate(UNITS[i])
             for u in range(2):
                 copy_out(UNITS[i - 1], u, nc.scalar.copy)
-            square(UNITS[i], 1)
 
         def stage_g(unit, h):
-            g_bank[unit, h] = psum.tile([P, 4, P, 2], BF16, name="ring_bank", bufs=3)
+            g_bank[unit, h] = psum.tile([P, 4, P, 2], BF16, name=next_in_ring())
             pairs = g_t[unit[0]][:, :, group(unit)].rearrange("p j (q h b) -> p j h q b", h=2, b=2)
             for u in range(2):
                 nc.tensor.matmul(
@@ -214,17 +222,17 @@ def tile_dedicomdecoder_v_kernel(tc, z_i, z_j, w_r, d_w, rz_in, scores, grad_out
                     op1=ALU.mult,
                 )
 
-        def transpose(unit, places=range(4)):
+        def transpose(unit, halves=range(2), places=range(4)):
             words = tok_t[unit][:].bitcast(F32).rearrange("p (t q u) -> p t u q", t=4, u=2)
-            for u in range(2):
+            for u in halves:
                 if 0 in places:
-                    tr_bank[unit, u] = psum.tile([P, 4, P], F32, name="tr_bank", bufs=2)
+                    tr_bank[unit, u] = psum.tile([P, 4, P], F32, name="tr_bank%d" % u)
                 for t in places:
                     nc.tensor.transpose(tr_bank[unit, u][:, t, :], words[:, t, u, :], ident[:])
 
         def copy_out(unit, u, copy):
             if u == 0:
-                rel_t[unit] = ring.tile([P, 2048], BF16, name="rel", align_bytes=64)
+                rel_t[unit] = rel_stage()
             copy(
                 out=rel_t[unit][:, 1024 * u : 1024 * (u + 1)].rearrange("q (e p t) -> q e p t", e=2, t=4),
                 in_=tr_bank[unit, u][:].bitcast(BF16).rearrange("q t (p e) -> q e p t", e=2),
@@ -272,9 +280,9 @@ def tile_dedicomdecoder_v_kernel(tc, z_i, z_j, w_r, d_w, rz_in, scores, grad_out
         o0_bank, o1_bank, o1_done, out_t = {}, {}, {}, {}
 
         def new_bank(tag):
-            return psum.tile([P, H], F32, name=tag, bufs={"tr_bank": 2, "ring_bank": 3}.get(tag, 1))
+            return psum.tile([P, H], F32, name=tag or next_in_ring())
 
-        def matmul_0(row, groups=range(NG), tag="ring_bank"):
+        def matmul_0(row, groups=range(NG), tag=None):
             t, j = divmod(row, 4)
             for g in groups:
                 if g == 0:
@@ -310,15 +318,24 @@ def tile_dedicomdecoder_v_kernel(tc, z_i, z_j, w_r, d_w, rz_in, scores, grad_out
 
         aside_t = {}
 
-        def copy_aside(g, r):
-            nc.scalar.mul(out=out_row(1, 4 * g + r), in_=o1_bank[g, r][:], mul=-2.0)
+        def final_of(key):
+            which, row = key
+            if which == 0:
+                return o0_bank[row], -1.0, rz_t[row // 4][:, row % 4, :]
+            return o1_bank[divmod(row, 4)], -2.0, d_t[row // 4][:, row % 4, :]
 
-        def finish_aside(g, r, held):
-            aside_t[g, r] = held
-            nc.gpsimd.tensor_tensor(out=held, in0=out_row(1, 4 * g + r), in1=d_t[g][:, r, :], op=ALU.mult)
+        def copy_aside(key):
+            bank, factor, other = final_of(key)
+            nc.scalar.mul(out=out_row(*key), in_=bank[:], mul=factor)
 
-        def store_aside(g, r, queue):
-            queue.dma_start(out=four_rows(out_1, g)[:, r, :], in_=aside_t[g, r])
+        def finish_aside(key, held=None):
+            bank, factor, other = final_of(key)
+            aside_t[key] = out_row(*key) if held is None else held[:].bitcast(F32)[:, :H]
+            nc.gpsimd.tensor_tensor(out=aside_t[key], in0=out_row(*key), in1=other, op=ALU.mult)
+
+        def store_aside(key, queue):
+            which, row = key
+            queue.dma_start(out=four_rows((out_0, out_1)[which], row // 4)[:, row % 4, :], in_=aside_t[key])
 
         def finish_0(row, cols=slice(0, H)):
             finish((0, row), o0_bank[row], -1.0, rz_t[row // 4][:, row % 4, :], cols)
@@ -339,46 +356,50 @@ def tile_dedicomdecoder_v_kernel(tc, z_i, z_j, w_r, d_w, rz_in, scores, grad_out
         load_s_row(2)
         load_g_rows(1)
         load_s_row(3)
-        load_s(UNITS[0])
         load_d(1)
+        load_s(UNITS[0])
         load_g(1)
         load_s(UNITS[1])
         load_z_rz(0)
         load_s(UNITS[2])
-        make_d2(0)
-        for j in range(4):
+
+        def activate_both(j):
             for func in (ACT.Tanh, ACT.Square):
                 activate_row(func, j, slice(0, 512))
                 activate_row(func, j, slice(512, R))
-        activate(UNITS[0])
+
+        make_d2(0)
+        for j in range(3):
+            activate_both(j)
         dz_row(0)
         transpose_row(0)
         quantize_d2(0)
         dz_row(1)
         transpose_row(1)
-        copy_row(0)
+        copy_row(0, nc.scalar.copy)
+        activate_both(3)
+        copy_row(1, nc.scalar.copy)
+        activate(UNITS[0])
         dz_row(2)
         transpose_row(2)
-        copy_row(1)
+        make_d2(1)
         dz_row(3)
         transpose_row(3)
-        make_d2(1)
         for h in range(2):
             stage_g(UNITS[0], h)
         load_g(2)
         load_z_rz(1)
         load_s(UNITS[3])
-        quantize_rel((0, 0))
         quantize_d2(1)
         regroup(0, nc.gpsimd.tensor_copy, slice(0, 3))
-        copy_row(2)
+        quantize_rel((0, 0))
+        copy_row(2, nc.vector.tensor_copy)
+        copy_row(3, nc.vector.tensor_copy)
         make_dz(UNITS[0], 0)
         stage_g(UNITS[1], 0)
         matmul_0(0)
-        copy_row(3)
-        transpose(UNITS[0], (0, 1))
         make_dz(UNITS[0], 1)
-        transpose(UNITS[0], (2, 3))
+        transpose(UNITS[0])
         stage_g(UNITS[1], 1)
         regroup(0, nc.vector.tensor_copy, slice(3, 4))
         quantize_tok(UNITS[0])
@@ -392,9 +413,11 @@ def tile_dedicomdecoder_v_kernel(tc, z_i, z_j, w_r, d_w, rz_in, scores, grad_out
             make_dz(unit, 0)
             matmul_0(2 * t + 1)
             finish_0(2 * t)
-            stage_g(UNITS[i + 1], 0)
             make_dz(unit, 1)
             transpose(unit)
+            if t == LAST:
+                break
+            stage_g(UNITS[i + 1], 0)
             finish_0(2 * t + 1)
             p_vector(t)
             if t + 2 < NT:
@@ -409,62 +432,70 @@ def tile_dedicomdecoder_v_kernel(tc, z_i, z_j, w_r, d_w, rz_in, scores, grad_out
             quantize_p(t)
             for r in range(3):
                 matmul_1(0, r, [t], "acc%d" % r)
+        matmul_1(0, 3, range(LAST))
+        stage_g(UNITS[5], 0)
+        finish_0(7)
+        stage_g(UNITS[5], 1)
+        p_vector(LAST)
+        quantize_tok(unit)
+        quantize_p(LAST)
+        quantize_rel(UNITS[3])
+        for r in (3, 0, 1, 2):
+            matmul_1(0, r, [LAST])
         for row in range(0, 8, 2):
             store(0, row)
 
         unit = UNITS[5]
-        scalar_round(5)
+        bank_a, bank_b, bank_c = ring_uses[-3:]
+        activate(unit)
         regroup(1, nc.gpsimd.tensor_copy)
-        make_dz(unit, 0)
-        matmul_1(0, 3, range(NT), "ring_bank")
-        finish_0(8)
-        store(0, 8, 1)
-        matmul_0(9)
+        finish_1(0, 3)
+        store(1, 3, 1)
+        matmul_0(8, tag=bank_a)
+        copy_aside((0, 8))
+        for u in range(2):
+            copy_out(UNITS[4], u, nc.scalar.copy)
+        finish_aside((0, 8))
         for r in range(3):
             finish_1(0, r)
+            store(1, r, 1)
             matmul_1(1, r, (1, 2), "acc%d" % r)
-            if r == 1:
-                store(1, 0)
-                transpose(unit, (0, 1))
-        store(1, 2, 1)
+        matmul_0(9, tag=bank_a)
+        make_dz(unit, 0)
+        matmul_0(10, tag=bank_b)
+        transpose(unit, [0], (0, 1))
         make_dz(unit, 1)
-        transpose(unit, (2, 3))
-        copy_aside(0, 3)
-        matmul_0(10)
-        matmul_0(11)
-        for u in range(2):
-            copy_out(unit, u, nc.scalar.copy)
-        quantize_tok(unit)
-        quantize_tok((0, 1))
-        finish_aside(0, 3, shared_stage()[:].bitcast(F32)[:, :H])
-        for r in range(3):
-            matmul_1(1, r, (LAST,))
-        for r in range(3):
-            matmul_1(1, r, (0,))
+        transpose(unit, [0], (2, 3))
+        transpose(unit, [1])
+        matmul_0(11, tag=bank_c)
+        copy_out(unit, 0, nc.scalar.copy)
+        copy_aside((0, 11))
+        copy_out(unit, 1, nc.scalar.copy)
         finish_0(9)
         store(0, 9, 1)
-        matmul_1(1, 3, (1, 2, 0, LAST), "ring_bank")
-        for row in (10, 11):
-            finish_0(row)
-            store(0, row, 1)
-        store_aside(0, 3, nc.sync)
-        for r in range(2):
-            copy_aside(1, r)
+        finish_0(10)
+        store(0, 8, 1)
+        store(0, 10, 1)
+        quantize_tok((0, 1))
+        quantize_tok(unit)
         quantize_rel(UNITS[4])
-        for row in (12, 13):
-            matmul_0(row, [0])
+        finish_aside((0, 11), rel_stage())
+        for r in range(3):
+            matmul_1(1, r, (0, LAST))
+        matmul_1(1, 3, (1, 2, 0, LAST), bank_a)
+        matmul_0(12, [0], bank_b)
+        matmul_0(13, [0], "tr_bank0")
+        for r in range(3):
+            finish_1(1, r)
+            store(1, 4 + r, 1)
+        store_aside((0, 11), nc.sync)
         quantize_rel(unit)
         for row in (12, 13):
             matmul_0(row, [1])
-        for row in (14, 15):
-            matmul_0(row, tag="tr_bank")
-        for r in range(2):
-            held = ring.tile([P, 2048], BF16, name="rel", align_bytes=64)
-            finish_aside(1, r, held[:].bitcast(F32)[:, :H])
-            store_aside(1, r, nc.scalar)
-        for r in (2, 3):
-            finish_1(1, r)
-            store(1, 4 + r, 1)
+        matmul_0(14, tag=bank_c)
+        matmul_0(15, tag="tr_bank1")
+        finish_1(1, 3)
+        store(1, 7, 1)
         for row in range(12, 15):
             finish_0(row)
             store(0, row, 1)

@@ -22,7 +22,7 @@ NT = B // 512
 NG = R // 512
 LAST = NT - 1
 UNITS = [(t, g) for t in range(1, NT) for g in range(NG)]
-GPSIMD_COLS = 224
+GPSIMD_COLS = 208
 RING = 3
 
 
@@ -198,11 +198,11 @@ def tile_dedicomdecoder_v_kernel(tc, z_i, z_j, w_r, d_w, rz_in, scores, grad_out
                 copy_out(UNITS[i - 1], u, nc.scalar.copy)
 
         def stage_g(unit, h):
-            g_bank[unit, h] = psum.tile([P, 4, P, 2], BF16, name=next_in_ring())
+            g_bank[unit, h] = psum.tile([P, P, 4, 2], BF16, name=next_in_ring())
             pairs = g_t[unit[0]][:, :, group(unit)].rearrange("p j (q h b) -> p j h q b", h=2, b=2)
             for u in range(2):
                 nc.tensor.matmul(
-                    out=g_bank[unit, h][:, 2 * u : 2 * u + 2],
+                    out=g_bank[unit, h][:].rearrange("p q j b -> p j q b")[:, 2 * u : 2 * u + 2],
                     lhsT=ident_bf[:],
                     rhs=pairs[:, 2 * u : 2 * u + 2, h],
                     start=True,
@@ -212,15 +212,14 @@ def tile_dedicomdecoder_v_kernel(tc, z_i, z_j, w_r, d_w, rz_in, scores, grad_out
         def make_dz(unit, h):
             if unit not in tok_t:
                 tok_t[unit] = ring.tile([P, 2048], BF16, name="tok", bufs=3, align_bytes=64)
-            for b in range(2):
-                nc.vector.scalar_tensor_tensor(
-                    out=tok_t[unit][:].rearrange("p (t q j) -> p t q j", t=4, j=4)[:, 2 * h + b],
-                    in0=squares(unit, h)[:, b],
-                    scalar=0.25,
-                    in1=g_bank[unit, h][:, :, :, b].rearrange("p j q -> p q j"),
-                    op0=ALU.subtract,
-                    op1=ALU.mult,
-                )
+            nc.vector.scalar_tensor_tensor(
+                out=tok_t[unit][:, 1024 * h : 1024 * (h + 1)].rearrange("p (b n) -> p b n", b=2),
+                in0=squares(unit, h).rearrange("p b q j -> p b (q j)"),
+                scalar=0.25,
+                in1=g_bank[unit, h][:].rearrange("p q j b -> p b (q j)"),
+                op0=ALU.subtract,
+                op1=ALU.mult,
+            )
 
         def transpose(unit, halves=range(2), places=range(4)):
             words = tok_t[unit][:].bitcast(F32).rearrange("p (t q u) -> p t u q", t=4, u=2)

@@ -62,9 +62,20 @@ def tile_dedicomdecoder_v_kernel(tc, z_i, z_j, w_r, d_w, rz_in, scores, grad_out
             if unit != UNITS[-1]:
                 nc.sync.dma_start(out=s_t[unit][:], in_=src)
 
+        g_at = {}
+
         def load_g(t):
             g_t[t] = ring.tile([P, 4, R], BF16, name="g_in")
             nc.sync.dma_start(out=g_t[t][:], in_=four_rows(grad_out, t))
+            for g in range(NG):
+                g_at[t, g] = g_t[t][:, :, 512 * g : 512 * (g + 1)]
+
+        def load_g_unit(unit):
+            t, g = unit
+            if g == 0:
+                g_t[t] = ring.tile([P, NG, 4, 512], BF16, name="g_in")
+            g_at[unit] = g_t[t][:, g]
+            nc.sync.dma_start(out=g_at[unit], in_=four_rows(grad_out, t)[:, :, 512 * g : 512 * (g + 1)])
 
         def load_d(g):
             d_t[g] = keep.tile([P, 4, H], BF16, name="d_rows%d" % g)
@@ -165,9 +176,6 @@ def tile_dedicomdecoder_v_kernel(tc, z_i, z_j, w_r, d_w, rz_in, scores, grad_out
                 in_=dz_rows[:, :, 512 * g : 512 * (g + 1)].rearrange("p j (q t) -> p t q j", t=4)[:, places],
             )
 
-        def group(unit):
-            return slice(512 * unit[1], 512 * (unit[1] + 1))
-
         def tanh(unit, u):
             if u == 0:
                 x_t[unit] = ring.tile([P, 2, 2, P, 2, 2], F32, name="x_half")
@@ -199,7 +207,7 @@ def tile_dedicomdecoder_v_kernel(tc, z_i, z_j, w_r, d_w, rz_in, scores, grad_out
 
         def stage_g(unit, h):
             g_bank[unit, h] = psum.tile([P, P, 4, 2], BF16, name=next_in_ring())
-            pairs = g_t[unit[0]][:, :, group(unit)].rearrange("p j (q h b) -> p j h q b", h=2, b=2)
+            pairs = g_at[unit].rearrange("p j (q h b) -> p j h q b", h=2, b=2)
             for u in range(2):
                 nc.tensor.matmul(
                     out=g_bank[unit, h][:].rearrange("p q j b -> p j q b")[:, 2 * u : 2 * u + 2],
@@ -422,8 +430,7 @@ def tile_dedicomdecoder_v_kernel(tc, z_i, z_j, w_r, d_w, rz_in, scores, grad_out
             if t + 2 < NT:
                 load_z_rz(t + 2)
                 load_s(UNITS[i + 3])
-            if i == 1:
-                load_g(LAST)
+                load_g_unit(UNITS[i + 3])
             quantize_rel(UNITS[i - 1])
             matmul_0(2 * t + 2)
             stage_g(UNITS[i + 1], 1)

@@ -24,6 +24,7 @@ LAST = NT - 1
 UNITS = [(t, g) for t in range(1, NT) for g in range(NG)]
 GPSIMD_COLS = 208
 RING = 3
+SHARED_ROUND = 2
 
 
 def tile_dedicomdecoder_v_kernel(tc, z_i, z_j, w_r, d_w, rz_in, scores, grad_out, out_0, out_1):
@@ -202,7 +203,7 @@ def tile_dedicomdecoder_v_kernel(tc, z_i, z_j, w_r, d_w, rz_in, scores, grad_out
 
         def scalar_round(i):
             activate(UNITS[i])
-            for u in range(2):
+            for u in range(1 if i == SHARED_ROUND else 2):
                 copy_out(UNITS[i - 1], u, nc.scalar.copy)
 
         def stage_g(unit, h):
@@ -233,16 +234,16 @@ def tile_dedicomdecoder_v_kernel(tc, z_i, z_j, w_r, d_w, rz_in, scores, grad_out
             words = tok_t[unit][:].bitcast(F32).rearrange("p (t q u) -> p t u q", t=4, u=2)
             for u in halves:
                 if 0 in places:
-                    tr_bank[unit, u] = psum.tile([P, 4, P], F32, name="tr_bank%d" % u)
+                    tr_bank[unit, u] = psum.tile([P, P, 4], F32, name="tr_bank%d" % u)
                 for t in places:
-                    nc.tensor.transpose(tr_bank[unit, u][:, t, :], words[:, t, u, :], ident[:])
+                    nc.tensor.transpose(tr_bank[unit, u][:, :, t], words[:, t, u, :], ident[:])
 
         def copy_out(unit, u, copy):
             if u == 0:
                 rel_t[unit] = rel_stage()
             copy(
-                out=rel_t[unit][:, 1024 * u : 1024 * (u + 1)].rearrange("q (e p t) -> q e p t", e=2, t=4),
-                in_=tr_bank[unit, u][:].bitcast(BF16).rearrange("q t (p e) -> q e p t", e=2),
+                out=rel_t[unit][:, 1024 * u : 1024 * (u + 1)].rearrange("q (e n) -> q e n", e=2),
+                in_=tr_bank[unit, u][:].rearrange("q p t -> q (p t)").bitcast(BF16).rearrange("q (n e) -> q e n", e=2),
             )
 
         def quantize_tok(unit):
@@ -417,6 +418,8 @@ def tile_dedicomdecoder_v_kernel(tc, z_i, z_j, w_r, d_w, rz_in, scores, grad_out
             unit, t = UNITS[i], i - 1
             scalar_round(i)
             p_gpsimd(t)
+            if i == SHARED_ROUND:
+                copy_out(UNITS[i - 1], 1, nc.vector.tensor_copy)
             make_dz(unit, 0)
             matmul_0(2 * t + 1)
             finish_0(2 * t)

@@ -22,9 +22,9 @@ NT = B // 512
 NG = R // 512
 LAST = NT - 1
 UNITS = [(t, g) for t in range(1, NT) for g in range(NG)]
-GPSIMD_COLS = 208
+GPSIMD_COLS = [352, 304, 304, 304]
 RING = 3
-SHARED_ROUND = 2
+ROWS = [range(0, 2), range(2, 5), range(5, 8), range(8, 12)]
 
 
 def tile_dedicomdecoder_v_kernel(tc, z_i, z_j, w_r, d_w, rz_in, scores, grad_out, out_0, out_1):
@@ -40,30 +40,38 @@ def tile_dedicomdecoder_v_kernel(tc, z_i, z_j, w_r, d_w, rz_in, scores, grad_out
 
         s_t, g_t, z_t, rz_t, d_t = {}, {}, {}, {}, {}
 
+        def new_s(t, u):
+            s_t[t, u] = ring.tile([P, 2, R], F32, name="s_in", bufs=5)
+
         def load_s_row(j):
             if j % 2 == 0:
-                s_t[0, j // 2] = ring.tile([P, 2, R], F32, name="s_in", bufs=5)
+                new_s(0, j // 2)
             nc.sync.dma_start(out=s_t[0, j // 2][:, j % 2, :], in_=four_rows(scores, 0)[:, j, :])
+
+        s_at, g_at = {}, {}
+
+        def load_s_pair(t, u):
+            new_s(t, u)
+            nc.sync.dma_start(out=s_t[t, u][:], in_=four_rows(scores, t)[:, 2 * u : 2 * u + 2, :])
+            for g in range(NG):
+                s_at[(t, g), u] = s_t[t, u][:, :, 512 * g : 512 * (g + 1)]
+
+        def load_s_unit(unit, pieces=1):
+            t, g = unit
+            s_t[unit] = ring.tile([P, 4, 512], F32, name="s_in", bufs=5)
+            rows = 4 // pieces
+            for lo in range(0, 4, rows):
+                nc.sync.dma_start(
+                    out=s_t[unit][:, lo : lo + rows, :],
+                    in_=four_rows(scores, t)[:, lo : lo + rows, 512 * g : 512 * (g + 1)],
+                )
+            for u in range(2):
+                s_at[unit, u] = s_t[unit][:, 2 * u : 2 * u + 2, :]
 
         def load_g_rows(u):
             if u == 0:
                 g_t[0] = ring.tile([P, 4, R], BF16, name="g_in")
             nc.sync.dma_start(out=g_t[0][:, 2 * u : 2 * u + 2, :], in_=four_rows(grad_out, 0)[:, 2 * u : 2 * u + 2, :])
-
-        s_at = {}
-
-        def load_s(unit):
-            t, g = unit
-            s_t[unit] = ring.tile([P, 4, 512], F32, name="s_in", bufs=5)
-            src = four_rows(scores, t)[:, :, 512 * g : 512 * (g + 1)]
-            for u in range(2):
-                s_at[unit, u] = s_t[unit][:, 2 * u : 2 * u + 2, :]
-                if unit == UNITS[-1]:
-                    nc.sync.dma_start(out=s_at[unit, u], in_=src[:, 2 * u : 2 * u + 2, :])
-            if unit != UNITS[-1]:
-                nc.sync.dma_start(out=s_t[unit][:], in_=src)
-
-        g_at = {}
 
         def load_g(t):
             g_t[t] = ring.tile([P, 4, R], BF16, name="g_in")
@@ -103,12 +111,15 @@ def tile_dedicomdecoder_v_kernel(tc, z_i, z_j, w_r, d_w, rz_in, scores, grad_out
                 codes[key] = keep.tile([P, 512], U32, name="code_%s%d%d" % key, align_bytes=64)
                 scales[key] = keep.tile([P, 512], U8, name="scale_%s%d%d" % key, align_bytes=64)
 
-        def quantize(key, staged, fmt):
-            new_codes(key)
-            nc.vector.quantize_mx(out=codes[key][:].bitcast(fmt), scales=scales[key][:], in_=staged[:])
+        def quantize(key, staged, fmt, lo=0, hi=512):
+            if key not in codes:
+                new_codes(key)
+            nc.vector.quantize_mx(
+                out=codes[key][:, lo:hi].bitcast(fmt), scales=scales[key][:, lo:hi], in_=staged[:, 4 * lo : 4 * hi]
+            )
 
-        def by_two(ap):
-            return ap.rearrange("p j (c i) -> p c j i", i=2)
+        def by_cols(ap, n=2):
+            return ap.rearrange("p j (c i) -> p c j i", i=n)
 
         tok_t, rel_t, tr_bank, x_t, g_bank, p_t = {}, {}, {}, {}, {}, {}
 
@@ -127,9 +138,9 @@ def tile_dedicomdecoder_v_kernel(tc, z_i, z_j, w_r, d_w, rz_in, scores, grad_out
         def make_d2(g):
             tok_t["d", g] = shared_stage()
             nc.vector.tensor_tensor(
-                out=by_two(tok_t["d", g][:].rearrange("p (c j) -> p j c", j=4)),
-                in0=by_two(d_t[g][:]),
-                in1=by_two(d_t[g][:]),
+                out=by_cols(tok_t["d", g][:].rearrange("p (c j) -> p j c", j=4)),
+                in0=by_cols(d_t[g][:]),
+                in1=by_cols(d_t[g][:]),
                 op=ALU.mult,
             )
 
@@ -138,9 +149,11 @@ def tile_dedicomdecoder_v_kernel(tc, z_i, z_j, w_r, d_w, rz_in, scores, grad_out
 
         dz_rows = keep.tile([P, 4, R], BF16, name="dz_rows")
 
-        def activate_row(func, j, cols=slice(None)):
-            s = s_t[0, j // 2][:, j % 2, cols]
-            nc.scalar.activation(out=s, in_=s, func=func, scale=0.5)
+        def activate_row(j):
+            for func in (ACT.Tanh, ACT.Square):
+                for cols in (slice(0, 512), slice(512, R)):
+                    s = s_t[0, j // 2][:, j % 2, cols]
+                    nc.scalar.activation(out=s, in_=s, func=func, scale=0.5)
 
         def dz_row(j):
             nc.vector.scalar_tensor_tensor(
@@ -169,12 +182,13 @@ def tile_dedicomdecoder_v_kernel(tc, z_i, z_j, w_r, d_w, rz_in, scores, grad_out
                 in_=tr_bank[0, j][:].rearrange("q g h p -> q g p h"),
             )
 
-        def regroup(g, copy, places=slice(0, 4)):
+        def regroup(g, copy, places=range(4)):
             if (0, g) not in tok_t:
                 tok_t[0, g] = shared_stage()
+            at = slice(places.start, places.stop)
             copy(
-                out=tok_t[0, g][:].rearrange("p (t q j) -> p t q j", t=4, j=4)[:, places],
-                in_=dz_rows[:, :, 512 * g : 512 * (g + 1)].rearrange("p j (q t) -> p t q j", t=4)[:, places],
+                out=tok_t[0, g][:].rearrange("p (t q j) -> p t q j", t=4, j=4)[:, at],
+                in_=dz_rows[:, :, 512 * g : 512 * (g + 1)].rearrange("p j (q t) -> p t q j", t=4)[:, at],
             )
 
         def tanh(unit, u):
@@ -195,19 +209,8 @@ def tile_dedicomdecoder_v_kernel(tc, z_i, z_j, w_r, d_w, rz_in, scores, grad_out
                 scale=0.5,
             )
 
-        def activate(unit):
-            for u in range(2):
-                tanh(unit, u)
-            for h in range(2):
-                square(unit, h)
-
-        def scalar_round(i):
-            activate(UNITS[i])
-            for u in range(1 if i == SHARED_ROUND else 2):
-                copy_out(UNITS[i - 1], u, nc.scalar.copy)
-
-        def stage_g(unit, h):
-            g_bank[unit, h] = psum.tile([P, P, 4, 2], BF16, name=next_in_ring())
+        def stage_g(unit, h, tag=None):
+            g_bank[unit, h] = psum.tile([P, P, 4, 2], BF16, name=tag or next_in_ring())
             pairs = g_at[unit].rearrange("p j (q h b) -> p j h q b", h=2, b=2)
             for u in range(2):
                 nc.tensor.matmul(
@@ -239,7 +242,7 @@ def tile_dedicomdecoder_v_kernel(tc, z_i, z_j, w_r, d_w, rz_in, scores, grad_out
                     nc.tensor.transpose(tr_bank[unit, u][:, :, t], words[:, t, u, :], ident[:])
 
         def copy_out(unit, u, copy):
-            if u == 0:
+            if unit not in rel_t:
                 rel_t[unit] = rel_stage()
             copy(
                 out=rel_t[unit][:, 1024 * u : 1024 * (u + 1)].rearrange("q (e n) -> q e n", e=2),
@@ -249,27 +252,23 @@ def tile_dedicomdecoder_v_kernel(tc, z_i, z_j, w_r, d_w, rz_in, scores, grad_out
         def quantize_tok(unit):
             quantize(("tok",) + unit, tok_t[unit], E5M2)
 
-        def quantize_rel(unit):
-            quantize(("rel",) + unit, rel_t[unit], E5M2)
+        def quantize_rel(unit, lo=0, hi=512):
+            quantize(("rel",) + unit, rel_t[unit], E5M2, lo, hi)
+
+        def make_p(t, engine, cols, n):
+            engine.tensor_tensor(
+                out=by_cols(p_t[t][:].rearrange("p (c j) -> p j c", j=4)[:, :, cols], n),
+                in0=by_cols(z_t[t][:, :, cols], n),
+                in1=by_cols(rz_t[t][:, :, cols], n),
+                op=ALU.mult,
+            )
 
         def p_gpsimd(t):
             p_t[t] = shared_stage()
-            cols = slice(0, GPSIMD_COLS)
-            nc.gpsimd.tensor_tensor(
-                out=by_two(p_t[t][:].rearrange("p (c j) -> p j c", j=4)[:, :, cols]),
-                in0=by_two(z_t[t][:, :, cols]),
-                in1=by_two(rz_t[t][:, :, cols]),
-                op=ALU.mult,
-            )
+            make_p(t, nc.gpsimd, slice(0, GPSIMD_COLS[t]), 4)
 
         def p_vector(t):
-            cols = slice(GPSIMD_COLS, H)
-            nc.vector.tensor_tensor(
-                out=by_two(p_t[t][:].rearrange("p (c j) -> p j c", j=4)[:, :, cols]),
-                in0=by_two(z_t[t][:, :, cols]),
-                in1=by_two(rz_t[t][:, :, cols]),
-                op=ALU.mult,
-            )
+            make_p(t, nc.vector, slice(GPSIMD_COLS[t], H), 2)
 
         def quantize_p(t):
             quantize(("p", t, 0), p_t[t], E4M3)
@@ -314,7 +313,14 @@ def tile_dedicomdecoder_v_kernel(tc, z_i, z_j, w_r, d_w, rz_in, scores, grad_out
                 out_t[which, row // 2] = ring.tile([P, 2, H], F32, name="out_rows", bufs=7)
             return out_t[which, row // 2][:, row % 2, :]
 
-        def finish(key, bank, factor, other, cols=slice(0, H)):
+        def final_of(key):
+            which, row = key
+            if which == 0:
+                return o0_bank[row], -1.0, rz_t[row // 4][:, row % 4, :]
+            return o1_bank[divmod(row, 4)], -2.0, d_t[row // 4][:, row % 4, :]
+
+        def finish(key, cols=slice(0, H)):
+            bank, factor, other = final_of(key)
             nc.vector.scalar_tensor_tensor(
                 out=out_row(*key)[:, cols],
                 in0=bank[:, cols],
@@ -326,12 +332,6 @@ def tile_dedicomdecoder_v_kernel(tc, z_i, z_j, w_r, d_w, rz_in, scores, grad_out
 
         aside_t = {}
 
-        def final_of(key):
-            which, row = key
-            if which == 0:
-                return o0_bank[row], -1.0, rz_t[row // 4][:, row % 4, :]
-            return o1_bank[divmod(row, 4)], -2.0, d_t[row // 4][:, row % 4, :]
-
         def copy_aside(key):
             bank, factor, other = final_of(key)
             nc.scalar.mul(out=out_row(*key), in_=bank[:], mul=factor)
@@ -341,21 +341,23 @@ def tile_dedicomdecoder_v_kernel(tc, z_i, z_j, w_r, d_w, rz_in, scores, grad_out
             aside_t[key] = out_row(*key) if held is None else held[:].bitcast(F32)[:, :H]
             nc.gpsimd.tensor_tensor(out=aside_t[key], in0=out_row(*key), in1=other, op=ALU.mult)
 
-        def store_aside(key, queue):
+        def store_aside(key):
             which, row = key
-            queue.dma_start(out=four_rows((out_0, out_1)[which], row // 4)[:, row % 4, :], in_=aside_t[key])
+            nc.sync.dma_start(out=four_rows((out_0, out_1)[which], row // 4)[:, row % 4, :], in_=aside_t[key])
 
-        def finish_0(row, cols=slice(0, H)):
-            finish((0, row), o0_bank[row], -1.0, rz_t[row // 4][:, row % 4, :], cols)
-
-        def finish_1(g, r):
-            finish((1, 4 * g + r), o1_bank[g, r], -2.0, d_t[g][:, r, :])
-
-        def store(which, row, count=2, cols=slice(0, H)):
+        def store(which, row, count=1, cols=slice(0, H)):
             nc.sync.dma_start(
                 out=four_rows((out_0, out_1)[which], row // 4)[:, row % 4 : row % 4 + count, cols],
                 in_=out_t[which, row // 2][:, row % 2 : row % 2 + count, cols],
             )
+
+        def scalar_unit(i, halves=range(2)):
+            for u in range(2):
+                tanh(UNITS[i], u)
+            for w in range(2):
+                square(UNITS[i], w)
+            for u in halves:
+                copy_out(UNITS[i - 1], u, nc.scalar.copy)
 
         load_s_row(0)
         load_d(0)
@@ -365,149 +367,145 @@ def tile_dedicomdecoder_v_kernel(tc, z_i, z_j, w_r, d_w, rz_in, scores, grad_out
         load_g_rows(1)
         load_s_row(3)
         load_d(1)
-        load_s(UNITS[0])
+        load_s_unit(UNITS[0], 2)
         load_g(1)
-        load_s(UNITS[1])
-        load_z_rz(0)
-        load_s(UNITS[2])
-
-        def activate_both(j):
-            for func in (ACT.Tanh, ACT.Square):
-                activate_row(func, j, slice(0, 512))
-                activate_row(func, j, slice(512, R))
+        load_s_unit(UNITS[1])
+        load_s_unit(UNITS[2])
 
         make_d2(0)
         for j in range(3):
-            activate_both(j)
+            activate_row(j)
         dz_row(0)
         transpose_row(0)
         quantize_d2(0)
         dz_row(1)
         transpose_row(1)
         copy_row(0, nc.scalar.copy)
-        activate_both(3)
+        activate_row(3)
         copy_row(1, nc.scalar.copy)
-        activate(UNITS[0])
+        scalar_unit(0, [])
         dz_row(2)
         transpose_row(2)
         make_d2(1)
         dz_row(3)
         transpose_row(3)
-        for h in range(2):
-            stage_g(UNITS[0], h)
+        for w in range(2):
+            stage_g(UNITS[0], w)
         load_g(2)
+        load_z_rz(0)
+        load_s_unit(UNITS[3])
         load_z_rz(1)
-        load_s(UNITS[3])
         quantize_d2(1)
-        regroup(0, nc.gpsimd.tensor_copy, slice(0, 3))
+        regroup(0, nc.gpsimd.tensor_copy, range(0, 3))
         quantize_rel((0, 0))
         copy_row(2, nc.vector.tensor_copy)
         copy_row(3, nc.vector.tensor_copy)
         make_dz(UNITS[0], 0)
         stage_g(UNITS[1], 0)
-        matmul_0(0)
         make_dz(UNITS[0], 1)
         transpose(UNITS[0])
         stage_g(UNITS[1], 1)
-        regroup(0, nc.vector.tensor_copy, slice(3, 4))
-        quantize_tok(UNITS[0])
+        regroup(0, nc.vector.tensor_copy, range(3, 4))
         quantize_rel((0, 1))
         quantize_tok((0, 0))
+        quantize_tok(UNITS[0])
 
-        for i in range(1, 5):
-            unit, t = UNITS[i], i - 1
-            scalar_round(i)
+        scalar_unit(1, [0])
+        regroup(1, nc.gpsimd.tensor_copy, range(0, 3))
+        copy_out(UNITS[0], 1, nc.vector.tensor_copy)
+        make_dz(UNITS[1], 0)
+        stage_g(UNITS[2], 0)
+        make_dz(UNITS[1], 1)
+        load_s_unit(UNITS[4])
+        load_g(3)
+        transpose(UNITS[1])
+        matmul_0(0)
+        stage_g(UNITS[2], 1)
+        regroup(1, nc.vector.tensor_copy, range(3, 4))
+        quantize_rel(UNITS[0])
+        quantize_tok((0, 1))
+        quantize_tok(UNITS[1])
+
+        for i in range(2, 6):
+            unit, t = UNITS[i], i - 2
+            rows = ROWS[t]
+            scalar_unit(i, [0] if i == 2 else [0, 1])
             p_gpsimd(t)
-            if i == SHARED_ROUND:
+            if i == 2:
                 copy_out(UNITS[i - 1], 1, nc.vector.tensor_copy)
             make_dz(unit, 0)
-            matmul_0(2 * t + 1)
-            finish_0(2 * t)
-            make_dz(unit, 1)
-            transpose(unit)
+            matmul_0(rows[1])
+            finish((0, rows[0]))
+            if len(rows) > 2:
+                matmul_0(rows[2])
+            if 0 < t < LAST:
+                matmul_1(0, 2, [t - 1], "acc2")
             if t == LAST:
                 break
+            make_dz(unit, 1)
+            transpose(unit)
             stage_g(UNITS[i + 1], 0)
-            finish_0(2 * t + 1)
+            for row in rows[1:]:
+                finish((0, row))
             p_vector(t)
-            if t + 2 < NT:
-                load_z_rz(t + 2)
-                load_s(UNITS[i + 3])
-                load_g_unit(UNITS[i + 3])
+            if t == 0:
+                load_z_rz(2)
+                load_s_unit(UNITS[5], 2)
+            if t == 1:
+                load_z_rz(3)
             quantize_rel(UNITS[i - 1])
-            matmul_0(2 * t + 2)
+            matmul_0(ROWS[t + 1][0])
             stage_g(UNITS[i + 1], 1)
-            quantize_tok(unit)
             quantize_p(t)
-            for r in range(3):
+            quantize_tok(unit)
+            for r in range(3 if t == LAST - 1 else 2):
                 matmul_1(0, r, [t], "acc%d" % r)
-        matmul_1(0, 3, range(LAST))
-        stage_g(UNITS[5], 0)
-        finish_0(7)
-        stage_g(UNITS[5], 1)
+        for row in range(0, 8, 2):
+            store(0, row, 2)
+
+        transpose(unit, places=(0, 1))
+        make_dz(unit, 1)
+        transpose(unit, places=(2, 3))
+        matmul_0(11)
+        bank_a, bank_b, bank_c = ring_uses[-3:]
+        for u in range(2):
+            copy_out(unit, u, nc.scalar.copy)
+        finish((0, 9))
+        store(0, 8, 2)
+        matmul_1(0, 3, range(LAST), bank_a)
+        finish((0, 10))
+        store(0, 10)
+        matmul_1(1, 0, range(LAST), bank_b)
         p_vector(LAST)
         quantize_tok(unit)
         quantize_p(LAST)
-        quantize_rel(UNITS[3])
-        for r in (3, 0, 1, 2):
+        for r in range(4):
             matmul_1(0, r, [LAST])
-        for row in range(0, 8, 2):
-            store(0, row)
-
-        unit = UNITS[5]
-        bank_a, bank_b, bank_c = ring_uses[-3:]
-        activate(unit)
-        regroup(1, nc.gpsimd.tensor_copy)
-        finish_1(0, 3)
-        store(1, 3, 1)
-        matmul_0(8, tag=bank_a)
-        copy_aside((0, 8))
-        for u in range(2):
-            copy_out(UNITS[4], u, nc.scalar.copy)
-        finish_aside((0, 8))
-        for r in range(3):
-            finish_1(0, r)
-            store(1, r, 1)
-            matmul_1(1, r, (1, 2), "acc%d" % r)
-        matmul_0(9, tag=bank_a)
-        make_dz(unit, 0)
-        matmul_0(10, tag=bank_b)
-        transpose(unit, [0], (0, 1))
-        make_dz(unit, 1)
-        transpose(unit, [0], (2, 3))
-        transpose(unit, [1])
-        matmul_0(11, tag=bank_c)
-        copy_out(unit, 0, nc.scalar.copy)
-        copy_aside((0, 11))
-        copy_out(unit, 1, nc.scalar.copy)
-        finish_0(9)
-        store(0, 9, 1)
-        finish_0(10)
-        store(0, 8, 1)
-        store(0, 10, 1)
-        quantize_tok((0, 1))
-        quantize_tok(unit)
+        matmul_1(1, 0, [LAST])
+        finish((0, 11))
+        store(0, 11)
+        for r, bank in enumerate(("tr_bank0", bank_c, "tr_bank1")):
+            matmul_1(1, r + 1, range(NT), bank)
+        copy_aside((1, 1))
+        finish_aside((1, 1))
+        for r in (0, 2, 3):
+            finish((1, r))
+            store(1, r)
+        for r in range(2):
+            finish((1, 4 + r))
+        store(1, 4, 2)
+        store(1, 1)
         quantize_rel(UNITS[4])
-        finish_aside((0, 11), rel_stage())
-        for r in range(3):
-            matmul_1(1, r, (0, LAST))
-        matmul_1(1, 3, (1, 2, 0, LAST), bank_a)
-        matmul_0(12, [0], bank_b)
-        matmul_0(13, [0], "tr_bank0")
-        for r in range(3):
-            finish_1(1, r)
-            store(1, 4 + r, 1)
-        store_aside((0, 11), nc.sync)
         quantize_rel(unit)
-        for row in (12, 13):
-            matmul_0(row, [1])
-        matmul_0(14, tag=bank_c)
-        matmul_0(15, tag="tr_bank1")
-        finish_1(1, 3)
-        store(1, 7, 1)
+        for k in range(3):
+            matmul_0(12 + k, tag="acc%d" % k)
+        matmul_0(15, tag=bank_a)
+        for r in range(2, 4):
+            finish((1, 4 + r))
+            store(1, 4 + r)
         for row in range(12, 15):
-            finish_0(row)
-            store(0, row, 1)
+            finish((0, row))
+            store(0, row)
         for cols in (slice(0, 256), slice(256, H)):
-            finish_0(15, cols)
+            finish((0, 15), cols)
             store(0, 15, 1, cols)

@@ -22,7 +22,7 @@ NT = B // 512
 NG = R // 512
 LAST = NT - 1
 UNITS = [(t, g) for t in range(1, NT) for g in range(NG)]
-GPSIMD_COLS = [352, 304, 304, 304]
+GPSIMD_COLS = [400, 352, 352, 352]
 RING = 3
 ROWS = [range(0, 2), range(2, 5), range(5, 8), range(8, 12)]
 
@@ -265,7 +265,7 @@ def tile_dedicomdecoder_v_kernel(tc, z_i, z_j, w_r, d_w, rz_in, scores, grad_out
 
         def p_gpsimd(t):
             p_t[t] = shared_stage()
-            make_p(t, nc.gpsimd, slice(0, GPSIMD_COLS[t]), 4)
+            make_p(t, nc.gpsimd, slice(0, GPSIMD_COLS[t]), 8)
 
         def p_vector(t):
             make_p(t, nc.vector, slice(GPSIMD_COLS[t], H), 2)
@@ -476,6 +476,7 @@ def tile_dedicomdecoder_v_kernel(tc, z_i, z_j, w_r, d_w, rz_in, scores, grad_out
         finish((0, 10))
         store(0, 10)
         matmul_1(1, 0, range(LAST), bank_b)
+        matmul_1(1, 1, [0], "tr_bank0")
         p_vector(LAST)
         quantize_tok(unit)
         quantize_p(LAST)
@@ -484,18 +485,19 @@ def tile_dedicomdecoder_v_kernel(tc, z_i, z_j, w_r, d_w, rz_in, scores, grad_out
         matmul_1(1, 0, [LAST])
         finish((0, 11))
         store(0, 11)
-        for r, bank in enumerate(("tr_bank0", bank_c, "tr_bank1")):
-            matmul_1(1, r + 1, range(NT), bank)
-        copy_aside((1, 1))
-        finish_aside((1, 1))
-        for r in (0, 2, 3):
+        quantize_rel(UNITS[4])
+        matmul_1(1, 1, range(1, NT))
+        for r, bank in enumerate((bank_c, "tr_bank1")):
+            matmul_1(1, r + 2, range(NT), bank)
+        copy_aside((1, 0))
+        finish_aside((1, 0))
+        for r in (1, 2, 3):
             finish((1, r))
             store(1, r)
         for r in range(2):
             finish((1, 4 + r))
+        store(1, 0)
         store(1, 4, 2)
-        store(1, 1)
-        quantize_rel(UNITS[4])
         quantize_rel(unit)
         for k in range(3):
             matmul_0(12 + k, tag="acc%d" % k)

@@ -22,7 +22,7 @@ NT = B // 512
 NG = R // 512
 LAST = NT - 1
 UNITS = [(t, g) for t in range(1, NT) for g in range(NG)]
-GPSIMD_COLS = [400, 352, 352, 352]
+GPSIMD_COLS = [376, 328, 328, 328]
 RING = 3
 ROWS = [range(0, 2), range(2, 5), range(5, 8), range(8, 12)]
 

@@ -22,8 +22,9 @@ NT = B // 512
 NG = R // 512
 LAST = NT - 1
 UNITS = [(t, g) for t in range(1, NT) for g in range(NG)]
-GPSIMD_COLS = [376, 328, 328, 328]
+GPSIMD_COLS = [376, 424, 328, 328]
 RING = 3
+SHARED_ROUNDS = (2, 3)
 ROWS = [range(0, 2), range(2, 5), range(5, 8), range(8, 12)]
 
 
@@ -429,9 +430,9 @@ def tile_dedicomdecoder_v_kernel(tc, z_i, z_j, w_r, d_w, rz_in, scores, grad_out
         for i in range(2, 6):
             unit, t = UNITS[i], i - 2
             rows = ROWS[t]
-            scalar_unit(i, [0] if i == 2 else [0, 1])
+            scalar_unit(i, [0] if i in SHARED_ROUNDS else [0, 1])
             p_gpsimd(t)
-            if i == 2:
+            if i in SHARED_ROUNDS:
                 copy_out(UNITS[i - 1], 1, nc.vector.tensor_copy)
             make_dz(unit, 0)
             matmul_0(rows[1])
@@ -505,9 +506,7 @@ def tile_dedicomdecoder_v_kernel(tc, z_i, z_j, w_r, d_w, rz_in, scores, grad_out
         for r in range(2, 4):
             finish((1, 4 + r))
             store(1, 4 + r)
-        for row in range(12, 15):
+        for row in range(12, 16):
             finish((0, row))
-            store(0, row)
-        for cols in (slice(0, 256), slice(256, H)):
-            finish((0, 15), cols)
-            store(0, 15, 1, cols)
+            if row % 2:
+                store(0, row - 1, 2)

@@ -506,7 +506,9 @@ def tile_dedicomdecoder_v_kernel(tc, z_i, z_j, w_r, d_w, rz_in, scores, grad_out
         for r in range(2, 4):
             finish((1, 4 + r))
             store(1, 4 + r)
-        for row in range(12, 16):
+        for row in range(12, 15):
             finish((0, row))
-            if row % 2:
-                store(0, row - 1, 2)
+            store(0, row)
+        for cols in (slice(0, 256), slice(256, H)):
+            finish((0, 15), cols)
+            store(0, 15, 1, cols)

@@ -136,12 +136,13 @@ def tile_dedicomdecoder_v_kernel(tc, z_i, z_j, w_r, d_w, rz_in, scores, grad_out
         def rel_stage():
             return ring.tile([P, 2048], BF16, name="rel", align_bytes=64)
 
-        def make_d2(g):
-            tok_t["d", g] = shared_stage()
+        def make_d2(g, cols=slice(0, H)):
+            if ("d", g) not in tok_t:
+                tok_t["d", g] = shared_stage()
             nc.vector.tensor_tensor(
-                out=by_cols(tok_t["d", g][:].rearrange("p (c j) -> p j c", j=4)),
-                in0=by_cols(d_t[g][:]),
-                in1=by_cols(d_t[g][:]),
+                out=by_cols(tok_t["d", g][:].rearrange("p (c j) -> p j c", j=4)[:, :, cols]),
+                in0=by_cols(d_t[g][:, :, cols]),
+                in1=by_cols(d_t[g][:, :, cols]),
                 op=ALU.mult,
             )
 
@@ -381,24 +382,26 @@ def tile_dedicomdecoder_v_kernel(tc, z_i, z_j, w_r, d_w, rz_in, scores, grad_out
         quantize_d2(0)
         dz_row(1)
         transpose_row(1)
-        copy_row(0, nc.scalar.copy)
+        copy_row(0, nc.vector.tensor_copy)
         activate_row(3)
         copy_row(1, nc.scalar.copy)
         scalar_unit(0, [])
         dz_row(2)
         transpose_row(2)
-        make_d2(1)
+        make_d2(1, slice(0, H // 2))
         dz_row(3)
         transpose_row(3)
+        make_d2(1, slice(H // 2, H))
         for w in range(2):
             stage_g(UNITS[0], w)
         load_g(2)
         load_z_rz(0)
         load_s_unit(UNITS[3])
         load_z_rz(1)
+        quantize_rel((0, 0))
         quantize_d2(1)
         regroup(0, nc.gpsimd.tensor_copy, range(0, 3))
-        quantize_rel((0, 0))
+        regroup(0, nc.scalar.copy, range(3, 4))
         copy_row(2, nc.vector.tensor_copy)
         copy_row(3, nc.vector.tensor_copy)
         make_dz(UNITS[0], 0)
@@ -406,7 +409,6 @@ def tile_dedicomdecoder_v_kernel(tc, z_i, z_j, w_r, d_w, rz_in, scores, grad_out
         make_dz(UNITS[0], 1)
         transpose(UNITS[0])
         stage_g(UNITS[1], 1)
-        regroup(0, nc.vector.tensor_copy, range(3, 4))
         quantize_rel((0, 1))
         quantize_tok((0, 0))
         quantize_tok(UNITS[0])

from contextlib import ExitStack

import concourse.mybir as mybir
from concourse.masks import make_identity

B, H, R = 2048, 512, 1024

FLOPS = 2 * 2 * B * H * R
BYTES = 2 * B * H + 2 * R * H + 4 * B * H + 4 * B * R + 2 * B * R + 4 * B * H + 4 * R * H

F32 = mybir.dt.float32
BF16 = mybir.dt.bfloat16
U32 = mybir.dt.uint32
U8 = mybir.dt.uint8
E4M3 = mybir.dt.float8_e4m3fn_x4
E5M2 = mybir.dt.float8_e5m2_x4
ACT = mybir.ActivationFunctionType
ALU = mybir.AluOpType

P = 128
NT = B // 512
NG = R // 512
LAST = NT - 1
UNITS = [(t, g) for t in range(1, NT) for g in range(NG)]
GPSIMD_COLS = [376, 424, 328, 328]
RING = 3
SHARED_ROUNDS = (2, 3)
ROWS = [range(0, 2), range(2, 5), range(5, 8), range(8, 12)]


def tile_dedicomdecoder_v_kernel(tc, z_i, z_j, w_r, d_w, rz_in, scores, grad_out, out_0, out_1):
    nc = tc.nc
    with ExitStack() as ctx:
        keep = ctx.enter_context(tc.tile_pool(name="keep", bufs=1))
        ring = ctx.enter_context(tc.tile_pool(name="ring", bufs=2))
        psum = ctx.enter_context(tc.psum_pool(name="psum", bufs=1))
        ctx.enter_context(tc.manual_schedule())

        def four_rows(hbm, t):
            return hbm[512 * t : 512 * (t + 1), :].rearrange("(p j) n -> p j n", j=4)

        s_t, g_t, z_t, rz_t, d_t = {}, {}, {}, {}, {}

        def new_s(t, u):
            s_t[t, u] = ring.tile([P, 2, R], F32, name="s_in", bufs=5)

        def load_s_row(j):
            if j % 2 == 0:
                new_s(0, j // 2)
            nc.sync.dma_start(out=s_t[0, j // 2][:, j % 2, :], in_=four_rows(scores, 0)[:, j, :])

        s_at, g_at = {}, {}

        def load_s_pair(t, u):
            new_s(t, u)
            nc.sync.dma_start(out=s_t[t, u][:], in_=four_rows(scores, t)[:, 2 * u : 2 * u + 2, :])
            for g in range(NG):
                s_at[(t, g), u] = s_t[t, u][:, :, 512 * g : 512 * (g + 1)]

        def load_s_unit(unit, pieces=1):
            t, g = unit
            s_t[unit] = ring.tile([P, 4, 512], F32, name="s_in", bufs=5)
            rows = 4 // pieces
            for lo in range(0, 4, rows):
                nc.sync.dma_start(
                    out=s_t[unit][:, lo : lo + rows, :],
                    in_=four_rows(scores, t)[:, lo : lo + rows, 512 * g : 512 * (g + 1)],
                )
            for u in range(2):
                s_at[unit, u] = s_t[unit][:, 2 * u : 2 * u + 2, :]

        def load_g_rows(u):
            if u == 0:
                g_t[0] = ring.tile([P, 4, R], BF16, name="g_in")
            nc.sync.dma_start(out=g_t[0][:, 2 * u : 2 * u + 2, :], in_=four_rows(grad_out, 0)[:, 2 * u : 2 * u + 2, :])

        def load_g(t):
            g_t[t] = ring.tile([P, 4, R], BF16, name="g_in")
            nc.sync.dma_start(out=g_t[t][:], in_=four_rows(grad_out, t))
            for g in range(NG):
                g_at[t, g] = g_t[t][:, :, 512 * g : 512 * (g + 1)]

        def load_g_unit(unit):
            t, g = unit
            if g == 0:
                g_t[t] = ring.tile([P, NG, 4, 512], BF16, name="g_in")
            g_at[unit] = g_t[t][:, g]
            nc.sync.dma_start(out=g_at[unit], in_=four_rows(grad_out, t)[:, :, 512 * g : 512 * (g + 1)])

        def load_d(g):
            d_t[g] = keep.tile([P, 4, H], BF16, name="d_rows%d" % g)
            nc.sync.dma_start(out=d_t[g][:], in_=four_rows(d_w, g))

        def load_z_rz(t):
            z_t[t] = ring.tile([P, 4, H], BF16, name="z_rows")
            nc.sync.dma_start(out=z_t[t][:], in_=four_rows(z_i, t))
            rz_t[t] = ring.tile([P, 4, H], F32, name="rz_rows", bufs=3)
            nc.sync.dma_start(out=rz_t[t][:], in_=four_rows(rz_in, t))

        ident = keep.tile([P, P], F32, name="ident")
        make_identity(nc, ident[:])
        ident_bf = keep.tile([P, P], BF16, name="ident_bf")
        make_identity(nc, ident_bf[:])

        codes, scales = {}, {}

        def new_codes(key):
            if key[0] == "rel":
                codes[key] = ring.tile([P, 512], U32, name="code_rel", bufs=4, align_bytes=64)
                scales[key] = ring.tile([P, 512], U8, name="scale_rel", bufs=4, align_bytes=64)
            else:
                codes[key] = keep.tile([P, 512], U32, name="code_%s%d%d" % key, align_bytes=64)
                scales[key] = keep.tile([P, 512], U8, name="scale_%s%d%d" % key, align_bytes=64)

        def quantize(key, staged, fmt, lo=0, hi=512):
            if key not in codes:
                new_codes(key)
            nc.vector.quantize_mx(
                out=codes[key][:, lo:hi].bitcast(fmt), scales=scales[key][:, lo:hi], in_=staged[:, 4 * lo : 4 * hi]
            )

        def by_cols(ap, n=2):
            return ap.rearrange("p j (c i) -> p c j i", i=n)

        tok_t, rel_t, tr_bank, x_t, g_bank, p_t = {}, {}, {}, {}, {}, {}

        ring_uses = []

        def next_in_ring():
            ring_uses.append("ring_bank%d" % (len(ring_uses) % RING))
            return ring_uses[-1]

        def shared_stage():
            return keep.tile([P, 2048], BF16, name="shared_stage", align_bytes=64)

        def rel_stage():
            return ring.tile([P, 2048], BF16, name="rel", align_bytes=64)

        def make_d2(g, cols=slice(0, H)):
            if ("d", g) not in tok_t:
                tok_t["d", g] = shared_stage()
            nc.vector.tensor_tensor(
                out=by_cols(tok_t["d", g][:].rearrange("p (c j) -> p j c", j=4)[:, :, cols]),
                in0=by_cols(d_t[g][:, :, cols]),
                in1=by_cols(d_t[g][:, :, cols]),
                op=ALU.mult,
            )

        def quantize_d2(g):
            quantize(("d", g, 0), tok_t["d", g], E4M3)

        dz_rows = keep.tile([P, 4, R], BF16, name="dz_rows")

        def activate_row(j):
            for func in (ACT.Tanh, ACT.Square):
                for cols in (slice(0, 512), slice(512, R)):
                    s = s_t[0, j // 2][:, j % 2, cols]
                    nc.scalar.activation(out=s, in_=s, func=func, scale=0.5)

        def dz_row(j):
            nc.vector.scalar_tensor_tensor(
                out=dz_rows[:, j, :],
                in0=s_t[0, j // 2][:, j % 2, :],
                scalar=0.25,
                in1=g_t[0][:, j, :],
                op0=ALU.subtract,
                op1=ALU.mult,
            )

        def transpose_row(j):
            tr_bank[0, j] = psum.tile([P, NG, 2, P], F32, name="tr_bank%d" % (j % 2))
            words = dz_rows[:, j, :].bitcast(F32)
            for g in range(NG):
                for h in range(2):
                    nc.tensor.transpose(tr_bank[0, j][:, g, h, :], words[:, 256 * g + h : 256 * (g + 1) : 2], ident[:])

        def copy_row(j, copy):
            if j % 2 == 0:
                rel_t[0, j // 2] = rel_stage()
            copy(
                out=rel_t[0, j // 2][:, 1024 * (j % 2) : 1024 * (j % 2 + 1)]
                .bitcast(F32)
                .rearrange("q (g p h) -> q g p h", g=NG, h=2),
                in_=tr_bank[0, j][:].rearrange("q g h p -> q g p h"),
            )

        def regroup(g, copy, places=range(4)):
            if (0, g) not in tok_t:
                tok_t[0, g] = shared_stage()
            at = slice(places.start, places.stop)
            copy(
                out=tok_t[0, g][:].rearrange("p (t q j) -> p t q j", t=4, j=4)[:, at],
                in_=dz_rows[:, :, 512 * g : 512 * (g + 1)].rearrange("p j (q t) -> p t q j", t=4)[:, at],
            )

        def tanh(unit, u):
            if u == 0:
                x_t[unit] = ring.tile([P, 2, 2, P, 2, 2], F32, name="x_half")
            pairs = s_at[unit, u].rearrange("p e (q h b) -> p h q b e", h=2, b=2)
            for h in range(2):
                nc.scalar.activation(out=x_t[unit][:, u, h], in_=pairs[:, h], func=ACT.Tanh, scale=0.5)

        def squares(unit, h):
            return s_at[unit, h].rearrange("p b (q j) -> p b q j", j=4)

        def square(unit, h):
            nc.scalar.activation(
                out=squares(unit, h).rearrange("p b q (u e) -> p q b u e", u=2),
                in_=x_t[unit][:, :, h].rearrange("p u q b e -> p q b u e"),
                func=ACT.Square,
                scale=0.5,
            )

        def stage_g(unit, h, tag=None):
            g_bank[unit, h] = psum.tile([P, P, 4, 2], BF16, name=tag or next_in_ring())
            pairs = g_at[unit].rearrange("p j (q h b) -> p j h q b", h=2, b=2)
            for u in range(2):
                nc.tensor.matmul(
                    out=g_bank[unit, h][:].rearrange("p q j b -> p j q b")[:, 2 * u : 2 * u + 2],
                    lhsT=ident_bf[:],
                    rhs=pairs[:, 2 * u : 2 * u + 2, h],
                    start=True,
                    stop=True,
                )

        def make_dz(unit, h):
            if unit not in tok_t:
                tok_t[unit] = ring.tile([P, 2048], BF16, name="tok", bufs=3, align_bytes=64)
            nc.vector.scalar_tensor_tensor(
                out=tok_t[unit][:, 1024 * h : 1024 * (h + 1)].rearrange("p (b n) -> p b n", b=2),
                in0=squares(unit, h).rearrange("p b q j -> p b (q j)"),
                scalar=0.25,
                in1=g_bank[unit, h][:].rearrange("p q j b -> p b (q j)"),
                op0=ALU.subtract,
                op1=ALU.mult,
            )

        def transpose(unit, halves=range(2), places=range(4)):
            words = tok_t[unit][:].bitcast(F32).rearrange("p (t q u) -> p t u q", t=4, u=2)
            for u in halves:
                if 0 in places:
                    tr_bank[unit, u] = psum.tile([P, P, 4], F32, name="tr_bank%d" % u)
                for t in places:
                    nc.tensor.transpose(tr_bank[unit, u][:, :, t], words[:, t, u, :], ident[:])

        def copy_out(unit, u, copy):
            if unit not in rel_t:
                rel_t[unit] = rel_stage()
            copy(
                out=rel_t[unit][:, 1024 * u : 1024 * (u + 1)].rearrange("q (e n) -> q e n", e=2),
                in_=tr_bank[unit, u][:].rearrange("q p t -> q (p t)").bitcast(BF16).rearrange("q (n e) -> q e n", e=2),
            )

        def quantize_tok(unit):
            quantize(("tok",) + unit, tok_t[unit], E5M2)

        def quantize_rel(unit, lo=0, hi=512):
            quantize(("rel",) + unit, rel_t[unit], E5M2, lo, hi)

        def make_p(t, engine, cols, n):
            engine.tensor_tensor(
                out=by_cols(p_t[t][:].rearrange("p (c j) -> p j c", j=4)[:, :, cols], n),
                in0=by_cols(z_t[t][:, :, cols], n),
                in1=by_cols(rz_t[t][:, :, cols], n),
                op=ALU.mult,
            )

        def p_gpsimd(t):
            p_t[t] = shared_stage()
            make_p(t, nc.gpsimd, slice(0, GPSIMD_COLS[t]), 8)

        def p_vector(t):
            make_p(t, nc.vector, slice(GPSIMD_COLS[t], H), 2)

        def quantize_p(t):
            quantize(("p", t, 0), p_t[t], E4M3)

        def pass_mx(bank, key, col, moving, start, stop):
            nc.tensor.matmul_mx(
                out=bank[:],
                lhsT=codes[key][:, col : col + P].bitcast(E5M2),
                lhsT_scale=scales[key][:, col : col + P],
                rhs=codes[moving][:].bitcast(E4M3),
                rhs_scale=scales[moving][:],
                start=start,
                stop=stop,
            )

        o0_bank, o1_bank, o1_done, out_t = {}, {}, {}, {}

        def new_bank(tag):
            return psum.tile([P, H], F32, name=tag or next_in_ring())

        def matmul_0(row, groups=range(NG), tag=None):
            t, j = divmod(row, 4)
            for g in groups:
                if g == 0:
                    o0_bank[row] = new_bank(tag)
                if t == 0:
                    key, col = ("rel", 0, j // 2), 256 * (j % 2) + P * g
                else:
                    key, col = ("rel", t, g), P * j
                pass_mx(o0_bank[row], key, col, ("d", g, 0), g == 0, g == NG - 1)

        def matmul_1(g, r, tiles, tag=None):
            for t in tiles:
                done = o1_done.setdefault((g, r), [])
                if not done:
                    o1_bank[g, r] = new_bank(tag)
                done.append(t)
                pass_mx(o1_bank[g, r], ("tok", t, g), P * r, ("p", t, 0), len(done) == 1, len(done) == NT)

        def out_row(which, row):
            if (which, row // 2) not in out_t:
                out_t[which, row // 2] = ring.tile([P, 2, H], F32, name="out_rows", bufs=7)
            return out_t[which, row // 2][:, row % 2, :]

        def final_of(key):
            which, row = key
            if which == 0:
                return o0_bank[row], -1.0, rz_t[row // 4][:, row % 4, :]
            return o1_bank[divmod(row, 4)], -2.0, d_t[row // 4][:, row % 4, :]

        def finish(key, cols=slice(0, H)):
            bank, factor, other = final_of(key)
            nc.vector.scalar_tensor_tensor(
                out=out_row(*key)[:, cols],
                in0=bank[:, cols],
                scalar=factor,
                in1=other[:, cols],
                op0=ALU.mult,
                op1=ALU.mult,
            )

        aside_t = {}

        def copy_aside(key):
            bank, factor, other = final_of(key)
            nc.scalar.mul(out=out_row(*key), in_=bank[:], mul=factor)

        def finish_aside(key, held=None):
            bank, factor, other = final_of(key)
            aside_t[key] = out_row(*key) if held is None else held[:].bitcast(F32)[:, :H]
            nc.gpsimd.tensor_tensor(out=aside_t[key], in0=out_row(*key), in1=other, op=ALU.mult)

        def store_aside(key):
            which, row = key
            nc.sync.dma_start(out=four_rows((out_0, out_1)[which], row // 4)[:, row % 4, :], in_=aside_t[key])

        def store(which, row, count=1, cols=slice(0, H)):
            nc.sync.dma_start(
                out=four_rows((out_0, out_1)[which], row // 4)[:, row % 4 : row % 4 + count, cols],
                in_=out_t[which, row // 2][:, row % 2 : row % 2 + count, cols],
            )

        def scalar_unit(i, halves=range(2)):
            for u in range(2):
                tanh(UNITS[i], u)
            for w in range(2):
                square(UNITS[i], w)
            for u in halves:
                copy_out(UNITS[i - 1], u, nc.scalar.copy)

        load_s_row(0)
        load_d(0)
        load_s_row(1)
        load_g_rows(0)
        load_s_row(2)
        load_g_rows(1)
        load_s_row(3)
        load_d(1)
        load_s_unit(UNITS[0], 2)
        load_g(1)
        load_s_unit(UNITS[1])
        load_s_unit(UNITS[2])

        make_d2(0)
        for j in range(3):
            activate_row(j)
        dz_row(0)
        transpose_row(0)
        quantize_d2(0)
        dz_row(1)
        transpose_row(1)
        copy_row(0, nc.vector.tensor_copy)
        activate_row(3)
        copy_row(1, nc.scalar.copy)
        scalar_unit(0, [])
        dz_row(2)
        transpose_row(2)
        make_d2(1, slice(0, H // 2))
        dz_row(3)
        transpose_row(3)
        make_d2(1, slice(H // 2, H))
        for w in range(2):
            stage_g(UNITS[0], w)
        load_g(2)
        load_z_rz(0)
        load_s_unit(UNITS[3])
        load_z_rz(1)
        quantize_rel((0, 0))
        quantize_d2(1)
        regroup(0, nc.gpsimd.tensor_copy, range(0, 3))
        regroup(0, nc.scalar.copy, range(3, 4))
        copy_row(2, nc.vector.tensor_copy)
        copy_row(3, nc.vector.tensor_copy)
        make_dz(UNITS[0], 0)
        stage_g(UNITS[1], 0)
        make_dz(UNITS[0], 1)
        transpose(UNITS[0])
        stage_g(UNITS[1], 1)
        quantize_rel((0, 1))
        quantize_tok((0, 0))
        quantize_tok(UNITS[0])

        scalar_unit(1, [0])
        regroup(1, nc.gpsimd.tensor_copy, range(0, 3))
        copy_out(UNITS[0], 1, nc.vector.tensor_copy)
        make_dz(UNITS[1], 0)
        stage_g(UNITS[2], 0)
        make_dz(UNITS[1], 1)
        load_s_unit(UNITS[4])
        load_g(3)
        transpose(UNITS[1])
        matmul_0(0)
        stage_g(UNITS[2], 1)
        regroup(1, nc.vector.tensor_copy, range(3, 4))
        quantize_rel(UNITS[0])
        quantize_tok((0, 1))
        quantize_tok(UNITS[1])

        for i in range(2, 6):
            unit, t = UNITS[i], i - 2
            rows = ROWS[t]
            scalar_unit(i, [0] if i in SHARED_ROUNDS else [0, 1])
            p_gpsimd(t)
            if i in SHARED_ROUNDS:
                copy_out(UNITS[i - 1], 1, nc.vector.tensor_copy)
            make_dz(unit, 0)
            matmul_0(rows[1])
            finish((0, rows[0]))
            if len(rows) > 2:
                matmul_0(rows[2])
            if 0 < t < LAST:
                matmul_1(0, 2, [t - 1], "acc2")
            if t == LAST:
                break
            make_dz(unit, 1)
            transpose(unit)
            stage_g(UNITS[i + 1], 0)
            for row in rows[1:]:
                finish((0, row))
            p_vector(t)
            if t == 0:
                load_z_rz(2)
                load_s_unit(UNITS[5], 2)
            if t == 1:
                load_z_rz(3)
            quantize_rel(UNITS[i - 1])
            matmul_0(ROWS[t + 1][0])
            stage_g(UNITS[i + 1], 1)
            quantize_p(t)
            quantize_tok(unit)
            for r in range(3 if t == LAST - 1 else 2):
                matmul_1(0, r, [t], "acc%d" % r)
        for row in range(0, 8, 2):
            store(0, row, 2)

        transpose(unit, places=(0, 1))
        make_dz(unit, 1)
        transpose(unit, places=(2, 3))
        matmul_0(11)
        bank_a, bank_b, bank_c = ring_uses[-3:]
        for u in range(2):
            copy_out(unit, u, nc.scalar.copy)
        finish((0, 9))
        store(0, 8, 2)
        matmul_1(0, 3, range(LAST), bank_a)
        finish((0, 10))
        store(0, 10)
        matmul_1(1, 0, range(LAST), bank_b)
        matmul_1(1, 1, [0], "tr_bank0")
        p_vector(LAST)
        quantize_tok(unit)
        quantize_p(LAST)
        for r in range(4):
            matmul_1(0, r, [LAST])
        matmul_1(1, 0, [LAST])
        finish((0, 11))
        store(0, 11)
        quantize_rel(UNITS[4])
        matmul_1(1, 1, range(1, NT))
        for r, bank in enumerate((bank_c, "tr_bank1")):
            matmul_1(1, r + 2, range(NT), bank)
        copy_aside((1, 0))
        finish_aside((1, 0))
        for r in (1, 2, 3):
            finish((1, r))
            store(1, r)
        for r in range(2):
            finish((1, 4 + r))
        store(1, 0)
        store(1, 4, 2)
        quantize_rel(unit)
        for k in range(3):
            matmul_0(12 + k, tag="acc%d" % k)
        matmul_0(15, tag=bank_a)
        for r in range(2, 4):
            finish((1, 4 + r))
            store(1, 4 + r)
        for row in range(12, 15):
            finish((0, row))
            store(0, row)
        for cols in (slice(0, 256), slice(256, H)):
            finish((0, 15), cols)
            store(0, 15, 1, cols)
